import numpy as np
import ml_dtypes


def mxq(x, axis, fmt="e4m3"):
    dtype, down = {"e4m3": (ml_dtypes.float8_e4m3fn, 7), "e5m2": (ml_dtypes.float8_e5m2, 14)}[fmt]
    v = np.moveaxis(np.asarray(x, np.float32).astype(ml_dtypes.bfloat16).astype(np.float64), axis, -1)
    blocks = v.reshape(v.shape[:-1] + (-1, 32))
    amax = np.abs(blocks).max(-1, keepdims=True)
    byte = np.maximum(np.where(amax > 0, np.frexp(amax)[1] - 1 + 127, 0) - down, 1)
    scale = np.exp2(byte - 127.0)
    codes = (blocks / scale).astype(np.float32).astype(dtype).astype(np.float64)
    return np.moveaxis((codes * scale).reshape(v.shape), -1, axis)


WIDE = False


def mx_kscale(k):
    if not WIDE:
        return np.ones(k)
    levels = np.array([10, -10, 5, -5, 0])
    a = np.random.permutation(np.resize(levels, k // 512 * 4)).reshape(k // 512, 4)
    idx = np.arange(k)
    return np.exp2(a[idx // 512, idx % 128 // 32])


BF16 = ml_dtypes.bfloat16


def bf(x):
    return np.asarray(x, np.float32).astype(BF16)


def f64(x):
    return np.asarray(x).astype(np.float64)


N, K, DN, DE, DT, H, DOUT = 256, 20, 512, 384, 128, 2, 1024
DH = DOUT // H
C = DN + DE + DT
CO = DOUT + DN
VS = 1.8
TS = 1.5
LN_EPS = 1e-5


def setup_inputs():
    g = np.random.standard_normal
    s = np.concatenate([mx_kscale(C)[:DN + DE], np.ones(DT)])
    u = mx_kscale(CO)
    t, sr = u[:DOUT], u[DOUT:]
    a = 1.4 * g((N, K, H))
    a = np.where(a >= 0.0, a, 0.2 * a)
    e = np.exp(a - a.max(axis=1, keepdims=True))
    return {
        "att": bf(e / e.sum(axis=1, keepdims=True)),
        "root_node_feature": bf(g((N, DN)) * sr),
        "root_ts": bf(np.random.uniform(size=N) * TS + TS),
        "neighbor_ts": bf(np.random.uniform(size=(N, K)) * TS),
        "neighbor_node_feature": bf(g((N, K, DN)) * s[:DN]),
        "neighbor_edge_feature": bf(g((N, K, DE)) * s[DN:DN + DE]),
        "time_w": bf((10.0 ** -np.linspace(0.0, 1.0, DT) * (1.0 + 0.1 * g(DT))).reshape(DT, 1)),
        "time_b": bf(0.2 * g(DT)),
        "wv_w": bf(g((DOUT, C)) * VS / np.sqrt(C) / s[None, :] * t[:, None]),
        "wv_b": bf(0.3 * g(DOUT) * t),
        "wo_w": bf(g((DOUT, CO)) / np.sqrt(CO) / u[None, :]),
        "wo_b": bf(0.3 * g(DOUT)),
        "ln_g": bf(1.0 + 0.1 * g(DOUT)),
        "ln_b": bf(0.1 * g(DOUT)),
    }


def reference(att, root_node_feature, root_ts, neighbor_ts, neighbor_node_feature, neighbor_edge_feature, time_w, time_b, wv_w, wv_b, wo_w, wo_b, ln_g, ln_b):
    n, k = neighbor_ts.shape
    tw, tb = f64(time_w)[:, 0], f64(time_b)
    dt = f64(root_ts)[:, None] - f64(neighbor_ts)
    edge_tf = np.cos(dt[..., None] * tw + tb)
    kv_in = np.concatenate([f64(neighbor_node_feature), f64(neighbor_edge_feature), edge_tf], axis=-1).reshape(n * k, C)
    h_v = (mxq(kv_in, 1, "e4m3") @ mxq(f64(wv_w), 1, "e4m3").T) + f64(wv_b)
    h_neigh = np.sum(h_v.reshape(n, k, H, DH) * f64(att)[..., None], axis=1).reshape(n, DOUT)
    cat = np.concatenate([h_neigh, f64(root_node_feature)], axis=1)
    h_out = (mxq(cat, 1, "e4m3") @ mxq(f64(wo_w), 1, "e4m3").T) + f64(wo_b)
    h_out = np.maximum(h_out, 0.0)
    mu = h_out.mean(axis=-1, keepdims=True)
    var = ((h_out - mu) ** 2).mean(axis=-1, keepdims=True)
    return (h_out - mu) / np.sqrt(var + LN_EPS) * f64(ln_g) + f64(ln_b)

@@ -1,0 +1,488 @@
+import math
+from contextlib import ExitStack
+
+import concourse.mybir as mybir
+from concourse.masks import make_identity
+
+F32 = mybir.dt.float32
+BF16 = mybir.dt.bfloat16
+I32 = mybir.dt.int32
+U32 = mybir.dt.uint32
+U8 = mybir.dt.uint8
+FP8X4 = mybir.dt.float8_e4m3fn_x4
+ALU = mybir.AluOpType
+ACT = mybir.ActivationFunctionType
+AX = mybir.AxisListType
+
+P = 128
+NROOT = 256
+NNEI = 20
+DN = 512
+DE = 384
+DOUT = 1024
+CO = 1536
+LN_EPS = 1e-5
+FLOPS = 2 * NROOT * NNEI * 1024 * DOUT + 2 * NROOT * CO * DOUT
+
+TF_CHUNKS = ((0, 256), (256, 512), (768, 512))
+
+
+def tile_transformeraggregator_pb_t_kernel(
+    tc,
+    att,
+    root_node_feature,
+    root_ts,
+    neighbor_ts,
+    neighbor_node_feature,
+    neighbor_edge_feature,
+    time_w,
+    time_b,
+    wv_w,
+    wv_b,
+    wo_w,
+    wo_b,
+    ln_g,
+    ln_b,
+    out,
+):
+    nc = tc.nc
+    with ExitStack() as es:
+        const = es.enter_context(tc.tile_pool(name="const", bufs=1))
+        wraw = es.enter_context(tc.tile_pool(name="wraw", bufs=8))
+        wgp = es.enter_context(tc.tile_pool(name="wgp", bufs=2))
+        vin = es.enter_context(tc.tile_pool(name="vin", bufs=3))
+        stg = es.enter_context(tc.tile_pool(name="stg", bufs=3))
+        ps_t = es.enter_context(tc.psum_pool(name="ps_t", bufs=1))
+        ps_v = es.enter_context(tc.psum_pool(name="ps_v", bufs=5))
+
+        identf = const.tile([P, P], F32, name="identf")
+        make_identity(nc, identf[:])
+        identb = const.tile([P, P], BF16, name="identb")
+        make_identity(nc, identb[:])
+        negi = const.tile([P, P], BF16, name="negi")
+        nc.vector.tensor_scalar_mul(out=negi[:], in0=identb[:], scalar1=-1.0)
+        sel = const.tile([P, P], BF16, name="sel")
+        nc.vector.tensor_copy(
+            out=sel[:].rearrange("p (a q) -> p a q", a=4),
+            in_=identb[:, 0:32].unsqueeze(1).to_broadcast([P, 4, 32]),
+        )
+        zin = const.tile([P, 1], F32, name="zin")
+        zout = const.tile([P, 1], F32, name="zout")
+        nc.vector.memset(zin[:], 0.0)
+        nc.scalar.activation(out=zout[:], in_=zin[:], func=ACT.Sin)
+
+        nt = const.tile([P, 2, NNEI], BF16, name="nt")
+        rt = const.tile([P, 2, 1], BF16, name="rt")
+        xw = const.tile([P, 32], BF16, name="xw")
+        nc.vector.memset(xw[:], 0.0)
+        with nc.allow_non_contiguous_dma(reason="a few short rows of time stamps"):
+            nc.sync.dma_start(out=nt[:], in_=neighbor_ts.rearrange("(h p) j -> p h j", p=P))
+            nc.sync.dma_start(out=rt[:], in_=root_ts.rearrange("(h p o) -> p h o", p=P, o=1))
+            nc.sync.dma_start(out=xw[0:32, 0:4], in_=time_w.rearrange("(p t) o -> p (t o)", t=4))
+            nc.sync.dma_start(out=xw[0:32, 16:20], in_=time_b.rearrange("(p t) -> p t", t=4))
+
+        wv_raw = []
+        wo_raw = []
+        chunks = {}
+
+        def load_w(dst, src, ct, width):
+            w = wraw.tile([P, CO], BF16, name="wr", tag="wr")
+            nc.sync.dma_start(out=w[:, 0:width], in_=src[ct * P : (ct + 1) * P, :])
+            dst.append(w)
+
+        def load_chunk(c):
+            nh = c // 5
+            j0 = 4 * (c % 5)
+            rows = slice(nh * P, (nh + 1) * P)
+            nd = vin.tile([P, 4 * DN], BF16, name="nd", tag="nd")
+            nc.sync.dma_start(
+                out=nd[:],
+                in_=neighbor_node_feature[rows, j0 : j0 + 4, :].rearrange("p j k -> p (j k)"),
+            )
+            ed = vin.tile([P, 4 * DE + 128], BF16, name="ed", tag="ed")
+            nc.gpsimd.memset(ed[:, 4 * DE : 4 * DE + 128], 0.0)
+            nc.sync.dma_start(
+                out=ed[:, 0 : 4 * DE],
+                in_=neighbor_edge_feature[rows, j0 : j0 + 4, :].rearrange("p j k -> p (j k)"),
+            )
+            chunks[c] = (nd, ed)
+
+        for ct in range(4):
+            load_w(wv_raw, wv_w, ct, 1024)
+        load_chunk(0)
+        for ct in range(4, 8):
+            load_w(wv_raw, wv_w, ct, 1024)
+        load_chunk(1)
+        attb = const.tile([P, 2, 2 * NNEI], BF16, name="attb")
+        with nc.allow_non_contiguous_dma(reason="80-byte rows of attention weights"):
+            nc.sync.dma_start(out=attb[:], in_=att.rearrange("(h p) j c -> p h (j c)", p=P))
+        wvb = const.tile([P, DOUT], BF16, name="wvb")
+        nc.sync.dma_start(out=wvb[:], in_=wv_b.partition_broadcast(P))
+        load_chunk(2)
+
+        wvc = const.tile([P, 2, DOUT], U32, name="wvc", align_bytes=64)
+        wvs = const.tile([P, 2, DOUT], U8, name="wvs", align_bytes=64)
+        woc = const.tile([P, 3, DOUT], U32, name="woc", align_bytes=64)
+        wos = const.tile([P, 3, DOUT], U8, name="wos", align_bytes=64)
+        rcc = const.tile([P, 256], U32, name="rcc", align_bytes=64)
+        rcs = const.tile([P, 256], U8, name="rcs", align_bytes=64)
+        ccc = const.tile([P, 2, 256], U32, name="ccc", align_bytes=64)
+        ccs = const.tile([P, 2, 256], U8, name="ccs", align_bytes=64)
+        g1seg = []
+        for a in range(4):
+            g1t = const.tile([P, 1280 * 4], BF16, name="g1seg%d" % a, align_bytes=64)
+            g1seg.append(g1t)
+        acc = []
+        acc2 = []
+        for nh in range(2):
+            acc_t = const.tile([P, DOUT], F32, name="acc%d" % nh)
+            acc.append(acc_t)
+            acc2_t = const.tile([P, 512], F32, name="accb%d" % nh)
+            acc2.append(acc2_t)
+
+        def words(ap):
+            return ap.bitcast(F32).rearrange("p (i r u) -> p i r u", i=2, u=2)
+
+        def unit4(srcs, dst_words, evac, parts, pool, tag):
+            t = pool.tile([P, 2, 2, P], F32, name="tr", tag=tag)
+            for s in range(4):
+                nc.tensor.transpose(t[:, s // 2, s % 2, :], srcs[s], identf[:])
+            evac(out=dst_words, in_=t[0:parts].rearrange("p i u r -> p i r u"))
+
+        with tc.tile_pool(name="tfp", bufs=1) as tfp:
+            lnt = tfp.tile([P, 10, P], BF16, name="lnt")
+            nc.vector.tensor_copy(
+                out=lnt[:].rearrange("p l (a q) -> p l a q", a=4),
+                in_=nt[:]
+                .rearrange("p h j -> p (h j)")
+                .rearrange("p (a l) -> p l a", a=4)
+                .unsqueeze(3)
+                .to_broadcast([P, 10, 4, 32]),
+            )
+            lrt = tfp.tile([P, P], BF16, name="lrt")
+            nc.vector.tensor_copy(
+                out=lrt[:].rearrange("p (h q) -> p h q", h=2),
+                in_=rt[:].to_broadcast([P, 2, 64]),
+            )
+            prm = ps_v.tile([P, 512], F32, name="prm", tag="v")
+            nc.tensor.matmul(out=prm[:, 0:32], lhsT=sel[:], rhs=xw[:], start=True, stop=True)
+            pa = const.tile([P, 4], F32, name="pa")
+            pb = const.tile([P, 4], F32, name="pb")
+            nc.vector.tensor_scalar_mul(out=pa[:], in0=prm[:, 0:4], scalar1=0.5 / math.pi)
+            nc.vector.tensor_scalar(
+                out=pb[:],
+                in0=prm[:, 16:20],
+                scalar1=0.5 / math.pi,
+                scalar2=0.25,
+                op0=ALU.mult,
+                op1=ALU.add,
+            )
+            dts = tfp.tile([P, 1280], F32, name="dts")
+            for b in range(3):
+                nl = min(4, 10 - 4 * b)
+                dtp = ps_v.tile([P, 512], F32, name="dtp", tag="v")
+                for l in range(nl):
+                    cols = slice(l * P, (l + 1) * P)
+                    nc.tensor.matmul(
+                        out=dtp[:, cols], lhsT=lrt[:], rhs=identb[:], start=True, stop=False
+                    )
+                    nc.tensor.matmul(
+                        out=dtp[:, cols], lhsT=lnt[:, 4 * b + l, :], rhs=negi[:], start=False, stop=True
+                    )
+                nc.scalar.copy(out=dts[:, 512 * b : 512 * b + nl * P], in_=dtp[:, 0 : nl * P])
+            for c0, cw in TF_CHUNKS:
+                ut = tfp.tile([P, 4, 512], F32, name="ut", tag="ut", bufs=2)
+                kt = tfp.tile([P, 4, 512], I32, name="kt", tag="kt", bufs=2)
+                for t in range(4):
+                    nc.scalar.activation(
+                        out=ut[:, t, 0:cw],
+                        in_=dts[:, c0 : c0 + cw],
+                        func=ACT.Identity,
+                        scale=pa[:, t : t + 1],
+                        bias=pb[:, t : t + 1],
+                    )
+                    nc.gpsimd.tensor_scalar(
+                        out=kt[:, t, 0:cw],
+                        in0=dts[:, c0 : c0 + cw],
+                        scalar1=pa[:, t : t + 1],
+                        scalar2=pb[:, t : t + 1],
+                        op0=ALU.mult,
+                        op1=ALU.add,
+                    )
+                gt = tfp.tile([P, 512, 4], F32, name="gt", tag="gt")
+                nc.vector.tensor_tensor(
+                    out=gt[:, 0:cw, :],
+                    in0=ut[:, :, 0:cw].rearrange("p t w -> p w t"),
+                    in1=kt[:, :, 0:cw].rearrange("p t w -> p w t"),
+                    op=ALU.subtract,
+                )
+                tfg = tfp.tile([P, 512 * 4], BF16, name="tfg", tag="tfg")
+                nc.scalar.activation(
+                    out=tfg[:, 0 : 4 * cw],
+                    in_=gt[:, 0:cw, :].rearrange("p w t -> p (w t)"),
+                    func=ACT.Sin,
+                    scale=2.0 * math.pi,
+                )
+                for a in range(4):
+                    nc.scalar.dma_start(
+                        out=g1seg[a][96:128, 4 * c0 : 4 * (c0 + cw)],
+                        in_=tfg[32 * a : 32 * a + 32, 0 : 4 * cw],
+                    )
+
+        late = es.enter_context(tc.tile_pool(name="late", bufs=1))
+
+        attf = const.tile([P, 2, NNEI, 2], F32, name="attf")
+        nc.vector.tensor_copy(out=attf[:].rearrange("p h j c -> p h (j c)"), in_=attb[:])
+        satt = const.tile([P, 2, 2], F32, name="satt")
+        nc.vector.tensor_reduce(
+            out=satt[:], in_=attf[:].rearrange("p h j c -> p h c j"), axis=AX.X, op=ALU.add
+        )
+        for nh in range(2):
+            for ch in range(2):
+                nc.gpsimd.tensor_scalar(
+                    out=acc[nh][:, ch * 512 : (ch + 1) * 512],
+                    in0=wvb[:, ch * 512 : (ch + 1) * 512],
+                    scalar1=satt[:, nh, ch : ch + 1],
+                    scalar2=0.0,
+                    op0=ALU.mult,
+                    op1=ALU.add,
+                )
+
+        def weight_unit(raw, g, ch, pair, natural, state, evac, pool, tag, codes, scales):
+            if pair == 0:
+                wg_t = wgp.tile([P, 2048], BF16, name="wg", tag="wg", align_bytes=64)
+                state["wg"] = wg_t
+            wg = state["wg"]
+            srcs = []
+            for i in range(2):
+                w = raw[ch * 4 + pair * 2 + i]
+                ww = w[:].bitcast(F32)
+                for u in range(2):
+                    if natural:
+                        srcs.append(
+                            ww[:, 256 * g : 256 * g + 256].rearrange("p (w u) -> p w u", u=2)[:, :, u]
+                        )
+                    else:
+                        srcs.append(ww[:, 256 * g + 128 * u : 256 * g + 128 * u + 128])
+            unit4(srcs, words(wg[:, pair * 1024 : (pair + 1) * 1024]), evac, P, pool, tag)
+            if pair == 1:
+                nc.vector.quantize_mx(
+                    out=codes[:, g, ch * 512 : (ch + 1) * 512].bitcast(FP8X4),
+                    scales=scales[:, g, ch * 512 : (ch + 1) * 512],
+                    in_=wg[:],
+                )
+
+        wstate = {}
+        for ch in range(2):
+            for g in range(2):
+                for pair in range(2):
+                    weight_unit(
+                        wv_raw, g, ch, pair, g == 1, wstate, nc.vector.tensor_copy, ps_v, "v", wvc, wvs
+                    )
+
+        for ct in range(8):
+            load_w(wo_raw, wo_w, ct, CO)
+        rootb = const.tile([P, 2, DN], BF16, name="rootb")
+        nc.sync.dma_start(out=rootb[:], in_=root_node_feature.rearrange("(h p) k -> p h k", p=P))
+        wob = const.tile([P, DOUT], BF16, name="wob")
+        nc.sync.dma_start(out=wob[:], in_=wo_b.partition_broadcast(P))
+        lng = const.tile([P, DOUT], BF16, name="lng")
+        nc.sync.dma_start(out=lng[:], in_=ln_g.partition_broadcast(P))
+        lnb = const.tile([P, DOUT], BF16, name="lnb")
+        nc.sync.dma_start(out=lnb[:], in_=ln_b.partition_broadcast(P))
+
+        wo_units = []
+        for g in range(3):
+            for ch in range(2):
+                for pair in range(2):
+                    wo_units.append((g, ch, pair))
+
+        staged = {}
+        quant = {}
+        banks = {}
+
+        def transposes(g):
+            nd, ed = chunks[g // 2]
+            jj = 2 * (g % 2)
+            ndw = nd[:].bitcast(F32)
+            edw = ed[:].bitcast(F32)
+            srcs_a = []
+            srcs_b = []
+            for i in range(2):
+                for u in range(2):
+                    lo = (jj + i) * 256 + 128 * u
+                    srcs_a.append(ndw[:, lo : lo + 128])
+                    eo = (jj + i) * 192
+                    srcs_b.append(edw[:, eo : eo + 256].rearrange("p (w u) -> p w u", u=2)[:, :, u])
+            g0 = stg.tile([P, 1024], BF16, name="g0", tag="g0", align_bytes=64)
+            unit4(srcs_a, words(g0[:]), nc.scalar.copy, P, ps_t, "ta")
+            seg = g1seg[g // 5]
+            cl = g % 5
+            unit4(
+                srcs_b, words(seg[0:96, cl * 1024 : (cl + 1) * 1024]), nc.scalar.copy, 96, ps_t, "tb"
+            )
+            staged[g] = g0
+
+        def quantise(g):
+            g0 = staged[g]
+            seg = g1seg[g // 5]
+            cl = g % 5
+            c0 = stg.tile([P, 256], U32, name="c0", tag="c0", align_bytes=64)
+            s0 = stg.tile([P, 256], U8, name="s0", tag="s0", align_bytes=64)
+            c1 = stg.tile([P, 256], U32, name="c1", tag="c1", align_bytes=64)
+            s1 = stg.tile([P, 256], U8, name="s1", tag="s1", align_bytes=64)
+            nc.vector.quantize_mx(out=c0[:].bitcast(FP8X4), scales=s0[:], in_=g0[:])
+            nc.vector.quantize_mx(
+                out=c1[:].bitcast(FP8X4), scales=s1[:], in_=seg[:, cl * 1024 : (cl + 1) * 1024]
+            )
+            quant[g] = ((c0, s0), (c1, s1))
+
+        def multiply(g):
+            ops = quant[g]
+            for i in range(2):
+                rows = slice(i * P, (i + 1) * P)
+                pair = []
+                for ch in range(2):
+                    v = ps_v.tile([P, 512], F32, name="v", tag="v")
+                    pair.append(v)
+                for k in range(2):
+                    cod, sca = ops[k]
+                    for ch in range(2):
+                        cs = slice(ch * 512, (ch + 1) * 512)
+                        nc.tensor.matmul_mx(
+                            out=pair[ch][:],
+                            lhsT=cod[:, rows].bitcast(FP8X4),
+                            lhsT_scale=sca[:, rows],
+                            rhs=wvc[:, k, cs].bitcast(FP8X4),
+                            rhs_scale=wvs[:, k, cs],
+                            start=(k == 0),
+                            stop=(k == 1),
+                        )
+                banks[(g, i)] = pair
+
+        def pool_rows(g):
+            nh = g // 10
+            for i in range(2):
+                j = 2 * (g % 10) + i
+                pair = banks[(g, i)]
+                for ch in range(2):
+                    w = attf[:, nh, j, ch : ch + 1]
+                    if i == 1 and ch == 1:
+                        if g % 10 == 0:
+                            nc.scalar.activation(out=acc2[nh][:], in_=pair[ch][:], func=ACT.Copy, scale=w)
+                        else:
+                            tmp = stg.tile([P, 512], F32, name="tmp", tag="tmp")
+                            nc.scalar.activation(out=tmp[:], in_=pair[ch][:], func=ACT.Copy, scale=w)
+                            nc.gpsimd.tensor_tensor(out=acc2[nh][:], in0=acc2[nh][:], in1=tmp[:], op=ALU.add)
+                    else:
+                        a = acc[nh][:, ch * 512 : (ch + 1) * 512]
+                        nc.vector.scalar_tensor_tensor(
+                            out=a, in0=pair[ch][:], scalar=w, in1=a, op0=ALU.mult, op1=ALU.add
+                        )
+
+        pbt = {}
+
+        def pooled_round(nh):
+            pbf = late.tile([P, 4, 2, P], BF16, name="pbf", tag="pbf")
+            lo = acc[nh][:, 0:512].rearrange("p (q i e) -> p q e i", q=2, e=2)
+            hi = acc[nh][:, 512:1024].rearrange("p (q i e) -> p q e i", q=2, e=2)
+            hi2 = acc2[nh][:].rearrange("p (q i e) -> p q e i", q=2, e=2)
+            nc.vector.tensor_copy(out=pbf[:, 0:2], in_=lo)
+            nc.vector.tensor_tensor(out=pbf[:, 2:4], in0=hi, in1=hi2, op=ALU.add)
+            pbt[nh] = pbf
+
+        def pooled_quantise(nh):
+            pbf = pbt[nh]
+            pt = ps_t.tile([P, 8, P], BF16, name="pt", tag="tc")
+            for s in range(8):
+                nc.tensor.transpose(pt[:, s, :], pbf[:, s // 2, s % 2, :], identb[:])
+            cg = late.tile([P, 1024], BF16, name="cg", tag="cg", align_bytes=64)
+            nc.scalar.copy(
+                out=cg[:].rearrange("p (g n t) -> p g n t", g=2, t=4),
+                in_=pt[:].rearrange("p (g t) n -> p g n t", g=2),
+            )
+            nc.vector.quantize_mx(out=ccc[:, nh, :].bitcast(FP8X4), scales=ccs[:, nh, :], in_=cg[:])
+
+        def output_rows(nh):
+            hb = late.tile([P, DOUT], F32, name="hb", tag="hb")
+            for ch in range(2):
+                cs = slice(ch * 512, (ch + 1) * 512)
+                h = ps_v.tile([P, 512], F32, name="h", tag="v")
+                for g in range(3):
+                    if g < 2:
+                        lt = ccc[:, nh, g * P : (g + 1) * P]
+                        ls = ccs[:, nh, g * P : (g + 1) * P]
+                    else:
+                        lt = rcc[:, nh * P : (nh + 1) * P]
+                        ls = rcs[:, nh * P : (nh + 1) * P]
+                    nc.tensor.matmul_mx(
+                        out=h[:],
+                        lhsT=lt.bitcast(FP8X4),
+                        lhsT_scale=ls,
+                        rhs=woc[:, g, cs].bitcast(FP8X4),
+                        rhs_scale=wos[:, g, cs],
+                        start=(g == 0),
+                        stop=(g == 2),
+                    )
+                nc.vector.tensor_tensor(out=hb[:, cs], in0=h[:], in1=wob[:, cs], op=ALU.add)
+            rl = late.tile([P, DOUT], F32, name="rl", tag="rl")
+            nc.scalar.activation(out=rl[:], in_=hb[:], func=ACT.Relu)
+            st = late.tile([P, 2, 6], F32, name="st", tag="st")
+            for ch in range(2):
+                nc.vector.bn_stats(out=st[:, ch, :], in_=rl[:, ch * 512 : (ch + 1) * 512])
+            mv = late.tile([P, 2], F32, name="mv", tag="mv")
+            nc.vector.bn_aggr(out=mv[:], in_=st[:].rearrange("p a b -> p (a b)"))
+            y1 = late.tile([P, DOUT], F32, name="y1", tag="hb")
+            nc.vector.scalar_tensor_tensor(
+                out=y1[:], in0=rl[:], scalar=mv[:, 0:1], in1=lng[:], op0=ALU.subtract, op1=ALU.mult
+            )
+            ve = late.tile([P, 1], F32, name="ve", tag="ve")
+            nc.vector.tensor_scalar_add(out=ve[:], in0=mv[:, 1:2], scalar1=LN_EPS)
+            sd = late.tile([P, 1], F32, name="sd", tag="sd")
+            nc.scalar.sqrt(out=sd[:], in_=ve[:])
+            rs = late.tile([P, 1], F32, name="rs", tag="rs")
+            nc.vector.reciprocal(out=rs[:], in_=sd[:])
+            yo = late.tile([P, DOUT], F32, name="yo", tag="rl")
+            nc.vector.scalar_tensor_tensor(
+                out=yo[:], in0=y1[:], scalar=rs[:, 0:1], in1=lnb[:], op0=ALU.mult, op1=ALU.add
+            )
+            nc.sync.dma_start(out=out[nh * P : (nh + 1) * P, :], in_=yo[:])
+
+        def root_unit():
+            rw = rootb[:].bitcast(F32)
+            srcs = []
+            for nh in range(2):
+                for u in range(2):
+                    srcs.append(rw[:, nh, 128 * u : 128 * u + 128])
+            rg = late.tile([P, 1024], BF16, name="rg", align_bytes=64)
+            unit4(srcs, words(rg[:]), nc.scalar.copy, P, ps_t, "tc")
+            nc.vector.quantize_mx(out=rcc[:].bitcast(FP8X4), scales=rcs[:], in_=rg[:])
+
+        transposes(0)
+        quantise(0)
+        transposes(1)
+        quantise(1)
+        wost = {}
+        for g in range(20):
+            multiply(g)
+            if g + 2 < 20:
+                if (g + 2) % 2 == 0 and (g + 2) // 2 + 2 < 10 and (g + 2) // 2 + 2 >= 3:
+                    load_chunk((g + 2) // 2 + 2)
+                transposes(g + 2)
+            if g < 12:
+                wg_, wch, wpair = wo_units[g]
+                weight_unit(wo_raw, wg_, wch, wpair, False, wost, nc.scalar.copy, ps_t, "tc", woc, wos)
+            if g == 12:
+                root_unit()
+            pool_rows(g)
+            if g + 2 < 20:
+                quantise(g + 2)
+            if g == 10:
+                pooled_round(0)
+            if g == 11:
+                pooled_quantise(0)
+            if g == 13:
+                output_rows(0)
+        pooled_round(1)
+        pooled_quantise(1)
+        output_rows(1)

@@ -15,16 +15,17 @@ ACT = mybir.ActivationFunctionType
 AX = mybir.AxisListType
 
 P = 128
-NROOT = 256
 NNEI = 20
 DN = 512
 DE = 384
 DOUT = 1024
 CO = 1536
 LN_EPS = 1e-5
-FLOPS = 2 * NROOT * NNEI * 1024 * DOUT + 2 * NROOT * CO * DOUT
-
-TF_CHUNKS = ((0, 256), (256, 512), (768, 512))
+FLOPS = 2 * 256 * NNEI * 1024 * DOUT + 2 * 256 * CO * DOUT
+NG = 20
+NBUF = 5
+LT = 4
+LQ = 2
 
 
 def tile_transformeraggregator_pb_t_kernel(
@@ -49,76 +50,70 @@ def tile_transformeraggregator_pb_t_kernel(
     with ExitStack() as es:
         const = es.enter_context(tc.tile_pool(name="const", bufs=1))
         wraw = es.enter_context(tc.tile_pool(name="wraw", bufs=8))
-        wgp = es.enter_context(tc.tile_pool(name="wgp", bufs=2))
-        vin = es.enter_context(tc.tile_pool(name="vin", bufs=3))
-        stg = es.enter_context(tc.tile_pool(name="stg", bufs=3))
+        wgp = es.enter_context(tc.tile_pool(name="wgp", bufs=3))
+        stg = es.enter_context(tc.tile_pool(name="stg", bufs=4))
+        tfp = es.enter_context(tc.tile_pool(name="tfp", bufs=1))
+        late = es.enter_context(tc.tile_pool(name="late", bufs=1))
         ps_t = es.enter_context(tc.psum_pool(name="ps_t", bufs=1))
         ps_v = es.enter_context(tc.psum_pool(name="ps_v", bufs=5))
+        es.enter_context(tc.manual_schedule())
 
         identf = const.tile([P, P], F32, name="identf")
         make_identity(nc, identf[:])
         identb = const.tile([P, P], BF16, name="identb")
         make_identity(nc, identb[:])
-        negi = const.tile([P, P], BF16, name="negi")
-        nc.vector.tensor_scalar_mul(out=negi[:], in0=identb[:], scalar1=-1.0)
-        sel = const.tile([P, P], BF16, name="sel")
-        nc.vector.tensor_copy(
-            out=sel[:].rearrange("p (a q) -> p a q", a=4),
-            in_=identb[:, 0:32].unsqueeze(1).to_broadcast([P, 4, 32]),
-        )
         zin = const.tile([P, 1], F32, name="zin")
         zout = const.tile([P, 1], F32, name="zout")
         nc.vector.memset(zin[:], 0.0)
         nc.scalar.activation(out=zout[:], in_=zin[:], func=ACT.Sin)
+        xw = const.tile([P, 32], BF16, name="xw")
+        nc.vector.memset(xw[:], 0.0)
+        nds = []
+        eds = []
+        for b in range(NBUF):
+            nd_t = const.tile([P, 2 * DN], BF16, name="nd%d" % b)
+            nds.append(nd_t)
+            ed_t = const.tile([P, 2 * DE + 128], BF16, name="ed%d" % b)
+            nc.vector.memset(ed_t[:, 2 * DE : 2 * DE + 128], 0.0)
+            eds.append(ed_t)
 
         nt = const.tile([P, 2, NNEI], BF16, name="nt")
         rt = const.tile([P, 2, 1], BF16, name="rt")
-        xw = const.tile([P, 32], BF16, name="xw")
-        nc.vector.memset(xw[:], 0.0)
-        with nc.allow_non_contiguous_dma(reason="a few short rows of time stamps"):
+        attb = const.tile([P, 2, 2 * NNEI], BF16, name="attb")
+        with nc.allow_non_contiguous_dma(reason="a few short rows of time stamps and weights"):
             nc.sync.dma_start(out=nt[:], in_=neighbor_ts.rearrange("(h p) j -> p h j", p=P))
             nc.sync.dma_start(out=rt[:], in_=root_ts.rearrange("(h p o) -> p h o", p=P, o=1))
             nc.sync.dma_start(out=xw[0:32, 0:4], in_=time_w.rearrange("(p t) o -> p (t o)", t=4))
             nc.sync.dma_start(out=xw[0:32, 16:20], in_=time_b.rearrange("(p t) -> p t", t=4))
+            nc.sync.dma_start(out=attb[:], in_=att.rearrange("(h p) j c -> p h (j c)", p=P))
 
         wv_raw = []
         wo_raw = []
-        chunks = {}
 
         def load_w(dst, src, ct, width):
             w = wraw.tile([P, CO], BF16, name="wr", tag="wr")
             nc.sync.dma_start(out=w[:, 0:width], in_=src[ct * P : (ct + 1) * P, :])
             dst.append(w)
 
-        def load_chunk(c):
-            nh = c // 5
-            j0 = 4 * (c % 5)
-            rows = slice(nh * P, (nh + 1) * P)
-            nd = vin.tile([P, 4 * DN], BF16, name="nd", tag="nd")
+        def load_group(g):
+            rows = slice((g // 10) * P, (g // 10 + 1) * P)
+            j0 = 2 * (g % 10)
             nc.sync.dma_start(
-                out=nd[:],
-                in_=neighbor_node_feature[rows, j0 : j0 + 4, :].rearrange("p j k -> p (j k)"),
+                out=nds[g % NBUF][:],
+                in_=neighbor_node_feature[rows, j0 : j0 + 2, :].rearrange("p j k -> p (j k)"),
             )
-            ed = vin.tile([P, 4 * DE + 128], BF16, name="ed", tag="ed")
-            nc.gpsimd.memset(ed[:, 4 * DE : 4 * DE + 128], 0.0)
             nc.sync.dma_start(
-                out=ed[:, 0 : 4 * DE],
-                in_=neighbor_edge_feature[rows, j0 : j0 + 4, :].rearrange("p j k -> p (j k)"),
+                out=eds[g % NBUF][:, 0 : 2 * DE],
+                in_=neighbor_edge_feature[rows, j0 : j0 + 2, :].rearrange("p j k -> p (j k)"),
             )
-            chunks[c] = (nd, ed)
 
-        for ct in range(4):
+        for ct in range(8):
             load_w(wv_raw, wv_w, ct, 1024)
-        load_chunk(0)
-        for ct in range(4, 8):
-            load_w(wv_raw, wv_w, ct, 1024)
-        load_chunk(1)
-        attb = const.tile([P, 2, 2 * NNEI], BF16, name="attb")
-        with nc.allow_non_contiguous_dma(reason="80-byte rows of attention weights"):
-            nc.sync.dma_start(out=attb[:], in_=att.rearrange("(h p) j c -> p h (j c)", p=P))
+        load_group(0)
         wvb = const.tile([P, DOUT], BF16, name="wvb")
         nc.sync.dma_start(out=wvb[:], in_=wv_b.partition_broadcast(P))
-        load_chunk(2)
+        for g in range(1, NBUF):
+            load_group(g)
 
         wvc = const.tile([P, 2, DOUT], U32, name="wvc", align_bytes=64)
         wvs = const.tile([P, 2, DOUT], U8, name="wvs", align_bytes=64)
@@ -128,10 +123,6 @@ def tile_transformeraggregator_pb_t_kernel(
         rcs = const.tile([P, 256], U8, name="rcs", align_bytes=64)
         ccc = const.tile([P, 2, 256], U32, name="ccc", align_bytes=64)
         ccs = const.tile([P, 2, 256], U8, name="ccs", align_bytes=64)
-        g1seg = []
-        for a in range(4):
-            g1t = const.tile([P, 1280 * 4], BF16, name="g1seg%d" % a, align_bytes=64)
-            g1seg.append(g1t)
         acc = []
         acc2 = []
         for nh in range(2):
@@ -149,94 +140,355 @@ def tile_transformeraggregator_pb_t_kernel(
                 nc.tensor.transpose(t[:, s // 2, s % 2, :], srcs[s], identf[:])
             evac(out=dst_words, in_=t[0:parts].rearrange("p i u r -> p i r u"))
 
-        with tc.tile_pool(name="tfp", bufs=1) as tfp:
-            lnt = tfp.tile([P, 10, P], BF16, name="lnt")
+        negi = const.tile([P, P], BF16, name="negi")
+        nc.vector.tensor_scalar_mul(out=negi[:], in0=identb[:], scalar1=-1.0)
+        sel = const.tile([P, P], BF16, name="sel")
+        nc.vector.tensor_copy(
+            out=sel[:].rearrange("p (a q) -> p a q", a=4),
+            in_=identb[:, 0:32].unsqueeze(1).to_broadcast([P, 4, 32]),
+        )
+        lnt = const.tile([P, 5, 2, P], BF16, name="lnt")
+        nt40 = nt[:].rearrange("p h j -> p (h j)").rearrange("p (m a i) -> p m i a", m=5, a=4)
+        for i in range(2):
             nc.vector.tensor_copy(
-                out=lnt[:].rearrange("p l (a q) -> p l a q", a=4),
-                in_=nt[:]
-                .rearrange("p h j -> p (h j)")
-                .rearrange("p (a l) -> p l a", a=4)
-                .unsqueeze(3)
-                .to_broadcast([P, 10, 4, 32]),
+                out=lnt[:, :, i, :].rearrange("p m (a q) -> p m a q", a=4),
+                in_=nt40[:, :, i, :].unsqueeze(3).to_broadcast([P, 5, 4, 32]),
             )
-            lrt = tfp.tile([P, P], BF16, name="lrt")
-            nc.vector.tensor_copy(
-                out=lrt[:].rearrange("p (h q) -> p h q", h=2),
-                in_=rt[:].to_broadcast([P, 2, 64]),
-            )
-            prm = ps_v.tile([P, 512], F32, name="prm", tag="v")
-            nc.tensor.matmul(out=prm[:, 0:32], lhsT=sel[:], rhs=xw[:], start=True, stop=True)
-            pa = const.tile([P, 4], F32, name="pa")
-            pb = const.tile([P, 4], F32, name="pb")
-            nc.vector.tensor_scalar_mul(out=pa[:], in0=prm[:, 0:4], scalar1=0.5 / math.pi)
-            nc.vector.tensor_scalar(
-                out=pb[:],
-                in0=prm[:, 16:20],
-                scalar1=0.5 / math.pi,
-                scalar2=0.25,
-                op0=ALU.mult,
-                op1=ALU.add,
-            )
-            dts = tfp.tile([P, 1280], F32, name="dts")
-            for b in range(3):
-                nl = min(4, 10 - 4 * b)
-                dtp = ps_v.tile([P, 512], F32, name="dtp", tag="v")
-                for l in range(nl):
-                    cols = slice(l * P, (l + 1) * P)
-                    nc.tensor.matmul(
-                        out=dtp[:, cols], lhsT=lrt[:], rhs=identb[:], start=True, stop=False
-                    )
-                    nc.tensor.matmul(
-                        out=dtp[:, cols], lhsT=lnt[:, 4 * b + l, :], rhs=negi[:], start=False, stop=True
-                    )
-                nc.scalar.copy(out=dts[:, 512 * b : 512 * b + nl * P], in_=dtp[:, 0 : nl * P])
-            for c0, cw in TF_CHUNKS:
-                ut = tfp.tile([P, 4, 512], F32, name="ut", tag="ut", bufs=2)
-                kt = tfp.tile([P, 4, 512], I32, name="kt", tag="kt", bufs=2)
-                for t in range(4):
-                    nc.scalar.activation(
-                        out=ut[:, t, 0:cw],
-                        in_=dts[:, c0 : c0 + cw],
-                        func=ACT.Identity,
-                        scale=pa[:, t : t + 1],
-                        bias=pb[:, t : t + 1],
-                    )
-                    nc.gpsimd.tensor_scalar(
-                        out=kt[:, t, 0:cw],
-                        in0=dts[:, c0 : c0 + cw],
-                        scalar1=pa[:, t : t + 1],
-                        scalar2=pb[:, t : t + 1],
-                        op0=ALU.mult,
-                        op1=ALU.add,
-                    )
-                gt = tfp.tile([P, 512, 4], F32, name="gt", tag="gt")
-                nc.vector.tensor_tensor(
-                    out=gt[:, 0:cw, :],
-                    in0=ut[:, :, 0:cw].rearrange("p t w -> p w t"),
-                    in1=kt[:, :, 0:cw].rearrange("p t w -> p w t"),
-                    op=ALU.subtract,
-                )
-                tfg = tfp.tile([P, 512 * 4], BF16, name="tfg", tag="tfg")
-                nc.scalar.activation(
-                    out=tfg[:, 0 : 4 * cw],
-                    in_=gt[:, 0:cw, :].rearrange("p w t -> p (w t)"),
-                    func=ACT.Sin,
-                    scale=2.0 * math.pi,
-                )
-                for a in range(4):
-                    nc.scalar.dma_start(
-                        out=g1seg[a][96:128, 4 * c0 : 4 * (c0 + cw)],
-                        in_=tfg[32 * a : 32 * a + 32, 0 : 4 * cw],
-                    )
+        lrt = const.tile([P, 3, P], BF16, name="lrt")
+        nc.vector.tensor_copy(out=lrt[:, 0, :], in_=rt[:, 0, :].to_broadcast([P, P]))
+        nc.vector.tensor_copy(
+            out=lrt[:, 1, :].rearrange("p (h q) -> p h q", h=2), in_=rt[:].to_broadcast([P, 2, 64])
+        )
+        nc.vector.tensor_copy(out=lrt[:, 2, :], in_=rt[:, 1, :].to_broadcast([P, P]))
+        lrt_of_m = (0, 0, 1, 2, 2)
 
-        late = es.enter_context(tc.tile_pool(name="late", bufs=1))
-
+        prm = ps_v.tile([P, 512], F32, name="prm", tag="v")
+        nc.tensor.matmul(out=prm[:, 0:32], lhsT=sel[:], rhs=xw[:], start=True, stop=True)
+        pa = const.tile([P, 4], F32, name="pa")
+        pb = const.tile([P, 4], F32, name="pb")
+        nc.vector.tensor_scalar_mul(out=pa[:], in0=prm[:, 0:4], scalar1=0.5 / math.pi)
+        nc.vector.tensor_scalar(
+            out=pb[:], in0=prm[:, 16:20], scalar1=0.5 / math.pi, scalar2=0.25, op0=ALU.mult, op1=ALU.add
+        )
         attf = const.tile([P, 2, NNEI, 2], F32, name="attf")
         nc.vector.tensor_copy(out=attf[:].rearrange("p h j c -> p h (j c)"), in_=attb[:])
         satt = const.tile([P, 2, 2], F32, name="satt")
         nc.vector.tensor_reduce(
             out=satt[:], in_=attf[:].rearrange("p h j c -> p h c j"), axis=AX.X, op=ALU.add
         )
+
+        dts = const.tile([P, 1280], F32, name="dts")
+        dt_banks = {}
+
+        def dt_bank(b):
+            nblk = min(4, 10 - 4 * b)
+            dtp = ps_v.tile([P, 512], F32, name="dtp", tag="v")
+            for l in range(nblk):
+                blk = 4 * b + l
+                cols = slice(l * P, (l + 1) * P)
+                nc.tensor.matmul(
+                    out=dtp[:, cols], lhsT=lrt[:, lrt_of_m[blk // 2], :], rhs=identb[:], start=True, stop=False
+                )
+                nc.tensor.matmul(
+                    out=dtp[:, cols], lhsT=lnt[:, blk // 2, blk % 2, :], rhs=negi[:], start=False, stop=True
+                )
+            dt_banks[b] = (dtp, nblk)
+
+        def dt_out(b):
+            dtp, nblk = dt_banks[b]
+            nc.scalar.copy(out=dts[:, 512 * b : 512 * b + nblk * P], in_=dtp[:, 0 : nblk * P])
+
+        tf_t = {}
+
+        def tf_affine(eng, dst, m, t):
+            eng.tensor_scalar(
+                out=dst[:, t, :],
+                in0=dts[:, 256 * m : 256 * (m + 1)],
+                scalar1=pa[:, t : t + 1],
+                scalar2=pb[:, t : t + 1],
+                op0=ALU.mult,
+                op1=ALU.add,
+            )
+
+        def tf_uk(m, split):
+            ut = tfp.tile([P, 4, 256], F32, name="ut", tag="ut")
+            kt = tfp.tile([P, 4, 256], I32, name="kt", tag="kt")
+            tf_t[m] = [ut, kt]
+            for t in range(4):
+                if split and t < 2:
+                    nc.scalar.activation(
+                        out=ut[:, t, :],
+                        in_=dts[:, 256 * m : 256 * (m + 1)],
+                        func=ACT.Identity,
+                        scale=pa[:, t : t + 1],
+                        bias=pb[:, t : t + 1],
+                    )
+                    tf_affine(nc.gpsimd, kt, m, t)
+                elif split:
+                    tf_affine(nc.vector, ut, m, t)
+                    tf_affine(nc.vector, kt, m, t)
+                else:
+                    tf_affine(nc.gpsimd, ut, m, t)
+                    tf_affine(nc.gpsimd, kt, m, t)
+
+        def tf_frac(m):
+            ut, kt = tf_t[m]
+            gt = tfp.tile([P, 256, 4], F32, name="gt", tag="gt")
+            nc.vector.tensor_tensor(
+                out=gt[:],
+                in0=ut[:].rearrange("p t w -> p w t"),
+                in1=kt[:].rearrange("p t w -> p w t"),
+                op=ALU.subtract,
+            )
+            tf_t[m] = [gt]
+
+        def tf_sin(m):
+            gt = tf_t[m][0]
+            tfg = tfp.tile([P, 1024], BF16, name="tfg", tag="tfg", bufs=2)
+            nc.scalar.activation(
+                out=tfg[:], in_=gt[:].rearrange("p w t -> p (w t)"), func=ACT.Sin, scale=2.0 * math.pi
+            )
+            tf_t[m] = [tfg]
+
+        ggs = {}
+
+        def get_gg(g):
+            if g not in ggs:
+                gg_t = stg.tile([P, 2048], BF16, name="gg", tag="gg", align_bytes=64)
+                ggs[g] = gg_t
+            return ggs[g]
+
+        def tf_dma(g):
+            a = g % 4
+            nc.scalar.dma_start(out=get_gg(g)[96:128, 1024:2048], in_=tf_t[g // 4][0][32 * a : 32 * a + 32, :])
+
+        def new_wg():
+            wg_t = wgp.tile([P, 2048], BF16, name="wg", tag="wg", align_bytes=64)
+            return wg_t
+
+        def weight_unit(raw, wg, g, ch, pair, natural, evac, pool, tag):
+            srcs = []
+            for i in range(2):
+                ww = raw[ch * 4 + pair * 2 + i][:].bitcast(F32)
+                for u in range(2):
+                    if natural:
+                        srcs.append(
+                            ww[:, 256 * g : 256 * g + 256].rearrange("p (w u) -> p w u", u=2)[:, :, u]
+                        )
+                    else:
+                        srcs.append(ww[:, 256 * g + 128 * u : 256 * g + 128 * u + 128])
+            unit4(srcs, words(wg[:, pair * 1024 : (pair + 1) * 1024]), evac, P, pool, tag)
+
+        def weight_quantise(wg, codes, scales, g, ch):
+            nc.vector.quantize_mx(
+                out=codes[:, g, ch * 512 : (ch + 1) * 512].bitcast(FP8X4),
+                scales=scales[:, g, ch * 512 : (ch + 1) * 512],
+                in_=wg[:],
+            )
+
+        quant = {}
+        banks = {}
+
+        def transposes(g):
+            ndw = nds[g % NBUF][:].bitcast(F32)
+            edw = eds[g % NBUF][:].bitcast(F32)
+            srcs_a = []
+            srcs_b = []
+            for i in range(2):
+                for u in range(2):
+                    lo = i * 256 + 128 * u
+                    srcs_a.append(ndw[:, lo : lo + 128])
+                    eo = i * 192
+                    srcs_b.append(edw[:, eo : eo + 256].rearrange("p (w u) -> p w u", u=2)[:, :, u])
+            gg = get_gg(g)
+            unit4(srcs_a, words(gg[:, 0:1024]), nc.scalar.copy, P, ps_t, "ta")
+            unit4(srcs_b, words(gg[0:96, 1024:2048]), nc.scalar.copy, 96, ps_t, "tb")
+
+        def quantise(g):
+            cq = stg.tile([P, 512], U32, name="cq", tag="cq", align_bytes=64)
+            sq = stg.tile([P, 512], U8, name="sq", tag="sq", align_bytes=64)
+            nc.vector.quantize_mx(out=cq[:].bitcast(FP8X4), scales=sq[:], in_=ggs[g][:])
+            quant[g] = (cq, sq)
+
+        def multiply(g, i):
+            cq, sq = quant[g]
+            pair = []
+            for ch in range(2):
+                v = ps_v.tile([P, 512], F32, name="v", tag="v")
+                pair.append(v)
+            for k in range(2):
+                rows = slice(k * 256 + i * P, k * 256 + (i + 1) * P)
+                for ch in range(2):
+                    cs = slice(ch * 512, (ch + 1) * 512)
+                    nc.tensor.matmul_mx(
+                        out=pair[ch][:],
+                        lhsT=cq[:, rows].bitcast(FP8X4),
+                        lhsT_scale=sq[:, rows],
+                        rhs=wvc[:, k, cs].bitcast(FP8X4),
+                        rhs_scale=wvs[:, k, cs],
+                        start=(k == 0),
+                        stop=(k == 1),
+                    )
+            banks[(g, i)] = pair
+
+        def offloaded(g, i, ch):
+            return i == 1 and ch == 1 and g % 10 < 8
+
+        def pool_rows(g, i):
+            nh = g // 10
+            j = 2 * (g % 10) + i
+            pair = banks[(g, i)]
+            for ch in range(2):
+                w = attf[:, nh, j, ch : ch + 1]
+                if offloaded(g, i, ch):
+                    if g % 10 == 0:
+                        nc.scalar.activation(out=acc2[nh][:], in_=pair[ch][:], func=ACT.Copy, scale=w)
+                    else:
+                        tmp = stg.tile([P, 512], F32, name="tmp", tag="tmp")
+                        nc.scalar.activation(out=tmp[:], in_=pair[ch][:], func=ACT.Copy, scale=w)
+                        nc.gpsimd.tensor_tensor(out=acc2[nh][:], in0=acc2[nh][:], in1=tmp[:], op=ALU.add)
+                else:
+                    a = acc[nh][:, ch * 512 : (ch + 1) * 512]
+                    nc.vector.scalar_tensor_tensor(
+                        out=a, in0=pair[ch][:], scalar=w, in1=a, op0=ALU.mult, op1=ALU.add
+                    )
+
+        ph = {}
+
+        def pooled_round(nh, h):
+            pbf = late.tile([P, 2, 2, P], BF16, name="pbf", tag="pbf%d" % h)
+            src = acc[nh][:, h * 512 : (h + 1) * 512].rearrange("p (q i e) -> p q e i", q=2, e=2)
+            if h == 0:
+                nc.scalar.copy(out=pbf[:], in_=src)
+            else:
+                nc.vector.tensor_tensor(
+                    out=pbf[:],
+                    in0=src,
+                    in1=acc2[nh][:].rearrange("p (q i e) -> p q e i", q=2, e=2),
+                    op=ALU.add,
+                )
+            ph[(nh, h)] = pbf
+
+        def pooled_transpose(nh, h, tag, evac):
+            pbf = ph[(nh, h)]
+            pt = ps_t.tile([P, 4, P], BF16, name="pt", tag=tag)
+            for s in range(4):
+                nc.tensor.transpose(pt[:, s, :], pbf[:, s // 2, s % 2, :], identb[:])
+            cg = late.tile([P, 512], BF16, name="cg", tag="cg%d" % h, align_bytes=64)
+            evac(out=cg[:].rearrange("p (n t) -> p n t", t=4), in_=pt[:].rearrange("p t n -> p n t"))
+            ph[(nh, h)] = cg
+
+        def pooled_quantise(nh, h):
+            cols = slice(h * P, (h + 1) * P)
+            nc.vector.quantize_mx(
+                out=ccc[:, nh, cols].bitcast(FP8X4), scales=ccs[:, nh, cols], in_=ph[(nh, h)][:]
+            )
+
+        hbank = {}
+
+        def out_pass(nh, g):
+            if g == 2:
+                pair = []
+                for o in range(2):
+                    h_t = ps_v.tile([P, 512], F32, name="h", tag="v")
+                    pair.append(h_t)
+                hbank[nh] = pair
+                lt = rcc[:, nh * P : (nh + 1) * P]
+                ls = rcs[:, nh * P : (nh + 1) * P]
+            else:
+                lt = ccc[:, nh, g * P : (g + 1) * P]
+                ls = ccs[:, nh, g * P : (g + 1) * P]
+            for o in range(2):
+                cs = slice(o * 512, (o + 1) * 512)
+                nc.tensor.matmul_mx(
+                    out=hbank[nh][o][:],
+                    lhsT=lt.bitcast(FP8X4),
+                    lhsT_scale=ls,
+                    rhs=woc[:, g, cs].bitcast(FP8X4),
+                    rhs_scale=wos[:, g, cs],
+                    start=(g == 2),
+                    stop=(g == 1),
+                )
+
+        ln = {}
+        halves = (slice(0, 512), slice(512, 1024))
+
+        def ln_bias(nh):
+            hb = late.tile([P, DOUT], F32, name="hb", tag="hb")
+            for o in range(2):
+                nc.vector.tensor_tensor(out=hb[:, halves[o]], in0=hbank[nh][o][:], in1=wob[:, halves[o]], op=ALU.add)
+            ln["hb"] = hb
+
+        def ln_relu(nh):
+            rl = late.tile([P, DOUT], F32, name="rl", tag="rl")
+            for o in range(2):
+                nc.scalar.activation(out=rl[:, halves[o]], in_=ln["hb"][:, halves[o]], func=ACT.Relu)
+            ln["rl"] = rl
+
+        def ln_stats(nh):
+            st = late.tile([P, 2, 6], F32, name="st", tag="st")
+            for o in range(2):
+                nc.vector.bn_stats(out=st[:, o, :], in_=ln["rl"][:, halves[o]])
+            mv = late.tile([P, 2], F32, name="mv", tag="mv")
+            nc.vector.bn_aggr(out=mv[:], in_=st[:].rearrange("p a b -> p (a b)"))
+            ve = late.tile([P, 1], F32, name="ve", tag="ve")
+            nc.vector.tensor_scalar_add(out=ve[:], in0=mv[:, 1:2], scalar1=LN_EPS)
+            ln["mv"] = mv
+            ln["ve"] = ve
+
+        def ln_sqrt(nh):
+            sd = late.tile([P, 1], F32, name="sd", tag="sd")
+            nc.scalar.sqrt(out=sd[:], in_=ln["ve"][:])
+            ln["sd"] = sd
+
+        def ln_centre(nh):
+            y1 = late.tile([P, DOUT], F32, name="y1", tag="y1")
+            for o in range(2):
+                nc.vector.scalar_tensor_tensor(
+                    out=y1[:, halves[o]],
+                    in0=ln["rl"][:, halves[o]],
+                    scalar=ln["mv"][:, 0:1],
+                    in1=lng[:, halves[o]],
+                    op0=ALU.subtract,
+                    op1=ALU.mult,
+                )
+            ln["y1"] = y1
+
+        def ln_finish(nh):
+            rs = late.tile([P, 1], F32, name="rs", tag="rs")
+            nc.vector.reciprocal(out=rs[:], in_=ln["sd"][:])
+            yo = late.tile([P, DOUT], F32, name="yo", tag="yo")
+            for o in range(2):
+                nc.vector.scalar_tensor_tensor(
+                    out=yo[:, halves[o]],
+                    in0=ln["y1"][:, halves[o]],
+                    scalar=rs[:, 0:1],
+                    in1=lnb[:, halves[o]],
+                    op0=ALU.mult,
+                    op1=ALU.add,
+                )
+                nc.sync.dma_start(out=out[nh * P : (nh + 1) * P, halves[o]], in_=yo[:, halves[o]])
+
+        vcopy = nc.vector.tensor_copy
+        scopy = nc.scalar.copy
+        dt_bank(0)
+        wg_a = new_wg()
+        wg_b = new_wg()
+        weight_unit(wv_raw, wg_a, 0, 0, 0, False, vcopy, ps_t, "ta")
+        weight_unit(wv_raw, wg_b, 1, 0, 0, True, scopy, ps_t, "tb")
+        dt_out(0)
+        tf_uk(0, True)
+        dt_bank(1)
+        dt_bank(2)
+        weight_unit(wv_raw, wg_a, 0, 0, 1, False, vcopy, ps_t, "tc")
+        weight_unit(wv_raw, wg_b, 1, 0, 1, True, scopy, ps_v, "v")
+        weight_quantise(wg_a, wvc, wvs, 0, 0)
+        tf_frac(0)
+        weight_quantise(wg_b, wvc, wvs, 1, 0)
+        tf_sin(0)
+        for g in range(3):
+            tf_dma(g)
+        tf_uk(1, False)
         for nh in range(2):
             for ch in range(2):
                 nc.gpsimd.tensor_scalar(
@@ -247,38 +499,16 @@ def tile_transformeraggregator_pb_t_kernel(
                     op0=ALU.mult,
                     op1=ALU.add,
                 )
-
-        def weight_unit(raw, g, ch, pair, natural, state, evac, pool, tag, codes, scales):
-            if pair == 0:
-                wg_t = wgp.tile([P, 2048], BF16, name="wg", tag="wg", align_bytes=64)
-                state["wg"] = wg_t
-            wg = state["wg"]
-            srcs = []
-            for i in range(2):
-                w = raw[ch * 4 + pair * 2 + i]
-                ww = w[:].bitcast(F32)
-                for u in range(2):
-                    if natural:
-                        srcs.append(
-                            ww[:, 256 * g : 256 * g + 256].rearrange("p (w u) -> p w u", u=2)[:, :, u]
-                        )
-                    else:
-                        srcs.append(ww[:, 256 * g + 128 * u : 256 * g + 128 * u + 128])
-            unit4(srcs, words(wg[:, pair * 1024 : (pair + 1) * 1024]), evac, P, pool, tag)
-            if pair == 1:
-                nc.vector.quantize_mx(
-                    out=codes[:, g, ch * 512 : (ch + 1) * 512].bitcast(FP8X4),
-                    scales=scales[:, g, ch * 512 : (ch + 1) * 512],
-                    in_=wg[:],
-                )
-
-        wstate = {}
-        for ch in range(2):
-            for g in range(2):
-                for pair in range(2):
-                    weight_unit(
-                        wv_raw, g, ch, pair, g == 1, wstate, nc.vector.tensor_copy, ps_v, "v", wvc, wvs
-                    )
+        wg_c = new_wg()
+        weight_unit(wv_raw, wg_c, 0, 1, 0, False, vcopy, ps_t, "ta")
+        wg_d = new_wg()
+        weight_unit(wv_raw, wg_d, 1, 1, 0, True, scopy, ps_t, "tb")
+        weight_unit(wv_raw, wg_c, 0, 1, 1, False, vcopy, ps_t, "tc")
+        weight_unit(wv_raw, wg_d, 1, 1, 1, True, scopy, ps_v, "v")
+        weight_quantise(wg_c, wvc, wvs, 0, 1)
+        weight_quantise(wg_d, wvc, wvs, 1, 1)
+        dt_out(1)
+        dt_out(2)
 
         for ct in range(8):
             load_w(wo_raw, wo_w, ct, CO)
@@ -291,162 +521,18 @@ def tile_transformeraggregator_pb_t_kernel(
         lnb = const.tile([P, DOUT], BF16, name="lnb")
         nc.sync.dma_start(out=lnb[:], in_=ln_b.partition_broadcast(P))
 
+        for g in range(LT):
+            transposes(g)
+            load_group(g + NBUF)
+        for g in range(LQ):
+            quantise(g)
+        tf_frac(1)
+
         wo_units = []
         for g in range(3):
             for ch in range(2):
                 for pair in range(2):
                     wo_units.append((g, ch, pair))
-
-        staged = {}
-        quant = {}
-        banks = {}
-
-        def transposes(g):
-            nd, ed = chunks[g // 2]
-            jj = 2 * (g % 2)
-            ndw = nd[:].bitcast(F32)
-            edw = ed[:].bitcast(F32)
-            srcs_a = []
-            srcs_b = []
-            for i in range(2):
-                for u in range(2):
-                    lo = (jj + i) * 256 + 128 * u
-                    srcs_a.append(ndw[:, lo : lo + 128])
-                    eo = (jj + i) * 192
-                    srcs_b.append(edw[:, eo : eo + 256].rearrange("p (w u) -> p w u", u=2)[:, :, u])
-            g0 = stg.tile([P, 1024], BF16, name="g0", tag="g0", align_bytes=64)
-            unit4(srcs_a, words(g0[:]), nc.scalar.copy, P, ps_t, "ta")
-            seg = g1seg[g // 5]
-            cl = g % 5
-            unit4(
-                srcs_b, words(seg[0:96, cl * 1024 : (cl + 1) * 1024]), nc.scalar.copy, 96, ps_t, "tb"
-            )
-            staged[g] = g0
-
-        def quantise(g):
-            g0 = staged[g]
-            seg = g1seg[g // 5]
-            cl = g % 5
-            c0 = stg.tile([P, 256], U32, name="c0", tag="c0", align_bytes=64)
-            s0 = stg.tile([P, 256], U8, name="s0", tag="s0", align_bytes=64)
-            c1 = stg.tile([P, 256], U32, name="c1", tag="c1", align_bytes=64)
-            s1 = stg.tile([P, 256], U8, name="s1", tag="s1", align_bytes=64)
-            nc.vector.quantize_mx(out=c0[:].bitcast(FP8X4), scales=s0[:], in_=g0[:])
-            nc.vector.quantize_mx(
-                out=c1[:].bitcast(FP8X4), scales=s1[:], in_=seg[:, cl * 1024 : (cl + 1) * 1024]
-            )
-            quant[g] = ((c0, s0), (c1, s1))
-
-        def multiply(g):
-            ops = quant[g]
-            for i in range(2):
-                rows = slice(i * P, (i + 1) * P)
-                pair = []
-                for ch in range(2):
-                    v = ps_v.tile([P, 512], F32, name="v", tag="v")
-                    pair.append(v)
-                for k in range(2):
-                    cod, sca = ops[k]
-                    for ch in range(2):
-                        cs = slice(ch * 512, (ch + 1) * 512)
-                        nc.tensor.matmul_mx(
-                            out=pair[ch][:],
-                            lhsT=cod[:, rows].bitcast(FP8X4),
-                            lhsT_scale=sca[:, rows],
-                            rhs=wvc[:, k, cs].bitcast(FP8X4),
-                            rhs_scale=wvs[:, k, cs],
-                            start=(k == 0),
-                            stop=(k == 1),
-                        )
-                banks[(g, i)] = pair
-
-        def pool_rows(g):
-            nh = g // 10
-            for i in range(2):
-                j = 2 * (g % 10) + i
-                pair = banks[(g, i)]
-                for ch in range(2):
-                    w = attf[:, nh, j, ch : ch + 1]
-                    if i == 1 and ch == 1:
-                        if g % 10 == 0:
-                            nc.scalar.activation(out=acc2[nh][:], in_=pair[ch][:], func=ACT.Copy, scale=w)
-                        else:
-                            tmp = stg.tile([P, 512], F32, name="tmp", tag="tmp")
-                            nc.scalar.activation(out=tmp[:], in_=pair[ch][:], func=ACT.Copy, scale=w)
-                            nc.gpsimd.tensor_tensor(out=acc2[nh][:], in0=acc2[nh][:], in1=tmp[:], op=ALU.add)
-                    else:
-                        a = acc[nh][:, ch * 512 : (ch + 1) * 512]
-                        nc.vector.scalar_tensor_tensor(
-                            out=a, in0=pair[ch][:], scalar=w, in1=a, op0=ALU.mult, op1=ALU.add
-                        )
-
-        pbt = {}
-
-        def pooled_round(nh):
-            pbf = late.tile([P, 4, 2, P], BF16, name="pbf", tag="pbf")
-            lo = acc[nh][:, 0:512].rearrange("p (q i e) -> p q e i", q=2, e=2)
-            hi = acc[nh][:, 512:1024].rearrange("p (q i e) -> p q e i", q=2, e=2)
-            hi2 = acc2[nh][:].rearrange("p (q i e) -> p q e i", q=2, e=2)
-            nc.vector.tensor_copy(out=pbf[:, 0:2], in_=lo)
-            nc.vector.tensor_tensor(out=pbf[:, 2:4], in0=hi, in1=hi2, op=ALU.add)
-            pbt[nh] = pbf
-
-        def pooled_quantise(nh):
-            pbf = pbt[nh]
-            pt = ps_t.tile([P, 8, P], BF16, name="pt", tag="tc")
-            for s in range(8):
-                nc.tensor.transpose(pt[:, s, :], pbf[:, s // 2, s % 2, :], identb[:])
-            cg = late.tile([P, 1024], BF16, name="cg", tag="cg", align_bytes=64)
-            nc.scalar.copy(
-                out=cg[:].rearrange("p (g n t) -> p g n t", g=2, t=4),
-                in_=pt[:].rearrange("p (g t) n -> p g n t", g=2),
-            )
-            nc.vector.quantize_mx(out=ccc[:, nh, :].bitcast(FP8X4), scales=ccs[:, nh, :], in_=cg[:])
-
-        def output_rows(nh):
-            hb = late.tile([P, DOUT], F32, name="hb", tag="hb")
-            for ch in range(2):
-                cs = slice(ch * 512, (ch + 1) * 512)
-                h = ps_v.tile([P, 512], F32, name="h", tag="v")
-                for g in range(3):
-                    if g < 2:
-                        lt = ccc[:, nh, g * P : (g + 1) * P]
-                        ls = ccs[:, nh, g * P : (g + 1) * P]
-                    else:
-                        lt = rcc[:, nh * P : (nh + 1) * P]
-                        ls = rcs[:, nh * P : (nh + 1) * P]
-                    nc.tensor.matmul_mx(
-                        out=h[:],
-                        lhsT=lt.bitcast(FP8X4),
-                        lhsT_scale=ls,
-                        rhs=woc[:, g, cs].bitcast(FP8X4),
-                        rhs_scale=wos[:, g, cs],
-                        start=(g == 0),
-                        stop=(g == 2),
-                    )
-                nc.vector.tensor_tensor(out=hb[:, cs], in0=h[:], in1=wob[:, cs], op=ALU.add)
-            rl = late.tile([P, DOUT], F32, name="rl", tag="rl")
-            nc.scalar.activation(out=rl[:], in_=hb[:], func=ACT.Relu)
-            st = late.tile([P, 2, 6], F32, name="st", tag="st")
-            for ch in range(2):
-                nc.vector.bn_stats(out=st[:, ch, :], in_=rl[:, ch * 512 : (ch + 1) * 512])
-            mv = late.tile([P, 2], F32, name="mv", tag="mv")
-            nc.vector.bn_aggr(out=mv[:], in_=st[:].rearrange("p a b -> p (a b)"))
-            y1 = late.tile([P, DOUT], F32, name="y1", tag="hb")
-            nc.vector.scalar_tensor_tensor(
-                out=y1[:], in0=rl[:], scalar=mv[:, 0:1], in1=lng[:], op0=ALU.subtract, op1=ALU.mult
-            )
-            ve = late.tile([P, 1], F32, name="ve", tag="ve")
-            nc.vector.tensor_scalar_add(out=ve[:], in0=mv[:, 1:2], scalar1=LN_EPS)
-            sd = late.tile([P, 1], F32, name="sd", tag="sd")
-            nc.scalar.sqrt(out=sd[:], in_=ve[:])
-            rs = late.tile([P, 1], F32, name="rs", tag="rs")
-            nc.vector.reciprocal(out=rs[:], in_=sd[:])
-            yo = late.tile([P, DOUT], F32, name="yo", tag="rl")
-            nc.vector.scalar_tensor_tensor(
-                out=yo[:], in0=y1[:], scalar=rs[:, 0:1], in1=lnb[:], op0=ALU.mult, op1=ALU.add
-            )
-            nc.sync.dma_start(out=out[nh * P : (nh + 1) * P, :], in_=yo[:])
 
         def root_unit():
             rw = rootb[:].bitcast(F32)
@@ -455,34 +541,84 @@ def tile_transformeraggregator_pb_t_kernel(
                 for u in range(2):
                     srcs.append(rw[:, nh, 128 * u : 128 * u + 128])
             rg = late.tile([P, 1024], BF16, name="rg", align_bytes=64)
-            unit4(srcs, words(rg[:]), nc.scalar.copy, P, ps_t, "tc")
-            nc.vector.quantize_mx(out=rcc[:].bitcast(FP8X4), scales=rcs[:], in_=rg[:])
+            unit4(srcs, words(rg[:]), scopy, P, ps_t, "tc")
+            return rg
 
-        transposes(0)
-        quantise(0)
-        transposes(1)
-        quantise(1)
-        wost = {}
-        for g in range(20):
-            multiply(g)
-            if g + 2 < 20:
-                if (g + 2) % 2 == 0 and (g + 2) // 2 + 2 < 10 and (g + 2) // 2 + 2 >= 3:
-                    load_chunk((g + 2) // 2 + 2)
-                transposes(g + 2)
+        pending = []
+        wo_wg = {}
+        for g in range(NG):
+            if g + 3 < NG:
+                tf_dma(g + 3)
+            multiply(g, 0)
+            pool_rows(g, 0)
+            multiply(g, 1)
+            if g == 16:
+                out_pass(0, 2)
+                out_pass(0, 0)
+                out_pass(0, 1)
+            if g == NG - 1:
+                out_pass(1, 2)
+            if g + LQ < NG:
+                quantise(g + LQ)
+            for job in pending:
+                job()
+            pending = []
+            pool_rows(g, 1)
+            if g == 16:
+                ln_bias(0)
+            if g + LT < NG:
+                transposes(g + LT)
+                if g + LT + NBUF < NG:
+                    load_group(g + LT + NBUF)
             if g < 12:
-                wg_, wch, wpair = wo_units[g]
-                weight_unit(wo_raw, wg_, wch, wpair, False, wost, nc.scalar.copy, ps_t, "tc", woc, wos)
-            if g == 12:
-                root_unit()
-            pool_rows(g)
-            if g + 2 < 20:
-                quantise(g + 2)
+                wg_i, wch, wpair = wo_units[g]
+                if wpair == 0:
+                    wo_wg[0] = new_wg()
+                weight_unit(wo_raw, wo_wg[0], wg_i, wch, wpair, False, scopy, ps_t, "tc")
+                if wpair == 1:
+                    pending.append(
+                        lambda t=wo_wg[0], a=wg_i, b=wch: weight_quantise(t, woc, wos, a, b)
+                    )
+            if g in (1, 5, 9):
+                tf_uk((g + 7) // 4, False)
+            if g in (2, 6, 10):
+                tf_frac((g + 6) // 4)
+            if g in (0, 3, 7, 11):
+                tf_sin((g + 5) // 4)
             if g == 10:
-                pooled_round(0)
-            if g == 11:
-                pooled_quantise(0)
+                pooled_round(0, 0)
+                pooled_round(0, 1)
+            if g == 12:
+                pooled_transpose(0, 0, "tc", scopy)
+                pending.append(lambda: pooled_quantise(0, 0))
             if g == 13:
-                output_rows(0)
-        pooled_round(1)
-        pooled_quantise(1)
-        output_rows(1)
+                pooled_transpose(0, 1, "tc", scopy)
+                pending.append(lambda: pooled_quantise(0, 1))
+            if g == 14:
+                rg_t = root_unit()
+                pending.append(
+                    lambda t=rg_t: nc.vector.quantize_mx(out=rcc[:].bitcast(FP8X4), scales=rcs[:], in_=t[:])
+                )
+            if g == 16:
+                ln_relu(0)
+            if g == 17:
+                ln_stats(0)
+                ln_sqrt(0)
+                ln_centre(0)
+            if g == 18:
+                ln_finish(0)
+
+        pooled_round(1, 0)
+        pooled_round(1, 1)
+        pooled_transpose(1, 0, "ta", scopy)
+        pooled_transpose(1, 1, "tb", vcopy)
+        pooled_quantise(1, 0)
+        out_pass(1, 0)
+        pooled_quantise(1, 1)
+        out_pass(1, 1)
+        ln_bias(1)
+        ln_relu(1)
+        ln_stats(1)
+        ln_sqrt(1)
+        ln_centre(1)
+        ln_finish(1)

@@ -289,20 +289,23 @@ def tile_transformeraggregator_pb_t_kernel(
         quant = {}
         banks = {}
 
-        def transposes(g):
+        def transposes_a(g):
             ndw = nds[g % NBUF][:].bitcast(F32)
-            edw = eds[g % NBUF][:].bitcast(F32)
-            srcs_a = []
-            srcs_b = []
+            srcs = []
             for i in range(2):
                 for u in range(2):
                     lo = i * 256 + 128 * u
-                    srcs_a.append(ndw[:, lo : lo + 128])
+                    srcs.append(ndw[:, lo : lo + 128])
+            unit4(srcs, words(get_gg(g)[:, 0:1024]), nc.scalar.copy, P, ps_t, "ta")
+
+        def transposes_b(g):
+            edw = eds[g % NBUF][:].bitcast(F32)
+            srcs = []
+            for i in range(2):
+                for u in range(2):
                     eo = i * 192
-                    srcs_b.append(edw[:, eo : eo + 256].rearrange("p (w u) -> p w u", u=2)[:, :, u])
-            gg = get_gg(g)
-            unit4(srcs_a, words(gg[:, 0:1024]), nc.scalar.copy, P, ps_t, "ta")
-            unit4(srcs_b, words(gg[0:96, 1024:2048]), nc.scalar.copy, 96, ps_t, "tb")
+                    srcs.append(edw[:, eo : eo + 256].rearrange("p (w u) -> p w u", u=2)[:, :, u])
+            unit4(srcs, words(get_gg(g)[0:96, 1024:2048]), nc.scalar.copy, 96, ps_t, "tb")
 
         def quantise(g):
             cq = stg.tile([P, 512], U32, name="cq", tag="cq", align_bytes=64)
@@ -522,7 +525,8 @@ def tile_transformeraggregator_pb_t_kernel(
         nc.sync.dma_start(out=lnb[:], in_=ln_b.partition_broadcast(P))
 
         for g in range(LT):
-            transposes(g)
+            transposes_a(g)
+            transposes_b(g)
             load_group(g + NBUF)
         for g in range(LQ):
             quantise(g)
@@ -551,6 +555,13 @@ def tile_transformeraggregator_pb_t_kernel(
                 tf_dma(g + 3)
             multiply(g, 0)
             pool_rows(g, 0)
+            if g + LT < NG:
+                transposes_a(g + LT)
+            if g < 12:
+                wg_i, wch, wpair = wo_units[g]
+                if wpair == 0:
+                    wo_wg[0] = new_wg()
+                weight_unit(wo_raw, wo_wg[0], wg_i, wch, wpair, False, scopy, ps_t, "tc")
             multiply(g, 1)
             if g == 16:
                 out_pass(0, 2)
@@ -567,14 +578,10 @@ def tile_transformeraggregator_pb_t_kernel(
             if g == 16:
                 ln_bias(0)
             if g + LT < NG:
-                transposes(g + LT)
+                transposes_b(g + LT)
                 if g + LT + NBUF < NG:
                     load_group(g + LT + NBUF)
             if g < 12:
-                wg_i, wch, wpair = wo_units[g]
-                if wpair == 0:
-                    wo_wg[0] = new_wg()
-                weight_unit(wo_raw, wo_wg[0], wg_i, wch, wpair, False, scopy, ps_t, "tc")
                 if wpair == 1:
                     pending.append(
                         lambda t=wo_wg[0], a=wg_i, b=wch: weight_quantise(t, woc, wos, a, b)

@@ -289,23 +289,20 @@ def tile_transformeraggregator_pb_t_kernel(
         quant = {}
         banks = {}
 
-        def transposes_a(g):
+        def transposes(g):
             ndw = nds[g % NBUF][:].bitcast(F32)
-            srcs = []
+            edw = eds[g % NBUF][:].bitcast(F32)
+            srcs_a = []
+            srcs_b = []
             for i in range(2):
                 for u in range(2):
                     lo = i * 256 + 128 * u
-                    srcs.append(ndw[:, lo : lo + 128])
-            unit4(srcs, words(get_gg(g)[:, 0:1024]), nc.scalar.copy, P, ps_t, "ta")
-
-        def transposes_b(g):
-            edw = eds[g % NBUF][:].bitcast(F32)
-            srcs = []
-            for i in range(2):
-                for u in range(2):
+                    srcs_a.append(ndw[:, lo : lo + 128])
                     eo = i * 192
-                    srcs.append(edw[:, eo : eo + 256].rearrange("p (w u) -> p w u", u=2)[:, :, u])
-            unit4(srcs, words(get_gg(g)[0:96, 1024:2048]), nc.scalar.copy, 96, ps_t, "tb")
+                    srcs_b.append(edw[:, eo : eo + 256].rearrange("p (w u) -> p w u", u=2)[:, :, u])
+            gg = get_gg(g)
+            unit4(srcs_a, words(gg[:, 0:1024]), nc.scalar.copy, P, ps_t, "ta")
+            unit4(srcs_b, words(gg[0:96, 1024:2048]), nc.scalar.copy, 96, ps_t, "tb")
 
         def quantise(g):
             cq = stg.tile([P, 512], U32, name="cq", tag="cq", align_bytes=64)
@@ -335,7 +332,7 @@ def tile_transformeraggregator_pb_t_kernel(
             banks[(g, i)] = pair
 
         def offloaded(g, i, ch):
-            return i == 1 and ch == 1 and g % 10 < 8
+            return False
 
         def pool_rows(g, i):
             nh = g // 10
@@ -364,12 +361,7 @@ def tile_transformeraggregator_pb_t_kernel(
             if h == 0:
                 nc.scalar.copy(out=pbf[:], in_=src)
             else:
-                nc.vector.tensor_tensor(
-                    out=pbf[:],
-                    in0=src,
-                    in1=acc2[nh][:].rearrange("p (q i e) -> p q e i", q=2, e=2),
-                    op=ALU.add,
-                )
+                nc.vector.tensor_copy(out=pbf[:], in_=src)
             ph[(nh, h)] = pbf
 
         def pooled_transpose(nh, h, tag, evac):
@@ -525,8 +517,7 @@ def tile_transformeraggregator_pb_t_kernel(
         nc.sync.dma_start(out=lnb[:], in_=ln_b.partition_broadcast(P))
 
         for g in range(LT):
-            transposes_a(g)
-            transposes_b(g)
+            transposes(g)
             load_group(g + NBUF)
         for g in range(LQ):
             quantise(g)
@@ -555,13 +546,6 @@ def tile_transformeraggregator_pb_t_kernel(
                 tf_dma(g + 3)
             multiply(g, 0)
             pool_rows(g, 0)
-            if g + LT < NG:
-                transposes_a(g + LT)
-            if g < 12:
-                wg_i, wch, wpair = wo_units[g]
-                if wpair == 0:
-                    wo_wg[0] = new_wg()
-                weight_unit(wo_raw, wo_wg[0], wg_i, wch, wpair, False, scopy, ps_t, "tc")
             multiply(g, 1)
             if g == 16:
                 out_pass(0, 2)
@@ -578,10 +562,14 @@ def tile_transformeraggregator_pb_t_kernel(
             if g == 16:
                 ln_bias(0)
             if g + LT < NG:
-                transposes_b(g + LT)
+                transposes(g + LT)
                 if g + LT + NBUF < NG:
                     load_group(g + LT + NBUF)
             if g < 12:
+                wg_i, wch, wpair = wo_units[g]
+                if wpair == 0:
+                    wo_wg[0] = new_wg()
+                weight_unit(wo_raw, wo_wg[0], wg_i, wch, wpair, False, scopy, ps_t, "tc")
                 if wpair == 1:
                     pending.append(
                         lambda t=wo_wg[0], a=wg_i, b=wch: weight_quantise(t, woc, wos, a, b)

@@ -124,12 +124,9 @@ def tile_transformeraggregator_pb_t_kernel(
         ccc = const.tile([P, 2, 256], U32, name="ccc", align_bytes=64)
         ccs = const.tile([P, 2, 256], U8, name="ccs", align_bytes=64)
         acc = []
-        acc2 = []
         for nh in range(2):
             acc_t = const.tile([P, DOUT], F32, name="acc%d" % nh)
             acc.append(acc_t)
-            acc2_t = const.tile([P, 512], F32, name="accb%d" % nh)
-            acc2.append(acc2_t)
 
         def words(ap):
             return ap.bitcast(F32).rearrange("p (i r u) -> p i r u", i=2, u=2)
@@ -215,7 +212,7 @@ def tile_transformeraggregator_pb_t_kernel(
             kt = tfp.tile([P, 4, 256], I32, name="kt", tag="kt")
             tf_t[m] = [ut, kt]
             for t in range(4):
-                if split and t < 2:
+                if t < 2 or not split:
                     nc.scalar.activation(
                         out=ut[:, t, :],
                         in_=dts[:, 256 * m : 256 * (m + 1)],
@@ -223,13 +220,14 @@ def tile_transformeraggregator_pb_t_kernel(
                         scale=pa[:, t : t + 1],
                         bias=pb[:, t : t + 1],
                     )
-                    tf_affine(nc.gpsimd, kt, m, t)
-                elif split:
-                    tf_affine(nc.vector, ut, m, t)
-                    tf_affine(nc.vector, kt, m, t)
                 else:
-                    tf_affine(nc.gpsimd, ut, m, t)
-                    tf_affine(nc.gpsimd, kt, m, t)
+                    tf_affine(nc.vector, ut, m, t)
+
+        def tf_int(m):
+            ut, kt = tf_t[m]
+            nc.vector.tensor_copy(
+                out=kt[:].rearrange("p t w -> p (t w)"), in_=ut[:].rearrange("p t w -> p (t w)")
+            )
 
         def tf_frac(m):
             ut, kt = tf_t[m]
@@ -331,37 +329,36 @@ def tile_transformeraggregator_pb_t_kernel(
                     )
             banks[(g, i)] = pair
 
-        def offloaded(g, i, ch):
-            return False
-
         def pool_rows(g, i):
             nh = g // 10
             j = 2 * (g % 10) + i
             pair = banks[(g, i)]
             for ch in range(2):
-                w = attf[:, nh, j, ch : ch + 1]
-                if offloaded(g, i, ch):
-                    if g % 10 == 0:
-                        nc.scalar.activation(out=acc2[nh][:], in_=pair[ch][:], func=ACT.Copy, scale=w)
-                    else:
-                        tmp = stg.tile([P, 512], F32, name="tmp", tag="tmp")
-                        nc.scalar.activation(out=tmp[:], in_=pair[ch][:], func=ACT.Copy, scale=w)
-                        nc.gpsimd.tensor_tensor(out=acc2[nh][:], in0=acc2[nh][:], in1=tmp[:], op=ALU.add)
-                else:
-                    a = acc[nh][:, ch * 512 : (ch + 1) * 512]
-                    nc.vector.scalar_tensor_tensor(
-                        out=a, in0=pair[ch][:], scalar=w, in1=a, op0=ALU.mult, op1=ALU.add
-                    )
+                a = acc[nh][:, ch * 512 : (ch + 1) * 512]
+                nc.vector.scalar_tensor_tensor(
+                    out=a,
+                    in0=pair[ch][:],
+                    scalar=attf[:, nh, j, ch : ch + 1],
+                    in1=a,
+                    op0=ALU.mult,
+                    op1=ALU.add,
+                )
+
+        def pool_bias(nh):
+            for ch in range(2):
+                nc.scalar.activation(
+                    out=acc[nh][:, ch * 512 : (ch + 1) * 512],
+                    in_=wvb[:, ch * 512 : (ch + 1) * 512],
+                    func=ACT.Copy,
+                    scale=satt[:, nh, ch : ch + 1],
+                )
 
         ph = {}
 
-        def pooled_round(nh, h):
+        def pooled_round(nh, h, cast):
             pbf = late.tile([P, 2, 2, P], BF16, name="pbf", tag="pbf%d" % h)
             src = acc[nh][:, h * 512 : (h + 1) * 512].rearrange("p (q i e) -> p q e i", q=2, e=2)
-            if h == 0:
-                nc.scalar.copy(out=pbf[:], in_=src)
-            else:
-                nc.vector.tensor_copy(out=pbf[:], in_=src)
+            cast(out=pbf[:], in_=src)
             ph[(nh, h)] = pbf
 
         def pooled_transpose(nh, h, tag, evac):
@@ -477,23 +474,14 @@ def tile_transformeraggregator_pb_t_kernel(
         dt_bank(2)
         weight_unit(wv_raw, wg_a, 0, 0, 1, False, vcopy, ps_t, "tc")
         weight_unit(wv_raw, wg_b, 1, 0, 1, True, scopy, ps_v, "v")
+        tf_int(0)
         weight_quantise(wg_a, wvc, wvs, 0, 0)
         tf_frac(0)
         weight_quantise(wg_b, wvc, wvs, 1, 0)
         tf_sin(0)
         for g in range(3):
             tf_dma(g)
-        tf_uk(1, False)
-        for nh in range(2):
-            for ch in range(2):
-                nc.gpsimd.tensor_scalar(
-                    out=acc[nh][:, ch * 512 : (ch + 1) * 512],
-                    in0=wvb[:, ch * 512 : (ch + 1) * 512],
-                    scalar1=satt[:, nh, ch : ch + 1],
-                    scalar2=0.0,
-                    op0=ALU.mult,
-                    op1=ALU.add,
-                )
+        pool_bias(0)
         wg_c = new_wg()
         weight_unit(wv_raw, wg_c, 0, 1, 0, False, vcopy, ps_t, "ta")
         wg_d = new_wg()
@@ -519,9 +507,9 @@ def tile_transformeraggregator_pb_t_kernel(
         for g in range(LT):
             transposes(g)
             load_group(g + NBUF)
+        tf_uk(1, False)
         for g in range(LQ):
             quantise(g)
-        tf_frac(1)
 
         wo_units = []
         for g in range(3):
@@ -576,13 +564,19 @@ def tile_transformeraggregator_pb_t_kernel(
                     )
             if g in (1, 5, 9):
                 tf_uk((g + 7) // 4, False)
+            if g == 0:
+                tf_int(1)
+                tf_frac(1)
+            if g == 4:
+                pool_bias(1)
             if g in (2, 6, 10):
+                tf_int((g + 6) // 4)
                 tf_frac((g + 6) // 4)
             if g in (0, 3, 7, 11):
                 tf_sin((g + 5) // 4)
             if g == 10:
-                pooled_round(0, 0)
-                pooled_round(0, 1)
+                pooled_round(0, 0, scopy)
+                pooled_round(0, 1, scopy)
             if g == 12:
                 pooled_transpose(0, 0, "tc", scopy)
                 pending.append(lambda: pooled_quantise(0, 0))
@@ -603,8 +597,8 @@ def tile_transformeraggregator_pb_t_kernel(
             if g == 18:
                 ln_finish(0)
 
-        pooled_round(1, 0)
-        pooled_round(1, 1)
+        pooled_round(1, 0, scopy)
+        pooled_round(1, 1, vcopy)
         pooled_transpose(1, 0, "ta", scopy)
         pooled_transpose(1, 1, "tb", vcopy)
         pooled_quantise(1, 0)

@@ -55,7 +55,8 @@ def tile_transformeraggregator_pb_t_kernel(
         tfp = es.enter_context(tc.tile_pool(name="tfp", bufs=1))
         late = es.enter_context(tc.tile_pool(name="late", bufs=1))
         ps_t = es.enter_context(tc.psum_pool(name="ps_t", bufs=1))
-        ps_v = es.enter_context(tc.psum_pool(name="ps_v", bufs=5))
+        ps_v = es.enter_context(tc.psum_pool(name="ps_v", bufs=4))
+        ps_p = es.enter_context(tc.psum_pool(name="ps_p", bufs=1))
         es.enter_context(tc.manual_schedule())
 
         identf = const.tile([P, P], F32, name="identf")
@@ -212,7 +213,7 @@ def tile_transformeraggregator_pb_t_kernel(
             kt = tfp.tile([P, 4, 256], I32, name="kt", tag="kt")
             tf_t[m] = [ut, kt]
             for t in range(4):
-                if t < 2 or not split:
+                if split and t < 2:
                     nc.scalar.activation(
                         out=ut[:, t, :],
                         in_=dts[:, 256 * m : 256 * (m + 1)],
@@ -220,14 +221,13 @@ def tile_transformeraggregator_pb_t_kernel(
                         scale=pa[:, t : t + 1],
                         bias=pb[:, t : t + 1],
                     )
-                else:
+                    tf_affine(nc.gpsimd, kt, m, t)
+                elif split:
                     tf_affine(nc.vector, ut, m, t)
-
-        def tf_int(m):
-            ut, kt = tf_t[m]
-            nc.vector.tensor_copy(
-                out=kt[:].rearrange("p t w -> p (t w)"), in_=ut[:].rearrange("p t w -> p (t w)")
-            )
+                    tf_affine(nc.vector, kt, m, t)
+                else:
+                    tf_affine(nc.gpsimd, ut, m, t)
+                    tf_affine(nc.gpsimd, kt, m, t)
 
         def tf_frac(m):
             ut, kt = tf_t[m]
@@ -329,43 +329,70 @@ def tile_transformeraggregator_pb_t_kernel(
                     )
             banks[(g, i)] = pair
 
+        def offloaded(g, i, ch):
+            return i == 1 and ch == 1
+
+        tmps = {}
+
         def pool_rows(g, i):
             nh = g // 10
             j = 2 * (g % 10) + i
             pair = banks[(g, i)]
             for ch in range(2):
-                a = acc[nh][:, ch * 512 : (ch + 1) * 512]
-                nc.vector.scalar_tensor_tensor(
-                    out=a,
-                    in0=pair[ch][:],
-                    scalar=attf[:, nh, j, ch : ch + 1],
-                    in1=a,
-                    op0=ALU.mult,
-                    op1=ALU.add,
-                )
-
-        def pool_bias(nh):
-            for ch in range(2):
-                nc.scalar.activation(
-                    out=acc[nh][:, ch * 512 : (ch + 1) * 512],
-                    in_=wvb[:, ch * 512 : (ch + 1) * 512],
-                    func=ACT.Copy,
-                    scale=satt[:, nh, ch : ch + 1],
-                )
+                w = attf[:, nh, j, ch : ch + 1]
+                if offloaded(g, i, ch):
+                    tmp = stg.tile([P, 512], F32, name="tmp", tag="tmp")
+                    nc.scalar.activation(
+                        out=tmp[:].rearrange("p (u e i) -> p u e i", u=2, e=2),
+                        in_=pair[ch][:].rearrange("p (u i e) -> p u e i", u=2, e=2),
+                        func=ACT.Copy,
+                        scale=w,
+                    )
+                    tmps[g] = tmp
+                else:
+                    a = acc[nh][:, ch * 512 : (ch + 1) * 512]
+                    nc.vector.scalar_tensor_tensor(
+                        out=a, in0=pair[ch][:], scalar=w, in1=a, op0=ALU.mult, op1=ALU.add
+                    )
 
         ph = {}
+        ptb = {}
 
-        def pooled_round(nh, h, cast):
-            pbf = late.tile([P, 2, 2, P], BF16, name="pbf", tag="pbf%d" % h)
-            src = acc[nh][:, h * 512 : (h + 1) * 512].rearrange("p (q i e) -> p q e i", q=2, e=2)
-            cast(out=pbf[:], in_=src)
-            ph[(nh, h)] = pbf
+        def pt_add(nh, blocks, first, last):
+            if first:
+                pt_t = ps_p.tile([P, 4, P], F32, name="ptb", tag="ptb")
+                ptb[nh] = pt_t
+            for t in range(4):
+                nc.tensor.matmul(
+                    out=ptb[nh][:, t, :],
+                    lhsT=blocks[t],
+                    rhs=identf[:],
+                    start=(first and t == 0),
+                    stop=(last and t == 3),
+                    is_transpose=True,
+                )
 
-        def pooled_transpose(nh, h, tag, evac):
-            pbf = ph[(nh, h)]
-            pt = ps_t.tile([P, 4, P], BF16, name="pt", tag=tag)
-            for s in range(4):
-                nc.tensor.transpose(pt[:, s, :], pbf[:, s // 2, s % 2, :], identb[:])
+        def acc_blocks(nh, h):
+            v = acc[nh][:, h * 512 : (h + 1) * 512].rearrange("p (u i e) -> p u e i", u=2, e=2)
+            blocks = []
+            for t in range(4):
+                blocks.append(v[:, t // 2, t % 2, :])
+            return blocks
+
+        def tmp_blocks(g):
+            blocks = []
+            for t in range(4):
+                blocks.append(tmps[g][:, t * P : (t + 1) * P])
+            return blocks
+
+        def pooled_out(nh, h, tag, evac):
+            if h == 1:
+                pt = ptb[nh]
+            else:
+                pt = ps_t.tile([P, 4, P], F32, name="pt", tag=tag)
+                blocks = acc_blocks(nh, 0)
+                for t in range(4):
+                    nc.tensor.transpose(pt[:, t, :], blocks[t], identf[:])
             cg = late.tile([P, 512], BF16, name="cg", tag="cg%d" % h, align_bytes=64)
             evac(out=cg[:].rearrange("p (n t) -> p n t", t=4), in_=pt[:].rearrange("p t n -> p n t"))
             ph[(nh, h)] = cg
@@ -378,7 +405,7 @@ def tile_transformeraggregator_pb_t_kernel(
 
         hbank = {}
 
-        def out_pass(nh, g):
+        def out_pass(nh, g, last):
             if g == 2:
                 pair = []
                 for o in range(2):
@@ -399,7 +426,7 @@ def tile_transformeraggregator_pb_t_kernel(
                     rhs=woc[:, g, cs].bitcast(FP8X4),
                     rhs_scale=wos[:, g, cs],
                     start=(g == 2),
-                    stop=(g == 1),
+                    stop=last,
                 )
 
         ln = {}
@@ -474,14 +501,23 @@ def tile_transformeraggregator_pb_t_kernel(
         dt_bank(2)
         weight_unit(wv_raw, wg_a, 0, 0, 1, False, vcopy, ps_t, "tc")
         weight_unit(wv_raw, wg_b, 1, 0, 1, True, scopy, ps_v, "v")
-        tf_int(0)
         weight_quantise(wg_a, wvc, wvs, 0, 0)
         tf_frac(0)
         weight_quantise(wg_b, wvc, wvs, 1, 0)
         tf_sin(0)
         for g in range(3):
             tf_dma(g)
-        pool_bias(0)
+        tf_uk(1, False)
+        for nh in range(2):
+            for ch in range(2):
+                nc.gpsimd.tensor_scalar(
+                    out=acc[nh][:, ch * 512 : (ch + 1) * 512],
+                    in0=wvb[:, ch * 512 : (ch + 1) * 512],
+                    scalar1=satt[:, nh, ch : ch + 1],
+                    scalar2=0.0,
+                    op0=ALU.mult,
+                    op1=ALU.add,
+                )
         wg_c = new_wg()
         weight_unit(wv_raw, wg_c, 0, 1, 0, False, vcopy, ps_t, "ta")
         wg_d = new_wg()
@@ -507,9 +543,9 @@ def tile_transformeraggregator_pb_t_kernel(
         for g in range(LT):
             transposes(g)
             load_group(g + NBUF)
-        tf_uk(1, False)
         for g in range(LQ):
             quantise(g)
+        tf_frac(1)
 
         wo_units = []
         for g in range(3):
@@ -536,11 +572,15 @@ def tile_transformeraggregator_pb_t_kernel(
             pool_rows(g, 0)
             multiply(g, 1)
             if g == 16:
-                out_pass(0, 2)
-                out_pass(0, 0)
-                out_pass(0, 1)
+                out_pass(0, 2, False)
+                out_pass(0, 0, False)
+                out_pass(0, 1, True)
             if g == NG - 1:
-                out_pass(1, 2)
+                out_pass(1, 2, False)
+            if g == 10:
+                pt_add(0, acc_blocks(0, 1), False, True)
+                pooled_out(0, 1, "", scopy)
+                pending.append(lambda: pooled_quantise(0, 1))
             if g + LQ < NG:
                 quantise(g + LQ)
             for job in pending:
@@ -562,27 +602,18 @@ def tile_transformeraggregator_pb_t_kernel(
                     pending.append(
                         lambda t=wo_wg[0], a=wg_i, b=wch: weight_quantise(t, woc, wos, a, b)
                     )
+            if g == NG - 1:
+                pt_add(1, acc_blocks(1, 1), False, False)
+            pt_add(g // 10, tmp_blocks(g), g % 10 == 0, g == NG - 1)
             if g in (1, 5, 9):
                 tf_uk((g + 7) // 4, False)
-            if g == 0:
-                tf_int(1)
-                tf_frac(1)
-            if g == 4:
-                pool_bias(1)
             if g in (2, 6, 10):
-                tf_int((g + 6) // 4)
                 tf_frac((g + 6) // 4)
             if g in (0, 3, 7, 11):
                 tf_sin((g + 5) // 4)
-            if g == 10:
-                pooled_round(0, 0, scopy)
-                pooled_round(0, 1, scopy)
             if g == 12:
-                pooled_transpose(0, 0, "tc", scopy)
+                pooled_out(0, 0, "tc", scopy)
                 pending.append(lambda: pooled_quantise(0, 0))
-            if g == 13:
-                pooled_transpose(0, 1, "tc", scopy)
-                pending.append(lambda: pooled_quantise(0, 1))
             if g == 14:
                 rg_t = root_unit()
                 pending.append(
@@ -597,14 +628,12 @@ def tile_transformeraggregator_pb_t_kernel(
             if g == 18:
                 ln_finish(0)
 
-        pooled_round(1, 0, scopy)
-        pooled_round(1, 1, vcopy)
-        pooled_transpose(1, 0, "ta", scopy)
-        pooled_transpose(1, 1, "tb", vcopy)
-        pooled_quantise(1, 0)
-        out_pass(1, 0)
+        pooled_out(1, 1, "", vcopy)
+        pooled_out(1, 0, "ta", scopy)
         pooled_quantise(1, 1)
-        out_pass(1, 1)
+        out_pass(1, 1, False)
+        pooled_quantise(1, 0)
+        out_pass(1, 0, True)
         ln_bias(1)
         ln_relu(1)
         ln_stats(1)

@@ -24,8 +24,6 @@ LN_EPS = 1e-5
 FLOPS = 2 * 256 * NNEI * 1024 * DOUT + 2 * 256 * CO * DOUT
 NG = 20
 NBUF = 5
-LT = 4
-LQ = 2
 
 
 def tile_transformeraggregator_pb_t_kernel(
@@ -55,8 +53,7 @@ def tile_transformeraggregator_pb_t_kernel(
         tfp = es.enter_context(tc.tile_pool(name="tfp", bufs=1))
         late = es.enter_context(tc.tile_pool(name="late", bufs=1))
         ps_t = es.enter_context(tc.psum_pool(name="ps_t", bufs=1))
-        ps_v = es.enter_context(tc.psum_pool(name="ps_v", bufs=4))
-        ps_p = es.enter_context(tc.psum_pool(name="ps_p", bufs=1))
+        ps_v = es.enter_context(tc.psum_pool(name="ps_v", bufs=5))
         es.enter_context(tc.manual_schedule())
 
         identf = const.tile([P, P], F32, name="identf")
@@ -69,14 +66,20 @@ def tile_transformeraggregator_pb_t_kernel(
         nc.scalar.activation(out=zout[:], in_=zin[:], func=ACT.Sin)
         xw = const.tile([P, 32], BF16, name="xw")
         nc.vector.memset(xw[:], 0.0)
+        brow = const.tile([P, DOUT], BF16, name="brow")
+        nc.vector.memset(brow[:], 0.0)
         nds = []
         eds = []
         for b in range(NBUF):
             nd_t = const.tile([P, 2 * DN], BF16, name="nd%d" % b)
             nds.append(nd_t)
-            ed_t = const.tile([P, 2 * DE + 128], BF16, name="ed%d" % b)
-            nc.vector.memset(ed_t[:, 2 * DE : 2 * DE + 128], 0.0)
+            ed_t = const.tile([P, 2 * DE], BF16, name="ed%d" % b)
             eds.append(ed_t)
+        ess = []
+        for b in range(3):
+            es_t = const.tile([P, 2, 2, P], F32, name="es%d" % b)
+            nc.vector.memset(es_t[:, :, :, 96:128], 0.0)
+            ess.append(es_t)
 
         nt = const.tile([P, 2, NNEI], BF16, name="nt")
         rt = const.tile([P, 2, 1], BF16, name="rt")
@@ -87,6 +90,7 @@ def tile_transformeraggregator_pb_t_kernel(
             nc.sync.dma_start(out=xw[0:32, 0:4], in_=time_w.rearrange("(p t) o -> p (t o)", t=4))
             nc.sync.dma_start(out=xw[0:32, 16:20], in_=time_b.rearrange("(p t) -> p t", t=4))
             nc.sync.dma_start(out=attb[:], in_=att.rearrange("(h p) j c -> p h (j c)", p=P))
+        nc.sync.dma_start(out=brow[0:1, :], in_=wv_b.rearrange("(o c) -> o c", o=1))
 
         wv_raw = []
         wo_raw = []
@@ -104,15 +108,13 @@ def tile_transformeraggregator_pb_t_kernel(
                 in_=neighbor_node_feature[rows, j0 : j0 + 2, :].rearrange("p j k -> p (j k)"),
             )
             nc.sync.dma_start(
-                out=eds[g % NBUF][:, 0 : 2 * DE],
+                out=eds[g % NBUF][:],
                 in_=neighbor_edge_feature[rows, j0 : j0 + 2, :].rearrange("p j k -> p (j k)"),
             )
 
         for ct in range(8):
             load_w(wv_raw, wv_w, ct, 1024)
         load_group(0)
-        wvb = const.tile([P, DOUT], BF16, name="wvb")
-        nc.sync.dma_start(out=wvb[:], in_=wv_b.partition_broadcast(P))
         for g in range(1, NBUF):
             load_group(g)
 
@@ -149,14 +151,15 @@ def tile_transformeraggregator_pb_t_kernel(
         nt40 = nt[:].rearrange("p h j -> p (h j)").rearrange("p (m a i) -> p m i a", m=5, a=4)
         for i in range(2):
             nc.vector.tensor_copy(
-                out=lnt[:, :, i, :].rearrange("p m (a q) -> p m a q", a=4),
-                in_=nt40[:, :, i, :].unsqueeze(3).to_broadcast([P, 5, 4, 32]),
+                out=lnt[:, :, i, 0:96].rearrange("p m (a q) -> p m a q", a=3),
+                in_=nt40[:, :, i, 1:4].unsqueeze(3).to_broadcast([P, 5, 3, 32]),
             )
+            nc.vector.tensor_copy(out=lnt[:, :, i, 96:128], in_=nt40[:, :, i, 0:1].to_broadcast([P, 5, 32]))
         lrt = const.tile([P, 3, P], BF16, name="lrt")
         nc.vector.tensor_copy(out=lrt[:, 0, :], in_=rt[:, 0, :].to_broadcast([P, P]))
-        nc.vector.tensor_copy(
-            out=lrt[:, 1, :].rearrange("p (h q) -> p h q", h=2), in_=rt[:].to_broadcast([P, 2, 64])
-        )
+        nc.vector.tensor_copy(out=lrt[:, 1, 0:32], in_=rt[:, 0, :].to_broadcast([P, 32]))
+        nc.vector.tensor_copy(out=lrt[:, 1, 32:96], in_=rt[:, 1, :].to_broadcast([P, 64]))
+        nc.vector.tensor_copy(out=lrt[:, 1, 96:128], in_=rt[:, 0, :].to_broadcast([P, 32]))
         nc.vector.tensor_copy(out=lrt[:, 2, :], in_=rt[:, 1, :].to_broadcast([P, P]))
         lrt_of_m = (0, 0, 1, 2, 2)
 
@@ -174,6 +177,18 @@ def tile_transformeraggregator_pb_t_kernel(
         nc.vector.tensor_reduce(
             out=satt[:], in_=attf[:].rearrange("p h j c -> p h c j"), axis=AX.X, op=ALU.add
         )
+
+        wvb = const.tile([P, DOUT], BF16, name="wvb")
+        for ch in range(2):
+            bp = ps_v.tile([P, 512], F32, name="bp", tag="v")
+            nc.tensor.matmul(
+                out=bp[:],
+                lhsT=identb[:, 0:1].to_broadcast([P, P]),
+                rhs=brow[:, ch * 512 : (ch + 1) * 512],
+                start=True,
+                stop=True,
+            )
+            nc.vector.tensor_copy(out=wvb[:, ch * 512 : (ch + 1) * 512], in_=bp[:])
 
         dts = const.tile([P, 1280], F32, name="dts")
         dt_banks = {}
@@ -243,9 +258,14 @@ def tile_transformeraggregator_pb_t_kernel(
         def tf_sin(m):
             gt = tf_t[m][0]
             tfg = tfp.tile([P, 1024], BF16, name="tfg", tag="tfg", bufs=2)
-            nc.scalar.activation(
-                out=tfg[:], in_=gt[:].rearrange("p w t -> p (w t)"), func=ACT.Sin, scale=2.0 * math.pi
-            )
+            gtf = gt[:].rearrange("p w t -> p (w t)")
+            if m == 0:
+                nc.scalar.activation(
+                    out=get_gg(0)[96:128, 1024:2048], in_=gtf[96:128, :], func=ACT.Sin, scale=2.0 * math.pi
+                )
+                nc.scalar.activation(out=tfg[0:96, :], in_=gtf[0:96, :], func=ACT.Sin, scale=2.0 * math.pi)
+            else:
+                nc.scalar.activation(out=tfg[:], in_=gtf, func=ACT.Sin, scale=2.0 * math.pi)
             tf_t[m] = [tfg]
 
         ggs = {}
@@ -257,7 +277,7 @@ def tile_transformeraggregator_pb_t_kernel(
             return ggs[g]
 
         def tf_dma(g):
-            a = g % 4
+            a = (g + 3) % 4
             nc.scalar.dma_start(out=get_gg(g)[96:128, 1024:2048], in_=tf_t[g // 4][0][32 * a : 32 * a + 32, :])
 
         def new_wg():
@@ -289,18 +309,22 @@ def tile_transformeraggregator_pb_t_kernel(
 
         def transposes(g):
             ndw = nds[g % NBUF][:].bitcast(F32)
-            edw = eds[g % NBUF][:].bitcast(F32)
             srcs_a = []
             srcs_b = []
             for i in range(2):
                 for u in range(2):
                     lo = i * 256 + 128 * u
                     srcs_a.append(ndw[:, lo : lo + 128])
-                    eo = i * 192
-                    srcs_b.append(edw[:, eo : eo + 256].rearrange("p (w u) -> p w u", u=2)[:, :, u])
+                    srcs_b.append(ess[g % 3][:, i, u, :])
             gg = get_gg(g)
             unit4(srcs_a, words(gg[:, 0:1024]), nc.scalar.copy, P, ps_t, "ta")
             unit4(srcs_b, words(gg[0:96, 1024:2048]), nc.scalar.copy, 96, ps_t, "tb")
+
+        def sort_edges(g):
+            nc.scalar.copy(
+                out=ess[g % 3][:, :, :, 0:96],
+                in_=eds[g % NBUF][:].bitcast(F32).rearrange("p (i w u) -> p i u w", i=2, u=2),
+            )
 
         def quantise(g):
             cq = stg.tile([P, 512], U32, name="cq", tag="cq", align_bytes=64)
@@ -329,70 +353,35 @@ def tile_transformeraggregator_pb_t_kernel(
                     )
             banks[(g, i)] = pair
 
-        def offloaded(g, i, ch):
-            return i == 1 and ch == 1
-
-        tmps = {}
-
         def pool_rows(g, i):
             nh = g // 10
             j = 2 * (g % 10) + i
             pair = banks[(g, i)]
             for ch in range(2):
-                w = attf[:, nh, j, ch : ch + 1]
-                if offloaded(g, i, ch):
-                    tmp = stg.tile([P, 512], F32, name="tmp", tag="tmp")
-                    nc.scalar.activation(
-                        out=tmp[:].rearrange("p (u e i) -> p u e i", u=2, e=2),
-                        in_=pair[ch][:].rearrange("p (u i e) -> p u e i", u=2, e=2),
-                        func=ACT.Copy,
-                        scale=w,
-                    )
-                    tmps[g] = tmp
-                else:
-                    a = acc[nh][:, ch * 512 : (ch + 1) * 512]
-                    nc.vector.scalar_tensor_tensor(
-                        out=a, in0=pair[ch][:], scalar=w, in1=a, op0=ALU.mult, op1=ALU.add
-                    )
-
-        ph = {}
-        ptb = {}
-
-        def pt_add(nh, blocks, first, last):
-            if first:
-                pt_t = ps_p.tile([P, 4, P], F32, name="ptb", tag="ptb")
-                ptb[nh] = pt_t
-            for t in range(4):
-                nc.tensor.matmul(
-                    out=ptb[nh][:, t, :],
-                    lhsT=blocks[t],
-                    rhs=identf[:],
-                    start=(first and t == 0),
-                    stop=(last and t == 3),
-                    is_transpose=True,
+                a = acc[nh][:, ch * 512 : (ch + 1) * 512]
+                nc.vector.scalar_tensor_tensor(
+                    out=a,
+                    in0=pair[ch][:],
+                    scalar=attf[:, nh, j, ch : ch + 1],
+                    in1=a,
+                    op0=ALU.mult,
+                    op1=ALU.add,
                 )
 
-        def acc_blocks(nh, h):
-            v = acc[nh][:, h * 512 : (h + 1) * 512].rearrange("p (u i e) -> p u e i", u=2, e=2)
-            blocks = []
-            for t in range(4):
-                blocks.append(v[:, t // 2, t % 2, :])
-            return blocks
 
-        def tmp_blocks(g):
-            blocks = []
-            for t in range(4):
-                blocks.append(tmps[g][:, t * P : (t + 1) * P])
-            return blocks
+        ph = {}
 
-        def pooled_out(nh, h, tag, evac):
-            if h == 1:
-                pt = ptb[nh]
-            else:
-                pt = ps_t.tile([P, 4, P], F32, name="pt", tag=tag)
-                blocks = acc_blocks(nh, 0)
-                for t in range(4):
-                    nc.tensor.transpose(pt[:, t, :], blocks[t], identf[:])
+        def pooled_round(nh, h, cast):
+            pbf = late.tile([P, 2, 2, P], BF16, name="pbf", tag="pbf%d" % h)
+            src = acc[nh][:, h * 512 : (h + 1) * 512].rearrange("p (q i e) -> p q e i", q=2, e=2)
+            cast(out=pbf[:], in_=src)
+            ph[(nh, h)] = pbf
+
+        def pooled_transpose(nh, h, pool, tag, evac):
+            pbf = ph[(nh, h)]
+            pt = pool.tile([P, 4, P], BF16, name="pt", tag=tag)
+            for s in range(4):
+                nc.tensor.transpose(pt[:, s, :], pbf[:, s // 2, s % 2, :], identb[:])
             cg = late.tile([P, 512], BF16, name="cg", tag="cg%d" % h, align_bytes=64)
             evac(out=cg[:].rearrange("p (n t) -> p n t", t=4), in_=pt[:].rearrange("p t n -> p n t"))
             ph[(nh, h)] = cg
@@ -405,11 +394,11 @@ def tile_transformeraggregator_pb_t_kernel(
 
         hbank = {}
 
-        def out_pass(nh, g, last):
+        def out_pass(nh, g, pool, tags):
             if g == 2:
                 pair = []
                 for o in range(2):
-                    h_t = ps_v.tile([P, 512], F32, name="h", tag="v")
+                    h_t = pool.tile([P, 512], F32, name="h", tag=tags[o])
                     pair.append(h_t)
                 hbank[nh] = pair
                 lt = rcc[:, nh * P : (nh + 1) * P]
@@ -426,61 +415,89 @@ def tile_transformeraggregator_pb_t_kernel(
                     rhs=woc[:, g, cs].bitcast(FP8X4),
                     rhs_scale=wos[:, g, cs],
                     start=(g == 2),
-                    stop=last,
+                    stop=(g == 1),
                 )
 
-        ln = {}
+        lns = ({}, {})
         halves = (slice(0, 512), slice(512, 1024))
 
         def ln_bias(nh):
-            hb = late.tile([P, DOUT], F32, name="hb", tag="hb")
+            hb = late.tile([P, DOUT], F32, name="hb", tag="hb%d" % nh)
             for o in range(2):
                 nc.vector.tensor_tensor(out=hb[:, halves[o]], in0=hbank[nh][o][:], in1=wob[:, halves[o]], op=ALU.add)
-            ln["hb"] = hb
+            lns[nh]["hb"] = hb
 
         def ln_relu(nh):
-            rl = late.tile([P, DOUT], F32, name="rl", tag="rl")
+            rl = late.tile([P, DOUT], F32, name="rl", tag="rl%d" % nh)
             for o in range(2):
-                nc.scalar.activation(out=rl[:, halves[o]], in_=ln["hb"][:, halves[o]], func=ACT.Relu)
-            ln["rl"] = rl
+                nc.scalar.activation(out=rl[:, halves[o]], in_=lns[nh]["hb"][:, halves[o]], func=ACT.Relu)
+            lns[nh]["rl"] = rl
 
         def ln_stats(nh):
-            st = late.tile([P, 2, 6], F32, name="st", tag="st")
+            st = late.tile([P, 2, 6], F32, name="st", tag="st%d" % nh)
             for o in range(2):
-                nc.vector.bn_stats(out=st[:, o, :], in_=ln["rl"][:, halves[o]])
-            mv = late.tile([P, 2], F32, name="mv", tag="mv")
+                nc.vector.bn_stats(out=st[:, o, :], in_=lns[nh]["rl"][:, halves[o]])
+            mv = late.tile([P, 2], F32, name="mv", tag="mv%d" % nh)
             nc.vector.bn_aggr(out=mv[:], in_=st[:].rearrange("p a b -> p (a b)"))
-            ve = late.tile([P, 1], F32, name="ve", tag="ve")
+            ve = late.tile([P, 1], F32, name="ve", tag="ve%d" % nh)
             nc.vector.tensor_scalar_add(out=ve[:], in0=mv[:, 1:2], scalar1=LN_EPS)
-            ln["mv"] = mv
-            ln["ve"] = ve
+            lns[nh]["mv"] = mv
+            lns[nh]["ve"] = ve
+
+        def ln_relu_sums(nh):
+            rl = late.tile([P, DOUT], F32, name="rl", tag="rl%d" % nh)
+            s1 = late.tile([P, 1], F32, name="s1", tag="s1")
+            nc.scalar.activation(out=rl[:], in_=lns[nh]["hb"][:], func=ACT.Relu, accum_out=s1[:])
+            s2 = late.tile([P, 1], F32, name="s2", tag="s2")
+            nc.scalar.activation(out=lns[nh]["hb"][:], in_=rl[:], func=ACT.Square, accum_out=s2[:])
+            lns[nh]["rl"] = rl
+            lns[nh]["s1"] = s1
+            lns[nh]["s2"] = s2
+
+        def ln_stats_from_sums(nh):
+            mv = late.tile([P, 2], F32, name="mv", tag="mv%d" % nh)
+            nc.vector.tensor_scalar_mul(out=mv[:, 0:1], in0=lns[nh]["s1"][:], scalar1=1.0 / DOUT)
+            nc.vector.tensor_scalar(
+                out=mv[:, 1:2],
+                in0=lns[nh]["s2"][:],
+                scalar1=1.0 / DOUT,
+                scalar2=LN_EPS,
+                op0=ALU.mult,
+                op1=ALU.add,
+            )
+            m2 = late.tile([P, 1], F32, name="m2", tag="m2")
+            nc.vector.tensor_tensor(out=m2[:], in0=mv[:, 0:1], in1=mv[:, 0:1], op=ALU.mult)
+            ve = late.tile([P, 1], F32, name="ve", tag="ve%d" % nh)
+            nc.vector.tensor_tensor(out=ve[:], in0=mv[:, 1:2], in1=m2[:], op=ALU.subtract)
+            lns[nh]["mv"] = mv
+            lns[nh]["ve"] = ve
 
         def ln_sqrt(nh):
-            sd = late.tile([P, 1], F32, name="sd", tag="sd")
-            nc.scalar.sqrt(out=sd[:], in_=ln["ve"][:])
-            ln["sd"] = sd
+            sd = late.tile([P, 1], F32, name="sd", tag="sd%d" % nh)
+            nc.scalar.sqrt(out=sd[:], in_=lns[nh]["ve"][:])
+            lns[nh]["sd"] = sd
 
         def ln_centre(nh):
-            y1 = late.tile([P, DOUT], F32, name="y1", tag="y1")
+            y1 = late.tile([P, DOUT], F32, name="y1", tag="y1%d" % nh)
             for o in range(2):
                 nc.vector.scalar_tensor_tensor(
                     out=y1[:, halves[o]],
-                    in0=ln["rl"][:, halves[o]],
-                    scalar=ln["mv"][:, 0:1],
+                    in0=lns[nh]["rl"][:, halves[o]],
+                    scalar=lns[nh]["mv"][:, 0:1],
                     in1=lng[:, halves[o]],
                     op0=ALU.subtract,
                     op1=ALU.mult,
                 )
-            ln["y1"] = y1
+            lns[nh]["y1"] = y1
 
         def ln_finish(nh):
-            rs = late.tile([P, 1], F32, name="rs", tag="rs")
-            nc.vector.reciprocal(out=rs[:], in_=ln["sd"][:])
-            yo = late.tile([P, DOUT], F32, name="yo", tag="yo")
+            rs = late.tile([P, 1], F32, name="rs", tag="rs%d" % nh)
+            nc.vector.reciprocal(out=rs[:], in_=lns[nh]["sd"][:])
+            yo = late.tile([P, DOUT], F32, name="yo", tag="yo%d" % nh)
             for o in range(2):
                 nc.vector.scalar_tensor_tensor(
                     out=yo[:, halves[o]],
-                    in0=ln["y1"][:, halves[o]],
+                    in0=lns[nh]["y1"][:, halves[o]],
                     scalar=rs[:, 0:1],
                     in1=lnb[:, halves[o]],
                     op0=ALU.mult,
@@ -497,15 +514,13 @@ def tile_transformeraggregator_pb_t_kernel(
         weight_unit(wv_raw, wg_b, 1, 0, 0, True, scopy, ps_t, "tb")
         dt_out(0)
         tf_uk(0, True)
-        dt_bank(1)
-        dt_bank(2)
         weight_unit(wv_raw, wg_a, 0, 0, 1, False, vcopy, ps_t, "tc")
         weight_unit(wv_raw, wg_b, 1, 0, 1, True, scopy, ps_v, "v")
         weight_quantise(wg_a, wvc, wvs, 0, 0)
         tf_frac(0)
         weight_quantise(wg_b, wvc, wvs, 1, 0)
         tf_sin(0)
-        for g in range(3):
+        for g in range(1, 3):
             tf_dma(g)
         tf_uk(1, False)
         for nh in range(2):
@@ -526,24 +541,24 @@ def tile_transformeraggregator_pb_t_kernel(
         weight_unit(wv_raw, wg_d, 1, 1, 1, True, scopy, ps_v, "v")
         weight_quantise(wg_c, wvc, wvs, 0, 1)
         weight_quantise(wg_d, wvc, wvs, 1, 1)
-        dt_out(1)
-        dt_out(2)
 
         for ct in range(8):
             load_w(wo_raw, wo_w, ct, CO)
         rootb = const.tile([P, 2, DN], BF16, name="rootb")
         nc.sync.dma_start(out=rootb[:], in_=root_node_feature.rearrange("(h p) k -> p h k", p=P))
         wob = const.tile([P, DOUT], BF16, name="wob")
-        nc.sync.dma_start(out=wob[:], in_=wo_b.partition_broadcast(P))
         lng = const.tile([P, DOUT], BF16, name="lng")
-        nc.sync.dma_start(out=lng[:], in_=ln_g.partition_broadcast(P))
         lnb = const.tile([P, DOUT], BF16, name="lnb")
-        nc.sync.dma_start(out=lnb[:], in_=ln_b.partition_broadcast(P))
 
-        for g in range(LT):
+        one = const.tile([P, 1], F32, name="one")
+        nc.vector.memset(one[:], 1.0)
+        for g in range(2):
+            sort_edges(g)
             transposes(g)
             load_group(g + NBUF)
-        for g in range(LQ):
+        for g in range(2, 4):
+            sort_edges(g)
+        for g in range(2):
             quantise(g)
         tf_frac(1)
 
@@ -565,34 +580,33 @@ def tile_transformeraggregator_pb_t_kernel(
 
         pending = []
         wo_wg = {}
+        vv = ("v", "v")
         for g in range(NG):
             if g + 3 < NG:
                 tf_dma(g + 3)
             multiply(g, 0)
             pool_rows(g, 0)
             multiply(g, 1)
-            if g == 16:
-                out_pass(0, 2, False)
-                out_pass(0, 0, False)
-                out_pass(0, 1, True)
             if g == NG - 1:
-                out_pass(1, 2, False)
-            if g == 10:
-                pt_add(0, acc_blocks(0, 1), False, True)
-                pooled_out(0, 1, "", scopy)
-                pending.append(lambda: pooled_quantise(0, 1))
-            if g + LQ < NG:
-                quantise(g + LQ)
+                out_pass(0, 2, ps_t, ("ta", "tb"))
+                out_pass(0, 0, ps_t, ("ta", "tb"))
+                out_pass(0, 1, ps_t, ("ta", "tb"))
+                out_pass(1, 2, ps_v, vv)
+            if g >= 1 and g + 2 < NG:
+                quantise(g + 2)
             for job in pending:
                 job()
             pending = []
             pool_rows(g, 1)
-            if g == 16:
-                ln_bias(0)
-            if g + LT < NG:
-                transposes(g + LT)
-                if g + LT + NBUF < NG:
-                    load_group(g + LT + NBUF)
+            ahead = []
+            if g == 0:
+                ahead = [2, 3]
+            elif g + 3 < NG:
+                ahead = [g + 3]
+            for t in ahead:
+                transposes(t)
+                if t + NBUF < NG:
+                    load_group(t + NBUF)
             if g < 12:
                 wg_i, wch, wpair = wo_units[g]
                 if wpair == 0:
@@ -602,9 +616,13 @@ def tile_transformeraggregator_pb_t_kernel(
                     pending.append(
                         lambda t=wo_wg[0], a=wg_i, b=wch: weight_quantise(t, woc, wos, a, b)
                     )
-            if g == NG - 1:
-                pt_add(1, acc_blocks(1, 1), False, False)
-            pt_add(g // 10, tmp_blocks(g), g % 10 == 0, g == NG - 1)
+            if g + 4 < NG:
+                sort_edges(g + 4)
+            if g < 2:
+                dt_bank(g + 1)
+                dt_out(g + 1)
+            if g == 0:
+                quantise(2)
             if g in (1, 5, 9):
                 tf_uk((g + 7) // 4, False)
             if g in (2, 6, 10):
@@ -612,30 +630,41 @@ def tile_transformeraggregator_pb_t_kernel(
             if g in (0, 3, 7, 11):
                 tf_sin((g + 5) // 4)
             if g == 12:
-                pooled_out(0, 0, "tc", scopy)
+                nc.sync.dma_start(out=wob[:], in_=wo_b.partition_broadcast(P))
+                nc.sync.dma_start(out=lng[:], in_=ln_g.partition_broadcast(P))
+                nc.sync.dma_start(out=lnb[:], in_=ln_b.partition_broadcast(P))
+            if g == 10:
+                pooled_round(0, 0, scopy)
+                pooled_round(0, 1, scopy)
+            if g == 12:
+                pooled_transpose(0, 0, ps_t, "tc", scopy)
                 pending.append(lambda: pooled_quantise(0, 0))
+                nc.scalar.sqrt(out=zout[:], in_=one[:])
+            if g == 13:
+                pooled_transpose(0, 1, ps_t, "tc", scopy)
+                pending.append(lambda: pooled_quantise(0, 1))
             if g == 14:
                 rg_t = root_unit()
                 pending.append(
                     lambda t=rg_t: nc.vector.quantize_mx(out=rcc[:].bitcast(FP8X4), scales=rcs[:], in_=t[:])
                 )
-            if g == 16:
-                ln_relu(0)
-            if g == 17:
-                ln_stats(0)
-                ln_sqrt(0)
-                ln_centre(0)
-            if g == 18:
-                ln_finish(0)
 
-        pooled_out(1, 1, "", vcopy)
-        pooled_out(1, 0, "ta", scopy)
-        pooled_quantise(1, 1)
-        out_pass(1, 1, False)
+        pooled_round(1, 0, scopy)
+        pooled_round(1, 1, vcopy)
+        ln_bias(0)
+        pooled_transpose(1, 0, ps_t, "tc", scopy)
+        pooled_transpose(1, 1, ps_v, "v", vcopy)
+        ln_relu_sums(0)
         pooled_quantise(1, 0)
-        out_pass(1, 0, True)
+        out_pass(1, 0, ps_v, vv)
+        pooled_quantise(1, 1)
+        out_pass(1, 1, ps_v, vv)
+        ln_stats_from_sums(0)
+        ln_sqrt(0)
         ln_bias(1)
         ln_relu(1)
+        ln_centre(0)
+        ln_finish(0)
         ln_stats(1)
         ln_sqrt(1)
         ln_centre(1)

@@ -89,8 +89,6 @@ def tile_transformeraggregator_pb_t_kernel(
             nc.sync.dma_start(out=rt[:], in_=root_ts.rearrange("(h p o) -> p h o", p=P, o=1))
             nc.sync.dma_start(out=xw[0:32, 0:4], in_=time_w.rearrange("(p t) o -> p (t o)", t=4))
             nc.sync.dma_start(out=xw[0:32, 16:20], in_=time_b.rearrange("(p t) -> p t", t=4))
-            nc.sync.dma_start(out=attb[:], in_=att.rearrange("(h p) j c -> p h (j c)", p=P))
-        nc.sync.dma_start(out=brow[0:1, :], in_=wv_b.rearrange("(o c) -> o c", o=1))
 
         wv_raw = []
         wo_raw = []
@@ -112,7 +110,12 @@ def tile_transformeraggregator_pb_t_kernel(
                 in_=neighbor_edge_feature[rows, j0 : j0 + 2, :].rearrange("p j k -> p (j k)"),
             )
 
-        for ct in range(8):
+        for ct in range(4):
+            load_w(wv_raw, wv_w, ct, 1024)
+        with nc.allow_non_contiguous_dma(reason="80-byte rows of attention weights"):
+            nc.sync.dma_start(out=attb[:], in_=att.rearrange("(h p) j c -> p h (j c)", p=P))
+        nc.sync.dma_start(out=brow[0:1, :], in_=wv_b.rearrange("(o c) -> o c", o=1))
+        for ct in range(4, 8):
             load_w(wv_raw, wv_w, ct, 1024)
         load_group(0)
         for g in range(1, NBUF):
@@ -171,25 +174,6 @@ def tile_transformeraggregator_pb_t_kernel(
         nc.vector.tensor_scalar(
             out=pb[:], in0=prm[:, 16:20], scalar1=0.5 / math.pi, scalar2=0.25, op0=ALU.mult, op1=ALU.add
         )
-        attf = const.tile([P, 2, NNEI, 2], F32, name="attf")
-        nc.vector.tensor_copy(out=attf[:].rearrange("p h j c -> p h (j c)"), in_=attb[:])
-        satt = const.tile([P, 2, 2], F32, name="satt")
-        nc.vector.tensor_reduce(
-            out=satt[:], in_=attf[:].rearrange("p h j c -> p h c j"), axis=AX.X, op=ALU.add
-        )
-
-        wvb = const.tile([P, DOUT], BF16, name="wvb")
-        for ch in range(2):
-            bp = ps_v.tile([P, 512], F32, name="bp", tag="v")
-            nc.tensor.matmul(
-                out=bp[:],
-                lhsT=identb[:, 0:1].to_broadcast([P, P]),
-                rhs=brow[:, ch * 512 : (ch + 1) * 512],
-                start=True,
-                stop=True,
-            )
-            nc.vector.tensor_copy(out=wvb[:, ch * 512 : (ch + 1) * 512], in_=bp[:])
-
         dts = const.tile([P, 1280], F32, name="dts")
         dt_banks = {}
 
@@ -446,9 +430,9 @@ def tile_transformeraggregator_pb_t_kernel(
 
         def ln_relu_sums(nh):
             rl = late.tile([P, DOUT], F32, name="rl", tag="rl%d" % nh)
-            s1 = late.tile([P, 1], F32, name="s1", tag="s1")
+            s1 = late.tile([P, 1], F32, name="s1", tag="s1%d" % nh)
             nc.scalar.activation(out=rl[:], in_=lns[nh]["hb"][:], func=ACT.Relu, accum_out=s1[:])
-            s2 = late.tile([P, 1], F32, name="s2", tag="s2")
+            s2 = late.tile([P, 1], F32, name="s2", tag="s2%d" % nh)
             nc.scalar.activation(out=lns[nh]["hb"][:], in_=rl[:], func=ACT.Square, accum_out=s2[:])
             lns[nh]["rl"] = rl
             lns[nh]["s1"] = s1
@@ -465,7 +449,7 @@ def tile_transformeraggregator_pb_t_kernel(
                 op0=ALU.mult,
                 op1=ALU.add,
             )
-            m2 = late.tile([P, 1], F32, name="m2", tag="m2")
+            m2 = late.tile([P, 1], F32, name="m2", tag="m2%d" % nh)
             nc.vector.tensor_tensor(out=m2[:], in0=mv[:, 0:1], in1=mv[:, 0:1], op=ALU.mult)
             ve = late.tile([P, 1], F32, name="ve", tag="ve%d" % nh)
             nc.vector.tensor_tensor(out=ve[:], in0=mv[:, 1:2], in1=m2[:], op=ALU.subtract)
@@ -519,6 +503,23 @@ def tile_transformeraggregator_pb_t_kernel(
         weight_quantise(wg_a, wvc, wvs, 0, 0)
         tf_frac(0)
         weight_quantise(wg_b, wvc, wvs, 1, 0)
+        attf = const.tile([P, 2, NNEI, 2], F32, name="attf")
+        nc.vector.tensor_copy(out=attf[:].rearrange("p h j c -> p h (j c)"), in_=attb[:])
+        satt = const.tile([P, 2, 2], F32, name="satt")
+        nc.vector.tensor_reduce(
+            out=satt[:], in_=attf[:].rearrange("p h j c -> p h c j"), axis=AX.X, op=ALU.add
+        )
+        wvb = const.tile([P, DOUT], BF16, name="wvb")
+        for ch in range(2):
+            bp = ps_v.tile([P, 512], F32, name="bp", tag="v")
+            nc.tensor.matmul(
+                out=bp[:],
+                lhsT=identb[:, 0:1].to_broadcast([P, P]),
+                rhs=brow[:, ch * 512 : (ch + 1) * 512],
+                start=True,
+                stop=True,
+            )
+            nc.vector.tensor_copy(out=wvb[:, ch * 512 : (ch + 1) * 512], in_=bp[:])
         tf_sin(0)
         for g in range(1, 3):
             tf_dma(g)
@@ -650,10 +651,10 @@ def tile_transformeraggregator_pb_t_kernel(
                 )
 
         pooled_round(1, 0, scopy)
-        pooled_round(1, 1, vcopy)
+        pooled_round(1, 1, scopy)
         ln_bias(0)
         pooled_transpose(1, 0, ps_t, "tc", scopy)
-        pooled_transpose(1, 1, ps_v, "v", vcopy)
+        pooled_transpose(1, 1, ps_v, "v", scopy)
         ln_relu_sums(0)
         pooled_quantise(1, 0)
         out_pass(1, 0, ps_v, vv)
@@ -662,10 +663,10 @@ def tile_transformeraggregator_pb_t_kernel(
         ln_stats_from_sums(0)
         ln_sqrt(0)
         ln_bias(1)
-        ln_relu(1)
+        ln_relu_sums(1)
         ln_centre(0)
         ln_finish(0)
-        ln_stats(1)
+        ln_stats_from_sums(1)
         ln_sqrt(1)
         ln_centre(1)
         ln_finish(1)

@@ -56,18 +56,28 @@ def tile_transformeraggregator_pb_t_kernel(
         ps_v = es.enter_context(tc.psum_pool(name="ps_v", bufs=5))
         es.enter_context(tc.manual_schedule())
 
-        identf = const.tile([P, P], F32, name="identf")
-        make_identity(nc, identf[:])
-        identb = const.tile([P, P], BF16, name="identb")
-        make_identity(nc, identb[:])
+        nt = const.tile([P, 2, NNEI], BF16, name="nt")
+        rt = const.tile([P, 2, 1], BF16, name="rt")
+        attb = const.tile([P, 2, 2 * NNEI], BF16, name="attb")
+        xw = const.tile([P, 32], BF16, name="xw")
+        brow = const.tile([P, DOUT], BF16, name="brow")
         zin = const.tile([P, 1], F32, name="zin")
         zout = const.tile([P, 1], F32, name="zout")
-        nc.vector.memset(zin[:], 0.0)
-        nc.scalar.activation(out=zout[:], in_=zin[:], func=ACT.Sin)
-        xw = const.tile([P, 32], BF16, name="xw")
+        warm = const.tile([P, 512], BF16, name="warm")
         nc.vector.memset(xw[:], 0.0)
-        brow = const.tile([P, DOUT], BF16, name="brow")
+        nc.vector.memset(zin[:], 0.0)
+        nc.vector.memset(warm[:], 0.0)
         nc.vector.memset(brow[:], 0.0)
+        identf = const.tile([P, P], F32, name="identf")
+        make_identity(nc, identf[:])
+        with nc.allow_non_contiguous_dma(reason="a few short rows of time stamps and weights"):
+            nc.scalar.dma_start(out=nt[:], in_=neighbor_ts.rearrange("(h p) j -> p h j", p=P))
+            nc.scalar.dma_start(out=rt[:], in_=root_ts.rearrange("(h p o) -> p h o", p=P, o=1))
+            nc.scalar.dma_start(out=xw[0:32, 0:4], in_=time_w.rearrange("(p t) o -> p (t o)", t=4))
+            nc.scalar.dma_start(out=xw[0:32, 16:20], in_=time_b.rearrange("(p t) -> p t", t=4))
+            nc.scalar.dma_start(out=brow[0:1, :], in_=wv_b.rearrange("(o c) -> o c", o=1))
+            nc.scalar.dma_start(out=attb[:], in_=att.rearrange("(h p) j c -> p h (j c)", p=P))
+        nc.scalar.activation(out=zout[:], in_=zin[:], func=ACT.Sin)
         nds = []
         eds = []
         for b in range(NBUF):
@@ -80,15 +90,6 @@ def tile_transformeraggregator_pb_t_kernel(
             es_t = const.tile([P, 2, 2, P], F32, name="es%d" % b)
             nc.vector.memset(es_t[:, :, :, 96:128], 0.0)
             ess.append(es_t)
-
-        nt = const.tile([P, 2, NNEI], BF16, name="nt")
-        rt = const.tile([P, 2, 1], BF16, name="rt")
-        attb = const.tile([P, 2, 2 * NNEI], BF16, name="attb")
-        with nc.allow_non_contiguous_dma(reason="a few short rows of time stamps and weights"):
-            nc.sync.dma_start(out=nt[:], in_=neighbor_ts.rearrange("(h p) j -> p h j", p=P))
-            nc.sync.dma_start(out=rt[:], in_=root_ts.rearrange("(h p o) -> p h o", p=P, o=1))
-            nc.sync.dma_start(out=xw[0:32, 0:4], in_=time_w.rearrange("(p t) o -> p (t o)", t=4))
-            nc.sync.dma_start(out=xw[0:32, 16:20], in_=time_b.rearrange("(p t) -> p t", t=4))
 
         wv_raw = []
         wo_raw = []
@@ -110,14 +111,13 @@ def tile_transformeraggregator_pb_t_kernel(
                 in_=neighbor_edge_feature[rows, j0 : j0 + 2, :].rearrange("p j k -> p (j k)"),
             )
 
-        for ct in range(4):
-            load_w(wv_raw, wv_w, ct, 1024)
-        with nc.allow_non_contiguous_dma(reason="80-byte rows of attention weights"):
-            nc.sync.dma_start(out=attb[:], in_=att.rearrange("(h p) j c -> p h (j c)", p=P))
-        nc.sync.dma_start(out=brow[0:1, :], in_=wv_b.rearrange("(o c) -> o c", o=1))
-        for ct in range(4, 8):
+        for ct in range(2):
             load_w(wv_raw, wv_w, ct, 1024)
         load_group(0)
+        for ct in range(2, 4):
+            load_w(wv_raw, wv_w, ct, 1024)
+        for ct in range(4, 8):
+            load_w(wv_raw, wv_w, ct, 1024)
         for g in range(1, NBUF):
             load_group(g)
 
@@ -137,14 +137,21 @@ def tile_transformeraggregator_pb_t_kernel(
         def words(ap):
             return ap.bitcast(F32).rearrange("p (i r u) -> p i r u", i=2, u=2)
 
-        def unit4(srcs, dst_words, evac, parts, pool, tag):
+        turn = [0]
+
+        def next_bank():
+            turn[0] += 1
+            return ("ta", "tb", "tc")[turn[0] % 3]
+
+        def unit4(srcs, dst_words, evac, parts, pool, tag, spins=0):
             t = pool.tile([P, 2, 2, P], F32, name="tr", tag=tag)
+            spin(t[:].rearrange("p i u r -> p (i u r)"), spins)
             for s in range(4):
                 nc.tensor.transpose(t[:, s // 2, s % 2, :], srcs[s], identf[:])
             evac(out=dst_words, in_=t[0:parts].rearrange("p i u r -> p i r u"))
 
-        negi = const.tile([P, P], BF16, name="negi")
-        nc.vector.tensor_scalar_mul(out=negi[:], in0=identb[:], scalar1=-1.0)
+        identb = const.tile([P, P], BF16, name="identb")
+        nc.vector.tensor_copy(out=identb[:], in_=identf[:])
         sel = const.tile([P, P], BF16, name="sel")
         nc.vector.tensor_copy(
             out=sel[:].rearrange("p (a q) -> p a q", a=4),
@@ -153,11 +160,14 @@ def tile_transformeraggregator_pb_t_kernel(
         lnt = const.tile([P, 5, 2, P], BF16, name="lnt")
         nt40 = nt[:].rearrange("p h j -> p (h j)").rearrange("p (m a i) -> p m i a", m=5, a=4)
         for i in range(2):
-            nc.vector.tensor_copy(
+            nc.vector.tensor_scalar_mul(
                 out=lnt[:, :, i, 0:96].rearrange("p m (a q) -> p m a q", a=3),
-                in_=nt40[:, :, i, 1:4].unsqueeze(3).to_broadcast([P, 5, 3, 32]),
+                in0=nt40[:, :, i, 1:4].unsqueeze(3).to_broadcast([P, 5, 3, 32]),
+                scalar1=-1.0,
             )
-            nc.vector.tensor_copy(out=lnt[:, :, i, 96:128], in_=nt40[:, :, i, 0:1].to_broadcast([P, 5, 32]))
+            nc.vector.tensor_scalar_mul(
+                out=lnt[:, :, i, 96:128], in0=nt40[:, :, i, 0:1].to_broadcast([P, 5, 32]), scalar1=-1.0
+            )
         lrt = const.tile([P, 3, P], BF16, name="lrt")
         nc.vector.tensor_copy(out=lrt[:, 0, :], in_=rt[:, 0, :].to_broadcast([P, P]))
         nc.vector.tensor_copy(out=lrt[:, 1, 0:32], in_=rt[:, 0, :].to_broadcast([P, 32]))
@@ -166,7 +176,12 @@ def tile_transformeraggregator_pb_t_kernel(
         nc.vector.tensor_copy(out=lrt[:, 2, :], in_=rt[:, 1, :].to_broadcast([P, P]))
         lrt_of_m = (0, 0, 1, 2, 2)
 
+        def spin(bank, n):
+            for r in range(n):
+                nc.tensor.matmul(out=bank, lhsT=warm[:, 0:128], rhs=warm[:], start=True, stop=True)
+
         prm = ps_v.tile([P, 512], F32, name="prm", tag="v")
+        spin(prm[:], 8)
         nc.tensor.matmul(out=prm[:, 0:32], lhsT=sel[:], rhs=xw[:], start=True, stop=True)
         pa = const.tile([P, 4], F32, name="pa")
         pb = const.tile([P, 4], F32, name="pb")
@@ -174,59 +189,80 @@ def tile_transformeraggregator_pb_t_kernel(
         nc.vector.tensor_scalar(
             out=pb[:], in0=prm[:, 16:20], scalar1=0.5 / math.pi, scalar2=0.25, op0=ALU.mult, op1=ALU.add
         )
-        dts = const.tile([P, 1280], F32, name="dts")
-        dt_banks = {}
+        dts = const.tile([P, 4, 256], F32, name="dts")
 
-        def dt_bank(b):
-            nblk = min(4, 10 - 4 * b)
+        def dt_bank(ms):
             dtp = ps_v.tile([P, 512], F32, name="dtp", tag="v")
-            for l in range(nblk):
-                blk = 4 * b + l
+            for l in range(2 * len(ms)):
+                m = ms[l // 2]
                 cols = slice(l * P, (l + 1) * P)
-                nc.tensor.matmul(
-                    out=dtp[:, cols], lhsT=lrt[:, lrt_of_m[blk // 2], :], rhs=identb[:], start=True, stop=False
-                )
-                nc.tensor.matmul(
-                    out=dtp[:, cols], lhsT=lnt[:, blk // 2, blk % 2, :], rhs=negi[:], start=False, stop=True
-                )
-            dt_banks[b] = (dtp, nblk)
+                nc.tensor.matmul(out=dtp[:, cols], lhsT=lrt[:, lrt_of_m[m], :], rhs=identb[:], start=True, stop=False)
+                nc.tensor.matmul(out=dtp[:, cols], lhsT=lnt[:, m, l % 2, :], rhs=identb[:], start=False, stop=True)
+            return dtp
 
-        def dt_out(b):
-            dtp, nblk = dt_banks[b]
-            nc.scalar.copy(out=dts[:, 512 * b : 512 * b + nblk * P], in_=dtp[:, 0 : nblk * P])
+        def dt_pair(m):
+            dtp = dt_bank((m, m + 1))
+            nc.scalar.copy(out=dts[:, m - 1 : m + 1, :].rearrange("p m w -> p (m w)"), in_=dtp[:])
 
         tf_t = {}
+        tf_first_g = []
 
-        def tf_affine(eng, dst, m, t):
-            eng.tensor_scalar(
-                out=dst[:, t, :],
-                in0=dts[:, 256 * m : 256 * (m + 1)],
-                scalar1=pa[:, t : t + 1],
-                scalar2=pb[:, t : t + 1],
-                op0=ALU.mult,
-                op1=ALU.add,
-            )
+        def tf_first():
+            bank_s = dt_bank((0,))
+            bank_v = dt_bank((0,))
+            ut = tfp.tile([P, 4, 256], F32, name="ut", tag="ut", bufs=2)
+            kt = tfp.tile([P, 4, 256], I32, name="kt", tag="kt", bufs=2)
+            for t in range(2):
+                nc.scalar.activation(
+                    out=ut[:, t, :],
+                    in_=bank_s[:, 0:256],
+                    func=ACT.Identity,
+                    scale=pa[:, t : t + 1],
+                    bias=pb[:, t : t + 1],
+                )
+            for t in range(2, 4):
+                nc.vector.tensor_scalar(
+                    out=ut[:, t, :],
+                    in0=bank_v[:, 0:256],
+                    scalar1=pa[:, t : t + 1],
+                    scalar2=pb[:, t : t + 1],
+                    op0=ALU.mult,
+                    op1=ALU.add,
+                )
+            nc.vector.tensor_copy(out=kt[:, 0:2, :], in_=ut[:, 0:2, :])
+            nc.vector.tensor_copy(out=kt[:, 2:4, :], in_=ut[:, 2:4, :])
+            gt = tfp.tile([P, 256, 4], F32, name="gt", tag="gt")
+            for i in range(2):
+                cols = slice(i * P, (i + 1) * P)
+                nc.vector.tensor_tensor(
+                    out=gt[:, cols, :],
+                    in0=ut[:, :, cols].rearrange("p t w -> p w t"),
+                    in1=kt[:, :, cols].rearrange("p t w -> p w t"),
+                    op=ALU.subtract,
+                )
+            tf_first_g.append(gt)
+            tfg = tfp.tile([P, 1024], BF16, name="tfg", tag="tfg", bufs=2)
+            tf_t[0] = [tfg]
 
-        def tf_uk(m, split):
-            ut = tfp.tile([P, 4, 256], F32, name="ut", tag="ut")
-            kt = tfp.tile([P, 4, 256], I32, name="kt", tag="kt")
+        def tf_first_sin(i):
+            gtf = tf_first_g[0][:].rearrange("p w t -> p (w t)")
+            cols = slice(512 * i, 512 * i + 512)
+            nc.scalar.activation(out=tf_t[0][0][:, cols], in_=gtf[:, cols], func=ACT.Sin, scale=2.0 * math.pi)
+
+        def tf_uk(m):
+            ut = tfp.tile([P, 4, 256], F32, name="ut", tag="ut", bufs=2)
+            kt = tfp.tile([P, 4, 256], I32, name="kt", tag="kt", bufs=2)
             tf_t[m] = [ut, kt]
             for t in range(4):
-                if split and t < 2:
-                    nc.scalar.activation(
-                        out=ut[:, t, :],
-                        in_=dts[:, 256 * m : 256 * (m + 1)],
-                        func=ACT.Identity,
-                        scale=pa[:, t : t + 1],
-                        bias=pb[:, t : t + 1],
+                for dst in (ut, kt):
+                    nc.gpsimd.tensor_scalar(
+                        out=dst[:, t, :],
+                        in0=dts[:, m - 1, :],
+                        scalar1=pa[:, t : t + 1],
+                        scalar2=pb[:, t : t + 1],
+                        op0=ALU.mult,
+                        op1=ALU.add,
                     )
-                    tf_affine(nc.gpsimd, kt, m, t)
-                elif split:
-                    tf_affine(nc.vector, ut, m, t)
-                    tf_affine(nc.vector, kt, m, t)
-                else:
-                    tf_affine(nc.gpsimd, ut, m, t)
-                    tf_affine(nc.gpsimd, kt, m, t)
 
         def tf_frac(m):
             ut, kt = tf_t[m]
@@ -243,13 +279,7 @@ def tile_transformeraggregator_pb_t_kernel(
             gt = tf_t[m][0]
             tfg = tfp.tile([P, 1024], BF16, name="tfg", tag="tfg", bufs=2)
             gtf = gt[:].rearrange("p w t -> p (w t)")
-            if m == 0:
-                nc.scalar.activation(
-                    out=get_gg(0)[96:128, 1024:2048], in_=gtf[96:128, :], func=ACT.Sin, scale=2.0 * math.pi
-                )
-                nc.scalar.activation(out=tfg[0:96, :], in_=gtf[0:96, :], func=ACT.Sin, scale=2.0 * math.pi)
-            else:
-                nc.scalar.activation(out=tfg[:], in_=gtf, func=ACT.Sin, scale=2.0 * math.pi)
+            nc.scalar.activation(out=tfg[:], in_=gtf, func=ACT.Sin, scale=2.0 * math.pi)
             tf_t[m] = [tfg]
 
         ggs = {}
@@ -268,7 +298,7 @@ def tile_transformeraggregator_pb_t_kernel(
             wg_t = wgp.tile([P, 2048], BF16, name="wg", tag="wg", align_bytes=64)
             return wg_t
 
-        def weight_unit(raw, wg, g, ch, pair, natural, evac, pool, tag):
+        def weight_unit(raw, wg, g, ch, pair, natural, evac, pool, tag, spins=0):
             srcs = []
             for i in range(2):
                 ww = raw[ch * 4 + pair * 2 + i][:].bitcast(F32)
@@ -279,7 +309,15 @@ def tile_transformeraggregator_pb_t_kernel(
                         )
                     else:
                         srcs.append(ww[:, 256 * g + 128 * u : 256 * g + 128 * u + 128])
-            unit4(srcs, words(wg[:, pair * 1024 : (pair + 1) * 1024]), evac, P, pool, tag)
+            unit4(srcs, words(wg[:, pair * 1024 : (pair + 1) * 1024]), evac, P, pool, tag, spins)
+
+        def weight_quantise_pair(wg, codes, scales, g, ch, pair):
+            lo = ch * 512 + pair * 256
+            nc.vector.quantize_mx(
+                out=codes[:, g, lo : lo + 256].bitcast(FP8X4),
+                scales=scales[:, g, lo : lo + 256],
+                in_=wg[:, pair * 1024 : (pair + 1) * 1024],
+            )
 
         def weight_quantise(wg, codes, scales, g, ch):
             nc.vector.quantize_mx(
@@ -291,21 +329,24 @@ def tile_transformeraggregator_pb_t_kernel(
         quant = {}
         banks = {}
 
-        def transposes(g):
+        def turn_nodes(g, spins=0):
             ndw = nds[g % NBUF][:].bitcast(F32)
-            srcs_a = []
-            srcs_b = []
+            srcs = []
             for i in range(2):
                 for u in range(2):
                     lo = i * 256 + 128 * u
-                    srcs_a.append(ndw[:, lo : lo + 128])
-                    srcs_b.append(ess[g % 3][:, i, u, :])
-            gg = get_gg(g)
-            unit4(srcs_a, words(gg[:, 0:1024]), nc.scalar.copy, P, ps_t, "ta")
-            unit4(srcs_b, words(gg[0:96, 1024:2048]), nc.scalar.copy, 96, ps_t, "tb")
+                    srcs.append(ndw[:, lo : lo + 128])
+            unit4(srcs, words(get_gg(g)[:, 0:1024]), nc.scalar.copy, P, ps_t, next_bank(), spins)
 
-        def sort_edges(g):
-            nc.scalar.copy(
+        def turn_edges(g):
+            srcs = []
+            for i in range(2):
+                for u in range(2):
+                    srcs.append(ess[g % 3][:, i, u, :])
+            unit4(srcs, words(get_gg(g)[0:96, 1024:2048]), nc.scalar.copy, 96, ps_t, next_bank())
+
+        def sort_edges(g, copy=nc.scalar.copy):
+            copy(
                 out=ess[g % 3][:, :, :, 0:96],
                 in_=eds[g % NBUF][:].bitcast(F32).rearrange("p (i w u) -> p i u w", i=2, u=2),
             )
@@ -316,16 +357,16 @@ def tile_transformeraggregator_pb_t_kernel(
             nc.vector.quantize_mx(out=cq[:].bitcast(FP8X4), scales=sq[:], in_=ggs[g][:])
             quant[g] = (cq, sq)
 
-        def multiply(g, i):
+        def multiply(g, i, chs):
             cq, sq = quant[g]
-            pair = []
-            for ch in range(2):
+            pair = {}
+            for ch in chs:
                 v = ps_v.tile([P, 512], F32, name="v", tag="v")
-                pair.append(v)
-            for k in range(2):
-                rows = slice(k * 256 + i * P, k * 256 + (i + 1) * P)
-                for ch in range(2):
-                    cs = slice(ch * 512, (ch + 1) * 512)
+                pair[ch] = v
+            for ch in chs:
+                cs = slice(ch * 512, (ch + 1) * 512)
+                for k in range(2):
+                    rows = slice(k * 256 + i * P, k * 256 + (i + 1) * P)
                     nc.tensor.matmul_mx(
                         out=pair[ch][:],
                         lhsT=cq[:, rows].bitcast(FP8X4),
@@ -337,11 +378,11 @@ def tile_transformeraggregator_pb_t_kernel(
                     )
             banks[(g, i)] = pair
 
-        def pool_rows(g, i):
+        def pool_rows(g, i, chs):
             nh = g // 10
             j = 2 * (g % 10) + i
             pair = banks[(g, i)]
-            for ch in range(2):
+            for ch in chs:
                 a = acc[nh][:, ch * 512 : (ch + 1) * 512]
                 nc.vector.scalar_tensor_tensor(
                     out=a,
@@ -491,26 +532,16 @@ def tile_transformeraggregator_pb_t_kernel(
 
         vcopy = nc.vector.tensor_copy
         scopy = nc.scalar.copy
-        dt_bank(0)
+        tf_first()
+        dt_pair(1)
+        tf_uk(1)
         wg_a = new_wg()
         wg_b = new_wg()
-        weight_unit(wv_raw, wg_a, 0, 0, 0, False, vcopy, ps_t, "ta")
-        weight_unit(wv_raw, wg_b, 1, 0, 0, True, scopy, ps_t, "tb")
-        dt_out(0)
-        tf_uk(0, True)
-        weight_unit(wv_raw, wg_a, 0, 0, 1, False, vcopy, ps_t, "tc")
-        weight_unit(wv_raw, wg_b, 1, 0, 1, True, scopy, ps_v, "v")
-        weight_quantise(wg_a, wvc, wvs, 0, 0)
-        tf_frac(0)
-        weight_quantise(wg_b, wvc, wvs, 1, 0)
-        attf = const.tile([P, 2, NNEI, 2], F32, name="attf")
-        nc.vector.tensor_copy(out=attf[:].rearrange("p h j c -> p h (j c)"), in_=attb[:])
-        satt = const.tile([P, 2, 2], F32, name="satt")
-        nc.vector.tensor_reduce(
-            out=satt[:], in_=attf[:].rearrange("p h j c -> p h c j"), axis=AX.X, op=ALU.add
-        )
+        weight_unit(wv_raw, wg_a, 0, 0, 0, False, scopy, ps_t, next_bank(), 1)
+        weight_unit(wv_raw, wg_b, 1, 0, 0, True, scopy, ps_t, next_bank(), 1)
         wvb = const.tile([P, DOUT], BF16, name="wvb")
-        for ch in range(2):
+
+        def bias_row(ch, evac):
             bp = ps_v.tile([P, 512], F32, name="bp", tag="v")
             nc.tensor.matmul(
                 out=bp[:],
@@ -519,49 +550,51 @@ def tile_transformeraggregator_pb_t_kernel(
                 start=True,
                 stop=True,
             )
-            nc.vector.tensor_copy(out=wvb[:, ch * 512 : (ch + 1) * 512], in_=bp[:])
-        tf_sin(0)
-        for g in range(1, 3):
-            tf_dma(g)
-        tf_uk(1, False)
-        for nh in range(2):
-            for ch in range(2):
-                nc.gpsimd.tensor_scalar(
-                    out=acc[nh][:, ch * 512 : (ch + 1) * 512],
-                    in0=wvb[:, ch * 512 : (ch + 1) * 512],
-                    scalar1=satt[:, nh, ch : ch + 1],
-                    scalar2=0.0,
-                    op0=ALU.mult,
-                    op1=ALU.add,
-                )
-        wg_c = new_wg()
-        weight_unit(wv_raw, wg_c, 0, 1, 0, False, vcopy, ps_t, "ta")
-        wg_d = new_wg()
-        weight_unit(wv_raw, wg_d, 1, 1, 0, True, scopy, ps_t, "tb")
-        weight_unit(wv_raw, wg_c, 0, 1, 1, False, vcopy, ps_t, "tc")
-        weight_unit(wv_raw, wg_d, 1, 1, 1, True, scopy, ps_v, "v")
-        weight_quantise(wg_c, wvc, wvs, 0, 1)
-        weight_quantise(wg_d, wvc, wvs, 1, 1)
+            evac(out=wvb[:, ch * 512 : (ch + 1) * 512], in_=bp[:])
 
-        for ct in range(8):
-            load_w(wo_raw, wo_w, ct, CO)
-        rootb = const.tile([P, 2, DN], BF16, name="rootb")
-        nc.sync.dma_start(out=rootb[:], in_=root_node_feature.rearrange("(h p) k -> p h k", p=P))
+        def acc_start(nh, ch):
+            nc.gpsimd.tensor_scalar(
+                out=acc[nh][:, ch * 512 : (ch + 1) * 512],
+                in0=wvb[:, ch * 512 : (ch + 1) * 512],
+                scalar1=satt[:, nh, ch : ch + 1],
+                scalar2=0.0,
+                op0=ALU.mult,
+                op1=ALU.add,
+            )
+
+        tf_first_sin(0)
+        bias_row(0, vcopy)
+        attf = const.tile([P, 2, NNEI, 2], F32, name="attf")
+        nc.vector.tensor_copy(out=attf[:].rearrange("p h j c -> p h (j c)"), in_=attb[:])
+        sort_edges(0, vcopy)
+        turn_nodes(0, 1)
+        tf_first_sin(1)
+        turn_edges(0)
+        satt = const.tile([P, 2, 2], F32, name="satt")
+        nc.vector.tensor_reduce(
+            out=satt[:], in_=attf[:].rearrange("p h j c -> p h c j"), axis=AX.X, op=ALU.add
+        )
+        acc_start(0, 0)
+        weight_quantise_pair(wg_a, wvc, wvs, 0, 0, 0)
+        weight_quantise_pair(wg_b, wvc, wvs, 1, 0, 0)
+        nc.vector.tensor_copy(out=get_gg(0)[96:128, 1024:2048], in_=tf_t[0][0][96:128, :])
+        for g in range(1, 4):
+            tf_dma(g)
+        weight_unit(wv_raw, wg_a, 0, 0, 1, False, scopy, ps_t, next_bank(), 1)
+        weight_unit(wv_raw, wg_b, 1, 0, 1, True, vcopy, ps_t, next_bank(), 1)
+        quantise(0)
+        weight_quantise_pair(wg_a, wvc, wvs, 0, 0, 1)
+        weight_quantise_pair(wg_b, wvc, wvs, 1, 0, 1)
+        wg_c = new_wg()
+        weight_unit(wv_raw, wg_c, 0, 1, 0, False, scopy, ps_t, next_bank(), 2)
+        wg_d = new_wg()
+        weight_unit(wv_raw, wg_d, 1, 1, 0, True, scopy, ps_t, next_bank(), 1)
         wob = const.tile([P, DOUT], BF16, name="wob")
         lng = const.tile([P, DOUT], BF16, name="lng")
         lnb = const.tile([P, DOUT], BF16, name="lnb")
-
+        rootb = const.tile([P, 2, DN], BF16, name="rootb")
         one = const.tile([P, 1], F32, name="one")
         nc.vector.memset(one[:], 1.0)
-        for g in range(2):
-            sort_edges(g)
-            transposes(g)
-            load_group(g + NBUF)
-        for g in range(2, 4):
-            sort_edges(g)
-        for g in range(2):
-            quantise(g)
-        tf_frac(1)
 
         wo_units = []
         for g in range(3):
@@ -579,58 +612,107 @@ def tile_transformeraggregator_pb_t_kernel(
             unit4(srcs, words(rg[:]), scopy, P, ps_t, "tc")
             return rg
 
+        sort_edges(1)
+        tf_frac(1)
+        for i in range(2):
+            multiply(0, i, (0,))
+        pool_rows(0, 0, (0,))
+        pool_rows(0, 1, (0,))
+        weight_unit(wv_raw, wg_c, 0, 1, 1, False, scopy, ps_t, next_bank())
+        bias_row(1, scopy)
+        weight_unit(wv_raw, wg_d, 1, 1, 1, True, vcopy, ps_t, next_bank())
+        acc_start(0, 1)
+        weight_quantise(wg_c, wvc, wvs, 0, 1)
+        turn_nodes(1, 1)
+        turn_edges(1)
+        sort_edges(2)
+        weight_quantise(wg_d, wvc, wvs, 1, 1)
+        for i in range(2):
+            multiply(0, i, (1,))
+        quantise(1)
+        pool_rows(0, 0, (1,))
+        pool_rows(0, 1, (1,))
+        turn_nodes(2)
+        turn_edges(2)
+        sort_edges(3)
+        tf_sin(1)
+        tf_dma(4)
+        acc_start(1, 0)
+        acc_start(1, 1)
+        load_group(NBUF)
+        for ct in range(2):
+            load_w(wo_raw, wo_w, ct, CO)
+        load_group(NBUF + 1)
+        load_group(NBUF + 2)
+
         pending = []
         wo_wg = {}
         vv = ("v", "v")
-        for g in range(NG):
-            if g + 3 < NG:
-                tf_dma(g + 3)
-            multiply(g, 0)
-            pool_rows(g, 0)
-            multiply(g, 1)
+        for g in range(1, NG):
+            if g + 4 < NG:
+                tf_dma(g + 4)
+            multiply(g, 0, (0, 1))
+            pool_rows(g, 0, (0, 1))
+            multiply(g, 1, (0, 1))
             if g == NG - 1:
                 out_pass(0, 2, ps_t, ("ta", "tb"))
                 out_pass(0, 0, ps_t, ("ta", "tb"))
                 out_pass(0, 1, ps_t, ("ta", "tb"))
                 out_pass(1, 2, ps_v, vv)
-            if g >= 1 and g + 2 < NG:
+            if g < 3:
+                quantise(g + 1)
+            elif g + 2 < NG:
                 quantise(g + 2)
             for job in pending:
                 job()
             pending = []
-            pool_rows(g, 1)
-            ahead = []
-            if g == 0:
-                ahead = [2, 3]
+            pool_rows(g, 1, (0, 1))
+            if g == 1:
+                turn_nodes(3)
+                turn_edges(3)
+                sort_edges(4)
+                turn_nodes(4)
+                load_group(3 + NBUF)
+            elif g == 2:
+                turn_edges(4)
+                sort_edges(5)
+                turn_nodes(5)
+                turn_edges(5)
+                sort_edges(6)
+                load_group(4 + NBUF)
+                load_group(5 + NBUF)
             elif g + 3 < NG:
-                ahead = [g + 3]
-            for t in ahead:
-                transposes(t)
-                if t + NBUF < NG:
-                    load_group(t + NBUF)
-            if g < 12:
-                wg_i, wch, wpair = wo_units[g]
+                turn_nodes(g + 3)
+                turn_edges(g + 3)
+                if g + 4 < NG:
+                    sort_edges(g + 4)
+                if g + 3 + NBUF < NG:
+                    load_group(g + 3 + NBUF)
+            if g == 2:
+                quantise(4)
+            if g < 4:
+                for ct in range(2):
+                    load_w(wo_raw, wo_w, 2 * g + ct, CO)
+            if g == 4:
+                nc.sync.dma_start(out=rootb[:], in_=root_node_feature.rearrange("(h p) k -> p h k", p=P))
+            if 3 <= g < 15:
+                wg_i, wch, wpair = wo_units[g - 3]
                 if wpair == 0:
                     wo_wg[0] = new_wg()
-                weight_unit(wo_raw, wo_wg[0], wg_i, wch, wpair, False, scopy, ps_t, "tc")
+                weight_unit(wo_raw, wo_wg[0], wg_i, wch, wpair, False, scopy, ps_t, next_bank())
                 if wpair == 1:
                     pending.append(
                         lambda t=wo_wg[0], a=wg_i, b=wch: weight_quantise(t, woc, wos, a, b)
                     )
-            if g + 4 < NG:
-                sort_edges(g + 4)
-            if g < 2:
-                dt_bank(g + 1)
-                dt_out(g + 1)
-            if g == 0:
-                quantise(2)
+            if g == 2:
+                dt_pair(3)
             if g in (1, 5, 9):
-                tf_uk((g + 7) // 4, False)
+                tf_uk((g + 7) // 4)
             if g in (2, 6, 10):
                 tf_frac((g + 6) // 4)
-            if g in (0, 3, 7, 11):
+            if g in (3, 7, 11):
                 tf_sin((g + 5) // 4)
-            if g == 12:
+            if g == 16:
                 nc.sync.dma_start(out=wob[:], in_=wo_b.partition_broadcast(P))
                 nc.sync.dma_start(out=lng[:], in_=ln_g.partition_broadcast(P))
                 nc.sync.dma_start(out=lnb[:], in_=ln_b.partition_broadcast(P))
@@ -638,11 +720,11 @@ def tile_transformeraggregator_pb_t_kernel(
                 pooled_round(0, 0, scopy)
                 pooled_round(0, 1, scopy)
             if g == 12:
-                pooled_transpose(0, 0, ps_t, "tc", scopy)
+                pooled_transpose(0, 0, ps_t, next_bank(), scopy)
                 pending.append(lambda: pooled_quantise(0, 0))
                 nc.scalar.sqrt(out=zout[:], in_=one[:])
             if g == 13:
-                pooled_transpose(0, 1, ps_t, "tc", scopy)
+                pooled_transpose(0, 1, ps_t, next_bank(), scopy)
                 pending.append(lambda: pooled_quantise(0, 1))
             if g == 14:
                 rg_t = root_unit()

@@ -75,8 +75,6 @@ def tile_transformeraggregator_pb_t_kernel(
             nc.scalar.dma_start(out=rt[:], in_=root_ts.rearrange("(h p o) -> p h o", p=P, o=1))
             nc.scalar.dma_start(out=xw[0:32, 0:4], in_=time_w.rearrange("(p t) o -> p (t o)", t=4))
             nc.scalar.dma_start(out=xw[0:32, 16:20], in_=time_b.rearrange("(p t) -> p t", t=4))
-            nc.scalar.dma_start(out=brow[0:1, :], in_=wv_b.rearrange("(o c) -> o c", o=1))
-            nc.scalar.dma_start(out=attb[:], in_=att.rearrange("(h p) j c -> p h (j c)", p=P))
         nc.scalar.activation(out=zout[:], in_=zin[:], func=ACT.Sin)
         nds = []
         eds = []
@@ -116,10 +114,12 @@ def tile_transformeraggregator_pb_t_kernel(
         load_group(0)
         for ct in range(2, 4):
             load_w(wv_raw, wv_w, ct, 1024)
+        nc.sync.dma_start(out=brow[0:1, :], in_=wv_b.rearrange("(o c) -> o c", o=1))
+        with nc.allow_non_contiguous_dma(reason="80-byte rows of attention weights"):
+            nc.sync.dma_start(out=attb[:], in_=att.rearrange("(h p) j c -> p h (j c)", p=P))
         for ct in range(4, 8):
             load_w(wv_raw, wv_w, ct, 1024)
-        for g in range(1, NBUF):
-            load_group(g)
+        load_group(1)
 
         wvc = const.tile([P, 2, DOUT], U32, name="wvc", align_bytes=64)
         wvs = const.tile([P, 2, DOUT], U8, name="wvs", align_bytes=64)
@@ -378,14 +378,21 @@ def tile_transformeraggregator_pb_t_kernel(
                     )
             banks[(g, i)] = pair
 
+        ph = {}
+
         def pool_rows(g, i, chs):
             nh = g // 10
             j = 2 * (g % 10) + i
             pair = banks[(g, i)]
             for ch in chs:
                 a = acc[nh][:, ch * 512 : (ch + 1) * 512]
+                sums = a
+                if j == NNEI - 1:
+                    pbf = late.tile([P, 512], BF16, name="pbf", tag="pbf%d" % ch)
+                    ph[(nh, ch)] = pbf
+                    sums = pbf[:]
                 nc.vector.scalar_tensor_tensor(
-                    out=a,
+                    out=sums,
                     in0=pair[ch][:],
                     scalar=attf[:, nh, j, ch : ch + 1],
                     in1=a,
@@ -394,21 +401,13 @@ def tile_transformeraggregator_pb_t_kernel(
                 )
 
 
-        ph = {}
-
-        def pooled_round(nh, h, cast):
-            pbf = late.tile([P, 2, 2, P], BF16, name="pbf", tag="pbf%d" % h)
-            src = acc[nh][:, h * 512 : (h + 1) * 512].rearrange("p (q i e) -> p q e i", q=2, e=2)
-            cast(out=pbf[:], in_=src)
-            ph[(nh, h)] = pbf
-
         def pooled_transpose(nh, h, pool, tag, evac):
-            pbf = ph[(nh, h)]
-            pt = pool.tile([P, 4, P], BF16, name="pt", tag=tag)
-            for s in range(4):
-                nc.tensor.transpose(pt[:, s, :], pbf[:, s // 2, s % 2, :], identb[:])
+            pw = ph[(nh, h)][:].bitcast(F32)
+            pt = pool.tile([P, 2, P], F32, name="pt", tag=tag)
+            for u in range(2):
+                nc.tensor.transpose(pt[:, u, :], pw[:, u * P : (u + 1) * P], identf[:])
             cg = late.tile([P, 512], BF16, name="cg", tag="cg%d" % h, align_bytes=64)
-            evac(out=cg[:].rearrange("p (n t) -> p n t", t=4), in_=pt[:].rearrange("p t n -> p n t"))
+            evac(out=cg[:].bitcast(F32).rearrange("p (n u) -> p n u", u=2), in_=pt[:].rearrange("p u n -> p n u"))
             ph[(nh, h)] = cg
 
         def pooled_quantise(nh, h):
@@ -419,13 +418,14 @@ def tile_transformeraggregator_pb_t_kernel(
 
         hbank = {}
 
-        def out_pass(nh, g, pool, tags):
+        def out_banks(nh, pools, tags):
+            hbank[nh] = []
+            for o in range(2):
+                h_t = pools[o].tile([P, 512], F32, name="h", tag=tags[o])
+                hbank[nh].append(h_t)
+
+        def out_pass(nh, g, start=False, stop=False):
             if g == 2:
-                pair = []
-                for o in range(2):
-                    h_t = pool.tile([P, 512], F32, name="h", tag=tags[o])
-                    pair.append(h_t)
-                hbank[nh] = pair
                 lt = rcc[:, nh * P : (nh + 1) * P]
                 ls = rcs[:, nh * P : (nh + 1) * P]
             else:
@@ -439,96 +439,85 @@ def tile_transformeraggregator_pb_t_kernel(
                     lhsT_scale=ls,
                     rhs=woc[:, g, cs].bitcast(FP8X4),
                     rhs_scale=wos[:, g, cs],
-                    start=(g == 2),
-                    stop=(g == 1),
+                    start=start,
+                    stop=stop,
                 )
 
-        lns = ({}, {})
         halves = (slice(0, 512), slice(512, 1024))
 
-        def ln_bias(nh):
-            hb = late.tile([P, DOUT], F32, name="hb", tag="hb%d" % nh)
-            for o in range(2):
-                nc.vector.tensor_tensor(out=hb[:, halves[o]], in0=hbank[nh][o][:], in1=wob[:, halves[o]], op=ALU.add)
-            lns[nh]["hb"] = hb
+        def ln_open(nh):
+            w = {}
+            for nm in ("hb", "rl", "y1", "yo"):
+                t = late.tile([P, DOUT], F32, name="ln_" + nm, tag="%s%d" % (nm, nh))
+                w[nm] = t
+            for nm in ("s1", "s2"):
+                t = late.tile([P, 2], F32, name="ln_" + nm, tag="%s%d" % (nm, nh))
+                w[nm] = t
+            for nm in ("mu", "m2", "ve", "rs", "nm"):
+                t = late.tile([P, 1], F32, name="ln_" + nm, tag="%s%d" % (nm, nh))
+                w[nm] = t
+            return w
 
-        def ln_relu(nh):
-            rl = late.tile([P, DOUT], F32, name="rl", tag="rl%d" % nh)
-            for o in range(2):
-                nc.scalar.activation(out=rl[:, halves[o]], in_=lns[nh]["hb"][:, halves[o]], func=ACT.Relu)
-            lns[nh]["rl"] = rl
+        def ln_relu(w, o):
+            nc.scalar.activation(
+                out=w["rl"][:, halves[o]], in_=w["hb"][:, halves[o]], func=ACT.Relu, accum_out=w["s1"][:, o : o + 1]
+            )
 
-        def ln_stats(nh):
-            st = late.tile([P, 2, 6], F32, name="st", tag="st%d" % nh)
-            for o in range(2):
-                nc.vector.bn_stats(out=st[:, o, :], in_=lns[nh]["rl"][:, halves[o]])
-            mv = late.tile([P, 2], F32, name="mv", tag="mv%d" % nh)
-            nc.vector.bn_aggr(out=mv[:], in_=st[:].rearrange("p a b -> p (a b)"))
-            ve = late.tile([P, 1], F32, name="ve", tag="ve%d" % nh)
-            nc.vector.tensor_scalar_add(out=ve[:], in0=mv[:, 1:2], scalar1=LN_EPS)
-            lns[nh]["mv"] = mv
-            lns[nh]["ve"] = ve
+        def ln_square(w, o):
+            nc.scalar.activation(
+                out=w["hb"][:, halves[o]], in_=w["rl"][:, halves[o]], func=ACT.Square, accum_out=w["s2"][:, o : o + 1]
+            )
 
-        def ln_relu_sums(nh):
-            rl = late.tile([P, DOUT], F32, name="rl", tag="rl%d" % nh)
-            s1 = late.tile([P, 1], F32, name="s1", tag="s1%d" % nh)
-            nc.scalar.activation(out=rl[:], in_=lns[nh]["hb"][:], func=ACT.Relu, accum_out=s1[:])
-            s2 = late.tile([P, 1], F32, name="s2", tag="s2%d" % nh)
-            nc.scalar.activation(out=lns[nh]["hb"][:], in_=rl[:], func=ACT.Square, accum_out=s2[:])
-            lns[nh]["rl"] = rl
-            lns[nh]["s1"] = s1
-            lns[nh]["s2"] = s2
-
-        def ln_stats_from_sums(nh):
-            mv = late.tile([P, 2], F32, name="mv", tag="mv%d" % nh)
-            nc.vector.tensor_scalar_mul(out=mv[:, 0:1], in0=lns[nh]["s1"][:], scalar1=1.0 / DOUT)
+        def ln_mean(w):
             nc.vector.tensor_scalar(
-                out=mv[:, 1:2],
-                in0=lns[nh]["s2"][:],
-                scalar1=1.0 / DOUT,
-                scalar2=LN_EPS,
+                out=w["mu"][:],
+                in0=w["s1"][:, 0:1],
+                scalar1=w["s1"][:, 1:2],
+                scalar2=1.0 / DOUT,
+                op0=ALU.add,
+                op1=ALU.mult,
+            )
+
+        def ln_mean_square(w):
+            nc.vector.tensor_scalar(
+                out=w["m2"][:], in0=w["mu"][:], scalar1=w["mu"][:], scalar2=-LN_EPS, op0=ALU.mult, op1=ALU.add
+            )
+
+        def ln_rstd(w):
+            nc.vector.tensor_scalar(
+                out=w["ve"][:],
+                in0=w["s2"][:, 0:1],
+                scalar1=w["s2"][:, 1:2],
+                scalar2=1.0 / DOUT,
+                op0=ALU.add,
+                op1=ALU.mult,
+            )
+            nc.vector.tensor_tensor(out=w["ve"][:], in0=w["ve"][:], in1=w["m2"][:], op=ALU.subtract)
+            nc.scalar.sqrt(out=w["m2"][:], in_=w["ve"][:])
+            nc.vector.reciprocal(out=w["rs"][:], in_=w["m2"][:])
+
+        def ln_centre(w, o):
+            nc.vector.scalar_tensor_tensor(
+                out=w["y1"][:, halves[o]],
+                in0=w["rl"][:, halves[o]],
+                scalar=w["mu"][:],
+                in1=lng[:, halves[o]],
+                op0=ALU.subtract,
+                op1=ALU.mult,
+            )
+
+        def ln_finish(w, o):
+            nc.vector.scalar_tensor_tensor(
+                out=w["yo"][:, halves[o]],
+                in0=w["y1"][:, halves[o]],
+                scalar=w["rs"][:],
+                in1=lnb[:, halves[o]],
                 op0=ALU.mult,
                 op1=ALU.add,
             )
-            m2 = late.tile([P, 1], F32, name="m2", tag="m2%d" % nh)
-            nc.vector.tensor_tensor(out=m2[:], in0=mv[:, 0:1], in1=mv[:, 0:1], op=ALU.mult)
-            ve = late.tile([P, 1], F32, name="ve", tag="ve%d" % nh)
-            nc.vector.tensor_tensor(out=ve[:], in0=mv[:, 1:2], in1=m2[:], op=ALU.subtract)
-            lns[nh]["mv"] = mv
-            lns[nh]["ve"] = ve
 
-        def ln_sqrt(nh):
-            sd = late.tile([P, 1], F32, name="sd", tag="sd%d" % nh)
-            nc.scalar.sqrt(out=sd[:], in_=lns[nh]["ve"][:])
-            lns[nh]["sd"] = sd
-
-        def ln_centre(nh):
-            y1 = late.tile([P, DOUT], F32, name="y1", tag="y1%d" % nh)
-            for o in range(2):
-                nc.vector.scalar_tensor_tensor(
-                    out=y1[:, halves[o]],
-                    in0=lns[nh]["rl"][:, halves[o]],
-                    scalar=lns[nh]["mv"][:, 0:1],
-                    in1=lng[:, halves[o]],
-                    op0=ALU.subtract,
-                    op1=ALU.mult,
-                )
-            lns[nh]["y1"] = y1
-
-        def ln_finish(nh):
-            rs = late.tile([P, 1], F32, name="rs", tag="rs%d" % nh)
-            nc.vector.reciprocal(out=rs[:], in_=lns[nh]["sd"][:])
-            yo = late.tile([P, DOUT], F32, name="yo", tag="yo%d" % nh)
-            for o in range(2):
-                nc.vector.scalar_tensor_tensor(
-                    out=yo[:, halves[o]],
-                    in0=lns[nh]["y1"][:, halves[o]],
-                    scalar=rs[:, 0:1],
-                    in1=lnb[:, halves[o]],
-                    op0=ALU.mult,
-                    op1=ALU.add,
-                )
-                nc.sync.dma_start(out=out[nh * P : (nh + 1) * P, halves[o]], in_=yo[:, halves[o]])
+        def store(nh, w, o):
+            nc.sync.dma_start(out=out[nh * P : (nh + 1) * P, halves[o]], in_=w["yo"][:, halves[o]])
 
         vcopy = nc.vector.tensor_copy
         scopy = nc.scalar.copy
@@ -563,10 +552,9 @@ def tile_transformeraggregator_pb_t_kernel(
             )
 
         tf_first_sin(0)
-        bias_row(0, vcopy)
+        sort_edges(0, vcopy)
         attf = const.tile([P, 2, NNEI, 2], F32, name="attf")
         nc.vector.tensor_copy(out=attf[:].rearrange("p h j c -> p h (j c)"), in_=attb[:])
-        sort_edges(0, vcopy)
         turn_nodes(0, 1)
         tf_first_sin(1)
         turn_edges(0)
@@ -574,15 +562,18 @@ def tile_transformeraggregator_pb_t_kernel(
         nc.vector.tensor_reduce(
             out=satt[:], in_=attf[:].rearrange("p h j c -> p h c j"), axis=AX.X, op=ALU.add
         )
-        acc_start(0, 0)
         weight_quantise_pair(wg_a, wvc, wvs, 0, 0, 0)
         weight_quantise_pair(wg_b, wvc, wvs, 1, 0, 0)
         nc.vector.tensor_copy(out=get_gg(0)[96:128, 1024:2048], in_=tf_t[0][0][96:128, :])
         for g in range(1, 4):
             tf_dma(g)
+        for g in range(2, NBUF):
+            load_group(g)
         weight_unit(wv_raw, wg_a, 0, 0, 1, False, scopy, ps_t, next_bank(), 1)
         weight_unit(wv_raw, wg_b, 1, 0, 1, True, vcopy, ps_t, next_bank(), 1)
         quantise(0)
+        bias_row(0, scopy)
+        acc_start(0, 0)
         weight_quantise_pair(wg_a, wvc, wvs, 0, 0, 1)
         weight_quantise_pair(wg_b, wvc, wvs, 1, 0, 1)
         wg_c = new_wg()
@@ -655,10 +646,8 @@ def tile_transformeraggregator_pb_t_kernel(
             pool_rows(g, 0, (0, 1))
             multiply(g, 1, (0, 1))
             if g == NG - 1:
-                out_pass(0, 2, ps_t, ("ta", "tb"))
-                out_pass(0, 0, ps_t, ("ta", "tb"))
-                out_pass(0, 1, ps_t, ("ta", "tb"))
-                out_pass(1, 2, ps_v, vv)
+                out_banks(1, (ps_t, ps_t), (next_bank(), next_bank()))
+                out_pass(1, 2, start=True)
             if g < 3:
                 quantise(g + 1)
             elif g + 2 < NG:
@@ -712,43 +701,85 @@ def tile_transformeraggregator_pb_t_kernel(
                 tf_frac((g + 6) // 4)
             if g in (3, 7, 11):
                 tf_sin((g + 5) // 4)
-            if g == 16:
+            if g == 12:
                 nc.sync.dma_start(out=wob[:], in_=wo_b.partition_broadcast(P))
+            if g == 13:
                 nc.sync.dma_start(out=lng[:], in_=ln_g.partition_broadcast(P))
+            if g == 14:
                 nc.sync.dma_start(out=lnb[:], in_=ln_b.partition_broadcast(P))
             if g == 10:
-                pooled_round(0, 0, scopy)
-                pooled_round(0, 1, scopy)
-            if g == 12:
                 pooled_transpose(0, 0, ps_t, next_bank(), scopy)
                 pending.append(lambda: pooled_quantise(0, 0))
-                nc.scalar.sqrt(out=zout[:], in_=one[:])
-            if g == 13:
+            if g == 11:
                 pooled_transpose(0, 1, ps_t, next_bank(), scopy)
                 pending.append(lambda: pooled_quantise(0, 1))
+            if g == 12:
+                nc.scalar.sqrt(out=zout[:], in_=one[:])
             if g == 14:
                 rg_t = root_unit()
                 pending.append(
                     lambda t=rg_t: nc.vector.quantize_mx(out=rcc[:].bitcast(FP8X4), scales=rcs[:], in_=t[:])
                 )
+            if g == 16:
+                out_banks(0, (ps_t, ps_t), (next_bank(), next_bank()))
+                ln0 = ln_open(0)
+                out_pass(0, 0, start=True)
+            if g == 17:
+                out_pass(0, 1)
+                out_pass(0, 2, stop=True)
+                for o in range(2):
+                    nc.scalar.copy(out=ln0["yo"][:, halves[o]], in_=hbank[0][o][:])
+                    nc.gpsimd.tensor_tensor(
+                        out=ln0["hb"][:, halves[o]], in0=ln0["yo"][:, halves[o]], in1=wob[:, halves[o]], op=ALU.add
+                    )
+            if g == 18:
+                for o in range(2):
+                    ln_relu(ln0, o)
+                for o in range(2):
+                    ln_square(ln0, o)
 
-        pooled_round(1, 0, scopy)
-        pooled_round(1, 1, scopy)
-        ln_bias(0)
-        pooled_transpose(1, 0, ps_t, "tc", scopy)
+        ln1 = ln_open(1)
+        ln_mean(ln0)
+        ln_mean_square(ln0)
+        pooled_transpose(1, 0, ps_t, next_bank(), scopy)
         pooled_transpose(1, 1, ps_v, "v", scopy)
-        ln_relu_sums(0)
         pooled_quantise(1, 0)
-        out_pass(1, 0, ps_v, vv)
+        out_pass(1, 0)
         pooled_quantise(1, 1)
-        out_pass(1, 1, ps_v, vv)
-        ln_stats_from_sums(0)
-        ln_sqrt(0)
-        ln_bias(1)
-        ln_relu_sums(1)
-        ln_centre(0)
-        ln_finish(0)
-        ln_stats_from_sums(1)
-        ln_sqrt(1)
-        ln_centre(1)
-        ln_finish(1)
+        out_pass(1, 1, stop=True)
+        ln_rstd(ln0)
+        nc.vector.tensor_scalar(
+            out=ln0["nm"][:], in0=ln0["mu"][:], scalar1=ln0["rs"][:], scalar2=-1.0, op0=ALU.mult, op1=ALU.mult
+        )
+        nc.scalar.activation(
+            out=ln0["y1"][:, halves[0]],
+            in_=ln0["rl"][:, halves[0]],
+            func=ACT.Identity,
+            scale=ln0["rs"][:],
+            bias=ln0["nm"][:],
+        )
+        nc.gpsimd.tensor_tensor(
+            out=ln0["hb"][:, halves[0]], in0=ln0["y1"][:, halves[0]], in1=lng[:, halves[0]], op=ALU.mult
+        )
+        nc.gpsimd.tensor_tensor(
+            out=ln0["yo"][:, halves[0]], in0=ln0["hb"][:, halves[0]], in1=lnb[:, halves[0]], op=ALU.add
+        )
+        store(0, ln0, 0)
+        ln_centre(ln0, 1)
+        for o in range(2):
+            nc.vector.tensor_tensor(
+                out=ln1["hb"][:, halves[o]], in0=hbank[1][o][:], in1=wob[:, halves[o]], op=ALU.add
+            )
+        ln_finish(ln0, 1)
+        store(0, ln0, 1)
+        for o in range(2):
+            ln_relu(ln1, o)
+        ln_mean(ln1)
+        for o in range(2):
+            ln_square(ln1, o)
+            ln_centre(ln1, o)
+        ln_mean_square(ln1)
+        ln_rstd(ln1)
+        for o in range(2):
+            ln_finish(ln1, o)
+            store(1, ln1, o)

@@ -523,14 +523,14 @@ def tile_transformeraggregator_pb_t_kernel(
         scopy = nc.scalar.copy
         tf_first()
         dt_pair(1)
+        dt_pair(3)
         tf_uk(1)
         wg_a = new_wg()
         wg_b = new_wg()
         weight_unit(wv_raw, wg_a, 0, 0, 0, False, scopy, ps_t, next_bank(), 1)
         weight_unit(wv_raw, wg_b, 1, 0, 0, True, scopy, ps_t, next_bank(), 1)
-        wvb = const.tile([P, DOUT], BF16, name="wvb")
 
-        def bias_row(ch, evac):
+        def acc_start(nh, ch):
             bp = ps_v.tile([P, 512], F32, name="bp", tag="v")
             nc.tensor.matmul(
                 out=bp[:],
@@ -539,16 +539,8 @@ def tile_transformeraggregator_pb_t_kernel(
                 start=True,
                 stop=True,
             )
-            evac(out=wvb[:, ch * 512 : (ch + 1) * 512], in_=bp[:])
-
-        def acc_start(nh, ch):
-            nc.gpsimd.tensor_scalar(
-                out=acc[nh][:, ch * 512 : (ch + 1) * 512],
-                in0=wvb[:, ch * 512 : (ch + 1) * 512],
-                scalar1=satt[:, nh, ch : ch + 1],
-                scalar2=0.0,
-                op0=ALU.mult,
-                op1=ALU.add,
+            nc.scalar.activation(
+                out=acc[nh][:, ch * 512 : (ch + 1) * 512], in_=bp[:], func=ACT.Copy, scale=satt[:, nh, ch : ch + 1]
             )
 
         tf_first_sin(0)
@@ -572,7 +564,6 @@ def tile_transformeraggregator_pb_t_kernel(
         weight_unit(wv_raw, wg_a, 0, 0, 1, False, scopy, ps_t, next_bank(), 1)
         weight_unit(wv_raw, wg_b, 1, 0, 1, True, vcopy, ps_t, next_bank(), 1)
         quantise(0)
-        bias_row(0, scopy)
         acc_start(0, 0)
         weight_quantise_pair(wg_a, wvc, wvs, 0, 0, 1)
         weight_quantise_pair(wg_b, wvc, wvs, 1, 0, 1)
@@ -604,15 +595,13 @@ def tile_transformeraggregator_pb_t_kernel(
             return rg
 
         sort_edges(1)
-        tf_frac(1)
         for i in range(2):
             multiply(0, i, (0,))
         pool_rows(0, 0, (0,))
         pool_rows(0, 1, (0,))
         weight_unit(wv_raw, wg_c, 0, 1, 1, False, scopy, ps_t, next_bank())
-        bias_row(1, scopy)
-        weight_unit(wv_raw, wg_d, 1, 1, 1, True, vcopy, ps_t, next_bank())
         acc_start(0, 1)
+        weight_unit(wv_raw, wg_d, 1, 1, 1, True, vcopy, ps_t, next_bank())
         weight_quantise(wg_c, wvc, wvs, 0, 1)
         turn_nodes(1, 1)
         turn_edges(1)
@@ -626,10 +615,7 @@ def tile_transformeraggregator_pb_t_kernel(
         turn_nodes(2)
         turn_edges(2)
         sort_edges(3)
-        tf_sin(1)
-        tf_dma(4)
-        acc_start(1, 0)
-        acc_start(1, 1)
+        tf_frac(1)
         load_group(NBUF)
         for ct in range(2):
             load_w(wo_raw, wo_w, ct, CO)
@@ -640,8 +626,10 @@ def tile_transformeraggregator_pb_t_kernel(
         wo_wg = {}
         vv = ("v", "v")
         for g in range(1, NG):
-            if g + 4 < NG:
-                tf_dma(g + 4)
+            if g == 1:
+                tf_sin(1)
+            if g + 3 < NG:
+                tf_dma(g + 3)
             multiply(g, 0, (0, 1))
             pool_rows(g, 0, (0, 1))
             multiply(g, 1, (0, 1))
@@ -693,14 +681,14 @@ def tile_transformeraggregator_pb_t_kernel(
                     pending.append(
                         lambda t=wo_wg[0], a=wg_i, b=wch: weight_quantise(t, woc, wos, a, b)
                     )
-            if g == 2:
-                dt_pair(3)
+            if g in (5, 6):
+                acc_start(1, g - 5)
             if g in (1, 5, 9):
                 tf_uk((g + 7) // 4)
-            if g in (2, 6, 10):
-                tf_frac((g + 6) // 4)
             if g in (3, 7, 11):
-                tf_sin((g + 5) // 4)
+                tf_frac((g + 5) // 4)
+            if g in (4, 8, 12):
+                tf_sin((g + 4) // 4)
             if g == 12:
                 nc.sync.dma_start(out=wob[:], in_=wo_b.partition_broadcast(P))
             if g == 13:

@@ -63,18 +63,16 @@ def tile_transformeraggregator_pb_t_kernel(
         brow = const.tile([P, DOUT], BF16, name="brow")
         zin = const.tile([P, 1], F32, name="zin")
         zout = const.tile([P, 1], F32, name="zout")
-        warm = const.tile([P, 512], BF16, name="warm")
         nc.vector.memset(xw[:], 0.0)
         nc.vector.memset(zin[:], 0.0)
-        nc.vector.memset(warm[:], 0.0)
         nc.vector.memset(brow[:], 0.0)
         identf = const.tile([P, P], F32, name="identf")
         make_identity(nc, identf[:])
         with nc.allow_non_contiguous_dma(reason="a few short rows of time stamps and weights"):
-            nc.scalar.dma_start(out=nt[:], in_=neighbor_ts.rearrange("(h p) j -> p h j", p=P))
-            nc.scalar.dma_start(out=rt[:], in_=root_ts.rearrange("(h p o) -> p h o", p=P, o=1))
-            nc.scalar.dma_start(out=xw[0:32, 0:4], in_=time_w.rearrange("(p t) o -> p (t o)", t=4))
-            nc.scalar.dma_start(out=xw[0:32, 16:20], in_=time_b.rearrange("(p t) -> p t", t=4))
+            nc.sync.dma_start(out=nt[:], in_=neighbor_ts.rearrange("(h p) j -> p h j", p=P))
+            nc.sync.dma_start(out=rt[:], in_=root_ts.rearrange("(h p o) -> p h o", p=P, o=1))
+            nc.sync.dma_start(out=xw[0:32, 0:4], in_=time_w.rearrange("(p t) o -> p (t o)", t=4))
+            nc.sync.dma_start(out=xw[0:32, 16:20], in_=time_b.rearrange("(p t) -> p t", t=4))
         nc.scalar.activation(out=zout[:], in_=zin[:], func=ACT.Sin)
         nds = []
         eds = []
@@ -143,9 +141,8 @@ def tile_transformeraggregator_pb_t_kernel(
             turn[0] += 1
             return ("ta", "tb", "tc")[turn[0] % 3]
 
-        def unit4(srcs, dst_words, evac, parts, pool, tag, spins=0):
+        def unit4(srcs, dst_words, evac, parts, pool, tag):
             t = pool.tile([P, 2, 2, P], F32, name="tr", tag=tag)
-            spin(t[:].rearrange("p i u r -> p (i u r)"), spins)
             for s in range(4):
                 nc.tensor.transpose(t[:, s // 2, s % 2, :], srcs[s], identf[:])
             evac(out=dst_words, in_=t[0:parts].rearrange("p i u r -> p i r u"))
@@ -176,12 +173,7 @@ def tile_transformeraggregator_pb_t_kernel(
         nc.vector.tensor_copy(out=lrt[:, 2, :], in_=rt[:, 1, :].to_broadcast([P, P]))
         lrt_of_m = (0, 0, 1, 2, 2)
 
-        def spin(bank, n):
-            for r in range(n):
-                nc.tensor.matmul(out=bank, lhsT=warm[:, 0:128], rhs=warm[:], start=True, stop=True)
-
         prm = ps_v.tile([P, 512], F32, name="prm", tag="v")
-        spin(prm[:], 8)
         nc.tensor.matmul(out=prm[:, 0:32], lhsT=sel[:], rhs=xw[:], start=True, stop=True)
         pa = const.tile([P, 4], F32, name="pa")
         pb = const.tile([P, 4], F32, name="pb")
@@ -286,7 +278,7 @@ def tile_transformeraggregator_pb_t_kernel(
 
         def get_gg(g):
             if g not in ggs:
-                gg_t = stg.tile([P, 2048], BF16, name="gg", tag="gg", align_bytes=64)
+                gg_t = stg.tile([P, 2048], BF16, name="gg", tag="gg", bufs=6, align_bytes=64)
                 ggs[g] = gg_t
             return ggs[g]
 
@@ -298,7 +290,7 @@ def tile_transformeraggregator_pb_t_kernel(
             wg_t = wgp.tile([P, 2048], BF16, name="wg", tag="wg", align_bytes=64)
             return wg_t
 
-        def weight_unit(raw, wg, g, ch, pair, natural, evac, pool, tag, spins=0):
+        def weight_unit(raw, wg, g, ch, pair, natural, evac, pool, tag):
             srcs = []
             for i in range(2):
                 ww = raw[ch * 4 + pair * 2 + i][:].bitcast(F32)
@@ -309,7 +301,7 @@ def tile_transformeraggregator_pb_t_kernel(
                         )
                     else:
                         srcs.append(ww[:, 256 * g + 128 * u : 256 * g + 128 * u + 128])
-            unit4(srcs, words(wg[:, pair * 1024 : (pair + 1) * 1024]), evac, P, pool, tag, spins)
+            unit4(srcs, words(wg[:, pair * 1024 : (pair + 1) * 1024]), evac, P, pool, tag)
 
         def weight_quantise_pair(wg, codes, scales, g, ch, pair):
             lo = ch * 512 + pair * 256
@@ -329,14 +321,14 @@ def tile_transformeraggregator_pb_t_kernel(
         quant = {}
         banks = {}
 
-        def turn_nodes(g, spins=0):
+        def turn_nodes(g):
             ndw = nds[g % NBUF][:].bitcast(F32)
             srcs = []
             for i in range(2):
                 for u in range(2):
                     lo = i * 256 + 128 * u
                     srcs.append(ndw[:, lo : lo + 128])
-            unit4(srcs, words(get_gg(g)[:, 0:1024]), nc.scalar.copy, P, ps_t, next_bank(), spins)
+            unit4(srcs, words(get_gg(g)[:, 0:1024]), nc.scalar.copy, P, ps_t, next_bank())
 
         def turn_edges(g):
             srcs = []
@@ -527,8 +519,8 @@ def tile_transformeraggregator_pb_t_kernel(
         tf_uk(1)
         wg_a = new_wg()
         wg_b = new_wg()
-        weight_unit(wv_raw, wg_a, 0, 0, 0, False, scopy, ps_t, next_bank(), 1)
-        weight_unit(wv_raw, wg_b, 1, 0, 0, True, scopy, ps_t, next_bank(), 1)
+        weight_unit(wv_raw, wg_a, 0, 0, 0, False, scopy, ps_t, next_bank())
+        weight_unit(wv_raw, wg_b, 1, 0, 0, True, scopy, ps_t, next_bank())
 
         def acc_start(nh, ch):
             bp = ps_v.tile([P, 512], F32, name="bp", tag="v")
@@ -547,7 +539,7 @@ def tile_transformeraggregator_pb_t_kernel(
         sort_edges(0, vcopy)
         attf = const.tile([P, 2, NNEI, 2], F32, name="attf")
         nc.vector.tensor_copy(out=attf[:].rearrange("p h j c -> p h (j c)"), in_=attb[:])
-        turn_nodes(0, 1)
+        turn_nodes(0)
         tf_first_sin(1)
         turn_edges(0)
         satt = const.tile([P, 2, 2], F32, name="satt")
@@ -561,16 +553,16 @@ def tile_transformeraggregator_pb_t_kernel(
             tf_dma(g)
         for g in range(2, NBUF):
             load_group(g)
-        weight_unit(wv_raw, wg_a, 0, 0, 1, False, scopy, ps_t, next_bank(), 1)
-        weight_unit(wv_raw, wg_b, 1, 0, 1, True, vcopy, ps_t, next_bank(), 1)
+        weight_unit(wv_raw, wg_a, 0, 0, 1, False, scopy, ps_t, next_bank())
+        weight_unit(wv_raw, wg_b, 1, 0, 1, True, vcopy, ps_t, next_bank())
         quantise(0)
         acc_start(0, 0)
         weight_quantise_pair(wg_a, wvc, wvs, 0, 0, 1)
         weight_quantise_pair(wg_b, wvc, wvs, 1, 0, 1)
         wg_c = new_wg()
-        weight_unit(wv_raw, wg_c, 0, 1, 0, False, scopy, ps_t, next_bank(), 2)
+        weight_unit(wv_raw, wg_c, 0, 1, 0, False, scopy, ps_t, next_bank())
         wg_d = new_wg()
-        weight_unit(wv_raw, wg_d, 1, 1, 0, True, scopy, ps_t, next_bank(), 1)
+        weight_unit(wv_raw, wg_d, 1, 1, 0, True, scopy, ps_t, next_bank())
         wob = const.tile([P, DOUT], BF16, name="wob")
         lng = const.tile([P, DOUT], BF16, name="lng")
         lnb = const.tile([P, DOUT], BF16, name="lnb")
@@ -603,7 +595,7 @@ def tile_transformeraggregator_pb_t_kernel(
         acc_start(0, 1)
         weight_unit(wv_raw, wg_d, 1, 1, 1, True, vcopy, ps_t, next_bank())
         weight_quantise(wg_c, wvc, wvs, 0, 1)
-        turn_nodes(1, 1)
+        turn_nodes(1)
         turn_edges(1)
         sort_edges(2)
         weight_quantise(wg_d, wvc, wvs, 1, 1)
@@ -611,11 +603,15 @@ def tile_transformeraggregator_pb_t_kernel(
             multiply(0, i, (1,))
         quantise(1)
         pool_rows(0, 0, (1,))
+        tf_frac(1)
+        tf_uk(2)
         pool_rows(0, 1, (1,))
         turn_nodes(2)
         turn_edges(2)
         sort_edges(3)
-        tf_frac(1)
+        tf_sin(1)
+        tf_dma(4)
+        tf_dma(5)
         load_group(NBUF)
         for ct in range(2):
             load_w(wo_raw, wo_w, ct, CO)
@@ -626,10 +622,8 @@ def tile_transformeraggregator_pb_t_kernel(
         wo_wg = {}
         vv = ("v", "v")
         for g in range(1, NG):
-            if g == 1:
-                tf_sin(1)
-            if g + 3 < NG:
-                tf_dma(g + 3)
+            if g + 5 < NG:
+                tf_dma(g + 5)
             multiply(g, 0, (0, 1))
             pool_rows(g, 0, (0, 1))
             multiply(g, 1, (0, 1))
@@ -683,12 +677,12 @@ def tile_transformeraggregator_pb_t_kernel(
                     )
             if g in (5, 6):
                 acc_start(1, g - 5)
+            if g in (1, 5):
+                tf_uk((g + 11) // 4)
             if g in (1, 5, 9):
-                tf_uk((g + 7) // 4)
-            if g in (3, 7, 11):
-                tf_frac((g + 5) // 4)
-            if g in (4, 8, 12):
-                tf_sin((g + 4) // 4)
+                tf_frac((g + 7) // 4)
+            if g in (2, 6, 10):
+                tf_sin((g + 6) // 4)
             if g == 12:
                 nc.sync.dma_start(out=wob[:], in_=wo_b.partition_broadcast(P))
             if g == 13:

@@ -460,19 +460,30 @@ def tile_transformeraggregator_pb_t_kernel(
                 out=w["hb"][:, halves[o]], in_=w["rl"][:, halves[o]], func=ACT.Square, accum_out=w["s2"][:, o : o + 1]
             )
 
+        def ln_square_sum(w, o):
+            nc.vector.scalar_tensor_tensor(
+                out=w["hb"][:, halves[o]],
+                in0=w["rl"][:, halves[o]],
+                scalar=1.0,
+                in1=w["rl"][:, halves[o]],
+                op0=ALU.mult,
+                op1=ALU.mult,
+                accum_out=w["s2"][:, o : o + 1],
+            )
+
         def ln_mean(w):
             nc.vector.tensor_scalar(
                 out=w["mu"][:],
                 in0=w["s1"][:, 0:1],
                 scalar1=w["s1"][:, 1:2],
-                scalar2=1.0 / DOUT,
+                scalar2=-1.0 / DOUT,
                 op0=ALU.add,
                 op1=ALU.mult,
             )
 
         def ln_mean_square(w):
             nc.vector.tensor_scalar(
-                out=w["m2"][:], in0=w["mu"][:], scalar1=w["mu"][:], scalar2=-LN_EPS, op0=ALU.mult, op1=ALU.add
+                out=w["m2"][:], in0=w["mu"][:], scalar1=w["mu"][:], scalar2=-1.0, op0=ALU.mult, op1=ALU.mult
             )
 
         def ln_rstd(w):
@@ -480,13 +491,13 @@ def tile_transformeraggregator_pb_t_kernel(
                 out=w["ve"][:],
                 in0=w["s2"][:, 0:1],
                 scalar1=w["s2"][:, 1:2],
-                scalar2=1.0 / DOUT,
+                scalar2=DOUT * LN_EPS,
                 op0=ALU.add,
-                op1=ALU.mult,
+                op1=ALU.add,
             )
-            nc.vector.tensor_tensor(out=w["ve"][:], in0=w["ve"][:], in1=w["m2"][:], op=ALU.subtract)
-            nc.scalar.sqrt(out=w["m2"][:], in_=w["ve"][:])
-            nc.vector.reciprocal(out=w["rs"][:], in_=w["m2"][:])
+            nc.scalar.activation(
+                out=w["rs"][:], in_=w["ve"][:], func=ACT.Abs_reciprocal_sqrt, scale=1.0 / DOUT, bias=w["m2"][:]
+            )
 
         def ln_centre(w, o):
             nc.vector.scalar_tensor_tensor(
@@ -494,7 +505,7 @@ def tile_transformeraggregator_pb_t_kernel(
                 in0=w["rl"][:, halves[o]],
                 scalar=w["mu"][:],
                 in1=lng[:, halves[o]],
-                op0=ALU.subtract,
+                op0=ALU.add,
                 op1=ALU.mult,
             )
 
@@ -696,7 +707,7 @@ def tile_transformeraggregator_pb_t_kernel(
                 pooled_transpose(0, 1, ps_t, next_bank(), scopy)
                 pending.append(lambda: pooled_quantise(0, 1))
             if g == 12:
-                nc.scalar.sqrt(out=zout[:], in_=one[:])
+                nc.scalar.activation(out=zout[:], in_=one[:], func=ACT.Abs_reciprocal_sqrt)
             if g == 14:
                 rg_t = root_unit()
                 pending.append(
@@ -731,7 +742,7 @@ def tile_transformeraggregator_pb_t_kernel(
         out_pass(1, 1, stop=True)
         ln_rstd(ln0)
         nc.vector.tensor_scalar(
-            out=ln0["nm"][:], in0=ln0["mu"][:], scalar1=ln0["rs"][:], scalar2=-1.0, op0=ALU.mult, op1=ALU.mult
+            out=ln0["nm"][:], in0=ln0["mu"][:], scalar1=ln0["rs"][:], scalar2=1.0, op0=ALU.mult, op1=ALU.mult
         )
         nc.scalar.activation(
             out=ln0["y1"][:, halves[0]],
@@ -756,9 +767,10 @@ def tile_transformeraggregator_pb_t_kernel(
         store(0, ln0, 1)
         for o in range(2):
             ln_relu(ln1, o)
+        ln_square_sum(ln1, 0)
+        ln_square(ln1, 1)
         ln_mean(ln1)
         for o in range(2):
-            ln_square(ln1, o)
             ln_centre(ln1, o)
         ln_mean_square(ln1)
         ln_rstd(ln1)

@@ -89,10 +89,22 @@ def tile_transformeraggregator_pb_t_kernel(
 
         wv_raw = []
         wo_raw = []
+        wo_src = []
+        for g in range(1):
+            ws_t = const.tile([P, 64, 64], BF16, name="ws%d" % g, align_bytes=64)
+            wo_src.append(ws_t)
+
+        def load_wo(g, a, u):
+            k0 = 512 * g + 256 * u + 64 * a
+            nc.sync.dma_start(
+                out=wo_src[g - 2][32 * a + u : 32 * a + 32 : 2, :, :],
+                in_=wo_w[:, k0 : k0 + 64].rearrange("(s r) k -> r s k", r=16),
+            )
+
 
         def load_w(dst, src, ct, width):
-            w = wraw.tile([P, CO], BF16, name="wr", tag="wr")
-            nc.sync.dma_start(out=w[:, 0:width], in_=src[ct * P : (ct + 1) * P, :])
+            w = wraw.tile([P, 1024], BF16, name="wr", tag="wr")
+            nc.sync.dma_start(out=w[:, 0:width], in_=src[ct * P : (ct + 1) * P, 0:width])
             dst.append(w)
 
         def load_group(g):
@@ -201,7 +213,6 @@ def tile_transformeraggregator_pb_t_kernel(
 
         def tf_first():
             bank_s = dt_bank((0,))
-            bank_v = dt_bank((0,))
             ut = tfp.tile([P, 4, 256], F32, name="ut", tag="ut", bufs=2)
             kt = tfp.tile([P, 4, 256], I32, name="kt", tag="kt", bufs=2)
             for t in range(2):
@@ -215,7 +226,7 @@ def tile_transformeraggregator_pb_t_kernel(
             for t in range(2, 4):
                 nc.vector.tensor_scalar(
                     out=ut[:, t, :],
-                    in0=bank_v[:, 0:256],
+                    in0=bank_s[:, 0:256],
                     scalar1=pa[:, t : t + 1],
                     scalar2=pb[:, t : t + 1],
                     op0=ALU.mult,
@@ -533,7 +544,7 @@ def tile_transformeraggregator_pb_t_kernel(
         weight_unit(wv_raw, wg_a, 0, 0, 0, False, scopy, ps_t, next_bank())
         weight_unit(wv_raw, wg_b, 1, 0, 0, True, scopy, ps_t, next_bank())
 
-        def acc_start(nh, ch):
+        def acc_start(ch):
             bp = ps_v.tile([P, 512], F32, name="bp", tag="v")
             nc.tensor.matmul(
                 out=bp[:],
@@ -542,9 +553,10 @@ def tile_transformeraggregator_pb_t_kernel(
                 start=True,
                 stop=True,
             )
-            nc.scalar.activation(
-                out=acc[nh][:, ch * 512 : (ch + 1) * 512], in_=bp[:], func=ACT.Copy, scale=satt[:, nh, ch : ch + 1]
-            )
+            for nh in range(2):
+                nc.scalar.activation(
+                    out=acc[nh][:, ch * 512 : (ch + 1) * 512], in_=bp[:], func=ACT.Copy, scale=satt[:, nh, ch : ch + 1]
+                )
 
         tf_first_sin(0)
         sort_edges(0, vcopy)
@@ -567,7 +579,7 @@ def tile_transformeraggregator_pb_t_kernel(
         weight_unit(wv_raw, wg_a, 0, 0, 1, False, scopy, ps_t, next_bank())
         weight_unit(wv_raw, wg_b, 1, 0, 1, True, vcopy, ps_t, next_bank())
         quantise(0)
-        acc_start(0, 0)
+        acc_start(0)
         weight_quantise_pair(wg_a, wvc, wvs, 0, 0, 1)
         weight_quantise_pair(wg_b, wvc, wvs, 1, 0, 1)
         wg_c = new_wg()
@@ -582,10 +594,17 @@ def tile_transformeraggregator_pb_t_kernel(
         nc.vector.memset(one[:], 1.0)
 
         wo_units = []
-        for g in range(3):
+        for g in range(2):
             for ch in range(2):
                 for pair in range(2):
                     wo_units.append((g, ch, pair))
+
+        def turn_wo(wg, piece):
+            src = wo_src[piece // 4][:].rearrange("p s k -> p (s k)").bitcast(F32)
+            dst = wg[:].bitcast(F32)
+            lo = 512 * (piece % 4)
+            hi = 512 * (piece % 2)
+            nc.vector.transpose(out=dst[:, hi : hi + 512], in_=src[:, lo : lo + 512])
 
         def root_unit():
             rw = rootb[:].bitcast(F32)
@@ -603,7 +622,7 @@ def tile_transformeraggregator_pb_t_kernel(
         pool_rows(0, 0, (0,))
         pool_rows(0, 1, (0,))
         weight_unit(wv_raw, wg_c, 0, 1, 1, False, scopy, ps_t, next_bank())
-        acc_start(0, 1)
+        acc_start(1)
         weight_unit(wv_raw, wg_d, 1, 1, 1, True, vcopy, ps_t, next_bank())
         weight_quantise(wg_c, wvc, wvs, 0, 1)
         turn_nodes(1)
@@ -625,7 +644,7 @@ def tile_transformeraggregator_pb_t_kernel(
         tf_dma(5)
         load_group(NBUF)
         for ct in range(2):
-            load_w(wo_raw, wo_w, ct, CO)
+            load_w(wo_raw, wo_w, ct, 1024)
         load_group(NBUF + 1)
         load_group(NBUF + 2)
 
@@ -674,10 +693,22 @@ def tile_transformeraggregator_pb_t_kernel(
                 quantise(4)
             if g < 4:
                 for ct in range(2):
-                    load_w(wo_raw, wo_w, 2 * g + ct, CO)
+                    load_w(wo_raw, wo_w, 2 * g + ct, 1024)
+            if 4 <= g < 6:
+                for a in range(4):
+                    load_wo(2 + (g - 4) // 2, a, g % 2)
             if g == 4:
                 nc.sync.dma_start(out=rootb[:], in_=root_node_feature.rearrange("(h p) k -> p h k", p=P))
-            if 3 <= g < 15:
+            if 11 <= g < 15:
+                piece = g - 11
+                if piece % 2 == 0:
+                    wo_wg[0] = new_wg()
+                turn_wo(wo_wg[0], piece)
+                if piece % 2 == 1:
+                    pending.append(
+                        lambda t=wo_wg[0], a=2 + piece // 4, b=(piece % 4) // 2: weight_quantise(t, woc, wos, a, b)
+                    )
+            if 3 <= g < 11:
                 wg_i, wch, wpair = wo_units[g - 3]
                 if wpair == 0:
                     wo_wg[0] = new_wg()
@@ -686,8 +717,6 @@ def tile_transformeraggregator_pb_t_kernel(
                     pending.append(
                         lambda t=wo_wg[0], a=wg_i, b=wch: weight_quantise(t, woc, wos, a, b)
                     )
-            if g in (5, 6):
-                acc_start(1, g - 5)
             if g in (1, 5):
                 tf_uk((g + 11) // 4)
             if g in (1, 5, 9):

@@ -770,39 +770,25 @@ def tile_transformeraggregator_pb_t_kernel(
         pooled_quantise(1, 1)
         out_pass(1, 1, stop=True)
         ln_rstd(ln0)
-        nc.vector.tensor_scalar(
-            out=ln0["nm"][:], in0=ln0["mu"][:], scalar1=ln0["rs"][:], scalar2=1.0, op0=ALU.mult, op1=ALU.mult
-        )
-        nc.scalar.activation(
-            out=ln0["y1"][:, halves[0]],
-            in_=ln0["rl"][:, halves[0]],
-            func=ACT.Identity,
-            scale=ln0["rs"][:],
-            bias=ln0["nm"][:],
-        )
-        nc.gpsimd.tensor_tensor(
-            out=ln0["hb"][:, halves[0]], in0=ln0["y1"][:, halves[0]], in1=lng[:, halves[0]], op=ALU.mult
-        )
-        nc.gpsimd.tensor_tensor(
-            out=ln0["yo"][:, halves[0]], in0=ln0["hb"][:, halves[0]], in1=lnb[:, halves[0]], op=ALU.add
-        )
-        store(0, ln0, 0)
+        ln_centre(ln0, 0)
         ln_centre(ln0, 1)
         for o in range(2):
             nc.vector.tensor_tensor(
                 out=ln1["hb"][:, halves[o]], in0=hbank[1][o][:], in1=wob[:, halves[o]], op=ALU.add
             )
-        ln_finish(ln0, 1)
-        store(0, ln0, 1)
+        ln_finish(ln0, 0)
+        store(0, ln0, 0)
         for o in range(2):
             ln_relu(ln1, o)
-        ln_square_sum(ln1, 0)
+        ln_square(ln1, 0)
         ln_square(ln1, 1)
         ln_mean(ln1)
+        ln_mean_square(ln1)
         for o in range(2):
             ln_centre(ln1, o)
-        ln_mean_square(ln1)
+        ln_finish(ln0, 1)
         ln_rstd(ln1)
+        store(0, ln0, 1)
         for o in range(2):
             ln_finish(ln1, o)
             store(1, ln1, o)

import math
from contextlib import ExitStack

import concourse.mybir as mybir
from concourse.masks import make_identity

F32 = mybir.dt.float32
BF16 = mybir.dt.bfloat16
I32 = mybir.dt.int32
U32 = mybir.dt.uint32
U8 = mybir.dt.uint8
FP8X4 = mybir.dt.float8_e4m3fn_x4
ALU = mybir.AluOpType
ACT = mybir.ActivationFunctionType
AX = mybir.AxisListType

P = 128
NNEI = 20
DN = 512
DE = 384
DOUT = 1024
CO = 1536
LN_EPS = 1e-5
FLOPS = 2 * 256 * NNEI * 1024 * DOUT + 2 * 256 * CO * DOUT
NG = 20
NBUF = 5


def tile_transformeraggregator_pb_t_kernel(
    tc,
    att,
    root_node_feature,
    root_ts,
    neighbor_ts,
    neighbor_node_feature,
    neighbor_edge_feature,
    time_w,
    time_b,
    wv_w,
    wv_b,
    wo_w,
    wo_b,
    ln_g,
    ln_b,
    out,
):
    nc = tc.nc
    with ExitStack() as es:
        const = es.enter_context(tc.tile_pool(name="const", bufs=1))
        wraw = es.enter_context(tc.tile_pool(name="wraw", bufs=8))
        wgp = es.enter_context(tc.tile_pool(name="wgp", bufs=3))
        stg = es.enter_context(tc.tile_pool(name="stg", bufs=4))
        tfp = es.enter_context(tc.tile_pool(name="tfp", bufs=1))
        late = es.enter_context(tc.tile_pool(name="late", bufs=1))
        ps_t = es.enter_context(tc.psum_pool(name="ps_t", bufs=1))
        ps_v = es.enter_context(tc.psum_pool(name="ps_v", bufs=5))
        es.enter_context(tc.manual_schedule())

        nt = const.tile([P, 2, NNEI], BF16, name="nt")
        rt = const.tile([P, 2, 1], BF16, name="rt")
        attb = const.tile([P, 2, 2 * NNEI], BF16, name="attb")
        xw = const.tile([P, 32], BF16, name="xw")
        brow = const.tile([P, DOUT], BF16, name="brow")
        zin = const.tile([P, 1], F32, name="zin")
        zout = const.tile([P, 1], F32, name="zout")
        nc.vector.memset(xw[:], 0.0)
        nc.vector.memset(zin[:], 0.0)
        nc.vector.memset(brow[:], 0.0)
        identf = const.tile([P, P], F32, name="identf")
        make_identity(nc, identf[:])
        with nc.allow_non_contiguous_dma(reason="a few short rows of time stamps and weights"):
            nc.sync.dma_start(out=nt[:], in_=neighbor_ts.rearrange("(h p) j -> p h j", p=P))
            nc.sync.dma_start(out=rt[:], in_=root_ts.rearrange("(h p o) -> p h o", p=P, o=1))
            nc.sync.dma_start(out=xw[0:32, 0:4], in_=time_w.rearrange("(p t) o -> p (t o)", t=4))
            nc.sync.dma_start(out=xw[0:32, 16:20], in_=time_b.rearrange("(p t) -> p t", t=4))
        nc.scalar.activation(out=zout[:], in_=zin[:], func=ACT.Sin)
        nds = []
        eds = []
        for b in range(NBUF):
            nd_t = const.tile([P, 2 * DN], BF16, name="nd%d" % b)
            nds.append(nd_t)
            ed_t = const.tile([P, 2 * DE], BF16, name="ed%d" % b)
            eds.append(ed_t)
        ess = []
        for b in range(3):
            es_t = const.tile([P, 2, 2, P], F32, name="es%d" % b)
            nc.vector.memset(es_t[:, :, :, 96:128], 0.0)
            ess.append(es_t)

        wv_raw = []
        wo_raw = []
        wo_src = []
        for g in range(1):
            ws_t = const.tile([P, 64, 64], BF16, name="ws%d" % g, align_bytes=64)
            wo_src.append(ws_t)

        def load_wo(g, a, u):
            k0 = 512 * g + 256 * u + 64 * a
            nc.sync.dma_start(
                out=wo_src[g - 2][32 * a + u : 32 * a + 32 : 2, :, :],
                in_=wo_w[:, k0 : k0 + 64].rearrange("(s r) k -> r s k", r=16),
            )


        def load_w(dst, src, ct, width):
            w = wraw.tile([P, 1024], BF16, name="wr", tag="wr")
            nc.sync.dma_start(out=w[:, 0:width], in_=src[ct * P : (ct + 1) * P, 0:width])
            dst.append(w)

        def load_group(g):
            rows = slice((g // 10) * P, (g // 10 + 1) * P)
            j0 = 2 * (g % 10)
            nc.sync.dma_start(
                out=nds[g % NBUF][:],
                in_=neighbor_node_feature[rows, j0 : j0 + 2, :].rearrange("p j k -> p (j k)"),
            )
            nc.sync.dma_start(
                out=eds[g % NBUF][:],
                in_=neighbor_edge_feature[rows, j0 : j0 + 2, :].rearrange("p j k -> p (j k)"),
            )

        for ct in range(2):
            load_w(wv_raw, wv_w, ct, 1024)
        load_group(0)
        for ct in range(2, 4):
            load_w(wv_raw, wv_w, ct, 1024)
        nc.sync.dma_start(out=brow[0:1, :], in_=wv_b.rearrange("(o c) -> o c", o=1))
        with nc.allow_non_contiguous_dma(reason="80-byte rows of attention weights"):
            nc.sync.dma_start(out=attb[:], in_=att.rearrange("(h p) j c -> p h (j c)", p=P))
        for ct in range(4, 8):
            load_w(wv_raw, wv_w, ct, 1024)
        load_group(1)

        wvc = const.tile([P, 2, DOUT], U32, name="wvc", align_bytes=64)
        wvs = const.tile([P, 2, DOUT], U8, name="wvs", align_bytes=64)
        woc = const.tile([P, 3, DOUT], U32, name="woc", align_bytes=64)
        wos = const.tile([P, 3, DOUT], U8, name="wos", align_bytes=64)
        rcc = const.tile([P, 256], U32, name="rcc", align_bytes=64)
        rcs = const.tile([P, 256], U8, name="rcs", align_bytes=64)
        ccc = const.tile([P, 2, 256], U32, name="ccc", align_bytes=64)
        ccs = const.tile([P, 2, 256], U8, name="ccs", align_bytes=64)
        acc = []
        for nh in range(2):
            acc_t = const.tile([P, DOUT], F32, name="acc%d" % nh)
            acc.append(acc_t)

        def words(ap):
            return ap.bitcast(F32).rearrange("p (i r u) -> p i r u", i=2, u=2)

        turn = [0]

        def next_bank():
            turn[0] += 1
            return ("ta", "tb", "tc")[turn[0] % 3]

        def unit4(srcs, dst_words, evac, parts, pool, tag):
            t = pool.tile([P, 2, 2, P], F32, name="tr", tag=tag)
            for s in range(4):
                nc.tensor.transpose(t[:, s // 2, s % 2, :], srcs[s], identf[:])
            evac(out=dst_words, in_=t[0:parts].rearrange("p i u r -> p i r u"))

        identb = const.tile([P, P], BF16, name="identb")
        nc.vector.tensor_copy(out=identb[:], in_=identf[:])
        sel = const.tile([P, P], BF16, name="sel")
        nc.vector.tensor_copy(
            out=sel[:].rearrange("p (a q) -> p a q", a=4),
            in_=identb[:, 0:32].unsqueeze(1).to_broadcast([P, 4, 32]),
        )
        lnt = const.tile([P, 5, 2, P], BF16, name="lnt")
        nt40 = nt[:].rearrange("p h j -> p (h j)").rearrange("p (m a i) -> p m i a", m=5, a=4)
        for i in range(2):
            nc.vector.tensor_scalar_mul(
                out=lnt[:, :, i, 0:96].rearrange("p m (a q) -> p m a q", a=3),
                in0=nt40[:, :, i, 1:4].unsqueeze(3).to_broadcast([P, 5, 3, 32]),
                scalar1=-1.0,
            )
            nc.vector.tensor_scalar_mul(
                out=lnt[:, :, i, 96:128], in0=nt40[:, :, i, 0:1].to_broadcast([P, 5, 32]), scalar1=-1.0
            )
        lrt = const.tile([P, 3, P], BF16, name="lrt")
        nc.vector.tensor_copy(out=lrt[:, 0, :], in_=rt[:, 0, :].to_broadcast([P, P]))
        nc.vector.tensor_copy(out=lrt[:, 1, 0:32], in_=rt[:, 0, :].to_broadcast([P, 32]))
        nc.vector.tensor_copy(out=lrt[:, 1, 32:96], in_=rt[:, 1, :].to_broadcast([P, 64]))
        nc.vector.tensor_copy(out=lrt[:, 1, 96:128], in_=rt[:, 0, :].to_broadcast([P, 32]))
        nc.vector.tensor_copy(out=lrt[:, 2, :], in_=rt[:, 1, :].to_broadcast([P, P]))
        lrt_of_m = (0, 0, 1, 2, 2)

        prm = ps_v.tile([P, 512], F32, name="prm", tag="v")
        nc.tensor.matmul(out=prm[:, 0:32], lhsT=sel[:], rhs=xw[:], start=True, stop=True)
        pa = const.tile([P, 4], F32, name="pa")
        pb = const.tile([P, 4], F32, name="pb")
        nc.vector.tensor_scalar_mul(out=pa[:], in0=prm[:, 0:4], scalar1=0.5 / math.pi)
        nc.vector.tensor_scalar(
            out=pb[:], in0=prm[:, 16:20], scalar1=0.5 / math.pi, scalar2=0.25, op0=ALU.mult, op1=ALU.add
        )
        dts = const.tile([P, 4, 256], F32, name="dts")

        def dt_bank(ms):
            dtp = ps_v.tile([P, 512], F32, name="dtp", tag="v")
            for l in range(2 * len(ms)):
                m = ms[l // 2]
                cols = slice(l * P, (l + 1) * P)
                nc.tensor.matmul(out=dtp[:, cols], lhsT=lrt[:, lrt_of_m[m], :], rhs=identb[:], start=True, stop=False)
                nc.tensor.matmul(out=dtp[:, cols], lhsT=lnt[:, m, l % 2, :], rhs=identb[:], start=False, stop=True)
            return dtp

        def dt_pair(m):
            dtp = dt_bank((m, m + 1))
            nc.scalar.copy(out=dts[:, m - 1 : m + 1, :].rearrange("p m w -> p (m w)"), in_=dtp[:])

        tf_t = {}
        tf_first_g = []

        def tf_first():
            bank_s = dt_bank((0,))
            ut = tfp.tile([P, 4, 256], F32, name="ut", tag="ut", bufs=2)
            kt = tfp.tile([P, 4, 256], I32, name="kt", tag="kt", bufs=2)
            for t in range(2):
                nc.scalar.activation(
                    out=ut[:, t, :],
                    in_=bank_s[:, 0:256],
                    func=ACT.Identity,
                    scale=pa[:, t : t + 1],
                    bias=pb[:, t : t + 1],
                )
            for t in range(2, 4):
                nc.vector.tensor_scalar(
                    out=ut[:, t, :],
                    in0=bank_s[:, 0:256],
                    scalar1=pa[:, t : t + 1],
                    scalar2=pb[:, t : t + 1],
                    op0=ALU.mult,
                    op1=ALU.add,
                )
            nc.vector.tensor_copy(out=kt[:, 0:2, :], in_=ut[:, 0:2, :])
            nc.vector.tensor_copy(out=kt[:, 2:4, :], in_=ut[:, 2:4, :])
            gt = tfp.tile([P, 256, 4], F32, name="gt", tag="gt")
            for i in range(2):
                cols = slice(i * P, (i + 1) * P)
                nc.vector.tensor_tensor(
                    out=gt[:, cols, :],
                    in0=ut[:, :, cols].rearrange("p t w -> p w t"),
                    in1=kt[:, :, cols].rearrange("p t w -> p w t"),
                    op=ALU.subtract,
                )
            tf_first_g.append(gt)
            tfg = tfp.tile([P, 1024], BF16, name="tfg", tag="tfg", bufs=2)
            tf_t[0] = [tfg]

        def tf_first_sin(i):
            gtf = tf_first_g[0][:].rearrange("p w t -> p (w t)")
            cols = slice(512 * i, 512 * i + 512)
            nc.scalar.activation(out=tf_t[0][0][:, cols], in_=gtf[:, cols], func=ACT.Sin, scale=2.0 * math.pi)

        def tf_uk(m):
            ut = tfp.tile([P, 4, 256], F32, name="ut", tag="ut", bufs=2)
            kt = tfp.tile([P, 4, 256], I32, name="kt", tag="kt", bufs=2)
            tf_t[m] = [ut, kt]
            for t in range(4):
                for dst in (ut, kt):
                    nc.gpsimd.tensor_scalar(
                        out=dst[:, t, :],
                        in0=dts[:, m - 1, :],
                        scalar1=pa[:, t : t + 1],
                        scalar2=pb[:, t : t + 1],
                        op0=ALU.mult,
                        op1=ALU.add,
                    )

        def tf_frac(m):
            ut, kt = tf_t[m]
            gt = tfp.tile([P, 256, 4], F32, name="gt", tag="gt")
            nc.vector.tensor_tensor(
                out=gt[:],
                in0=ut[:].rearrange("p t w -> p w t"),
                in1=kt[:].rearrange("p t w -> p w t"),
                op=ALU.subtract,
            )
            tf_t[m] = [gt]

        def tf_sin(m):
            gt = tf_t[m][0]
            tfg = tfp.tile([P, 1024], BF16, name="tfg", tag="tfg", bufs=2)
            gtf = gt[:].rearrange("p w t -> p (w t)")
            nc.scalar.activation(out=tfg[:], in_=gtf, func=ACT.Sin, scale=2.0 * math.pi)
            tf_t[m] = [tfg]

        ggs = {}

        def get_gg(g):
            if g not in ggs:
                gg_t = stg.tile([P, 2048], BF16, name="gg", tag="gg", bufs=6, align_bytes=64)
                ggs[g] = gg_t
            return ggs[g]

        def tf_dma(g):
            a = (g + 3) % 4
            nc.scalar.dma_start(out=get_gg(g)[96:128, 1024:2048], in_=tf_t[g // 4][0][32 * a : 32 * a + 32, :])

        def new_wg():
            wg_t = wgp.tile([P, 2048], BF16, name="wg", tag="wg", align_bytes=64)
            return wg_t

        def weight_unit(raw, wg, g, ch, pair, natural, evac, pool, tag):
            srcs = []
            for i in range(2):
                ww = raw[ch * 4 + pair * 2 + i][:].bitcast(F32)
                for u in range(2):
                    if natural:
                        srcs.append(
                            ww[:, 256 * g : 256 * g + 256].rearrange("p (w u) -> p w u", u=2)[:, :, u]
                        )
                    else:
                        srcs.append(ww[:, 256 * g + 128 * u : 256 * g + 128 * u + 128])
            unit4(srcs, words(wg[:, pair * 1024 : (pair + 1) * 1024]), evac, P, pool, tag)

        def weight_quantise_pair(wg, codes, scales, g, ch, pair):
            lo = ch * 512 + pair * 256
            nc.vector.quantize_mx(
                out=codes[:, g, lo : lo + 256].bitcast(FP8X4),
                scales=scales[:, g, lo : lo + 256],
                in_=wg[:, pair * 1024 : (pair + 1) * 1024],
            )

        def weight_quantise(wg, codes, scales, g, ch):
            nc.vector.quantize_mx(
                out=codes[:, g, ch * 512 : (ch + 1) * 512].bitcast(FP8X4),
                scales=scales[:, g, ch * 512 : (ch + 1) * 512],
                in_=wg[:],
            )

        quant = {}
        banks = {}

        def turn_nodes(g):
            ndw = nds[g % NBUF][:].bitcast(F32)
            srcs = []
            for i in range(2):
                for u in range(2):
                    lo = i * 256 + 128 * u
                    srcs.append(ndw[:, lo : lo + 128])
            unit4(srcs, words(get_gg(g)[:, 0:1024]), nc.scalar.copy, P, ps_t, next_bank())

        def turn_edges(g):
            srcs = []
            for i in range(2):
                for u in range(2):
                    srcs.append(ess[g % 3][:, i, u, :])
            unit4(srcs, words(get_gg(g)[0:96, 1024:2048]), nc.scalar.copy, 96, ps_t, next_bank())

        def sort_edges(g, copy=nc.scalar.copy):
            copy(
                out=ess[g % 3][:, :, :, 0:96],
                in_=eds[g % NBUF][:].bitcast(F32).rearrange("p (i w u) -> p i u w", i=2, u=2),
            )

        def quantise(g):
            cq = stg.tile([P, 512], U32, name="cq", tag="cq", align_bytes=64)
            sq = stg.tile([P, 512], U8, name="sq", tag="sq", align_bytes=64)
            nc.vector.quantize_mx(out=cq[:].bitcast(FP8X4), scales=sq[:], in_=ggs[g][:])
            quant[g] = (cq, sq)

        def multiply(g, i, chs):
            cq, sq = quant[g]
            pair = {}
            for ch in chs:
                v = ps_v.tile([P, 512], F32, name="v", tag="v")
                pair[ch] = v
            for ch in chs:
                cs = slice(ch * 512, (ch + 1) * 512)
                for k in range(2):
                    rows = slice(k * 256 + i * P, k * 256 + (i + 1) * P)
                    nc.tensor.matmul_mx(
                        out=pair[ch][:],
                        lhsT=cq[:, rows].bitcast(FP8X4),
                        lhsT_scale=sq[:, rows],
                        rhs=wvc[:, k, cs].bitcast(FP8X4),
                        rhs_scale=wvs[:, k, cs],
                        start=(k == 0),
                        stop=(k == 1),
                    )
            banks[(g, i)] = pair

        ph = {}

        def pool_rows(g, i, chs):
            nh = g // 10
            j = 2 * (g % 10) + i
            pair = banks[(g, i)]
            for ch in chs:
                a = acc[nh][:, ch * 512 : (ch + 1) * 512]
                sums = a
                if j == NNEI - 1:
                    pbf = late.tile([P, 512], BF16, name="pbf", tag="pbf%d" % ch)
                    ph[(nh, ch)] = pbf
                    sums = pbf[:]
                nc.vector.scalar_tensor_tensor(
                    out=sums,
                    in0=pair[ch][:],
                    scalar=attf[:, nh, j, ch : ch + 1],
                    in1=a,
                    op0=ALU.mult,
                    op1=ALU.add,
                )


        def pooled_transpose(nh, h, pool, tag, evac):
            pw = ph[(nh, h)][:].bitcast(F32)
            pt = pool.tile([P, 2, P], F32, name="pt", tag=tag)
            for u in range(2):
                nc.tensor.transpose(pt[:, u, :], pw[:, u * P : (u + 1) * P], identf[:])
            cg = late.tile([P, 512], BF16, name="cg", tag="cg%d" % h, align_bytes=64)
            evac(out=cg[:].bitcast(F32).rearrange("p (n u) -> p n u", u=2), in_=pt[:].rearrange("p u n -> p n u"))
            ph[(nh, h)] = cg

        def pooled_quantise(nh, h):
            cols = slice(h * P, (h + 1) * P)
            nc.vector.quantize_mx(
                out=ccc[:, nh, cols].bitcast(FP8X4), scales=ccs[:, nh, cols], in_=ph[(nh, h)][:]
            )

        hbank = {}

        def out_banks(nh, pools, tags):
            hbank[nh] = []
            for o in range(2):
                h_t = pools[o].tile([P, 512], F32, name="h", tag=tags[o])
                hbank[nh].append(h_t)

        def out_pass(nh, g, start=False, stop=False):
            if g == 2:
                lt = rcc[:, nh * P : (nh + 1) * P]
                ls = rcs[:, nh * P : (nh + 1) * P]
            else:
                lt = ccc[:, nh, g * P : (g + 1) * P]
                ls = ccs[:, nh, g * P : (g + 1) * P]
            for o in range(2):
                cs = slice(o * 512, (o + 1) * 512)
                nc.tensor.matmul_mx(
                    out=hbank[nh][o][:],
                    lhsT=lt.bitcast(FP8X4),
                    lhsT_scale=ls,
                    rhs=woc[:, g, cs].bitcast(FP8X4),
                    rhs_scale=wos[:, g, cs],
                    start=start,
                    stop=stop,
                )

        halves = (slice(0, 512), slice(512, 1024))

        def ln_open(nh):
            w = {}
            for nm in ("hb", "rl", "y1", "yo"):
                t = late.tile([P, DOUT], F32, name="ln_" + nm, tag="%s%d" % (nm, nh))
                w[nm] = t
            for nm in ("s1", "s2"):
                t = late.tile([P, 2], F32, name="ln_" + nm, tag="%s%d" % (nm, nh))
                w[nm] = t
            for nm in ("mu", "m2", "ve", "rs", "nm"):
                t = late.tile([P, 1], F32, name="ln_" + nm, tag="%s%d" % (nm, nh))
                w[nm] = t
            return w

        def ln_relu(w, o):
            nc.scalar.activation(
                out=w["rl"][:, halves[o]], in_=w["hb"][:, halves[o]], func=ACT.Relu, accum_out=w["s1"][:, o : o + 1]
            )

        def ln_square(w, o):
            nc.scalar.activation(
                out=w["hb"][:, halves[o]], in_=w["rl"][:, halves[o]], func=ACT.Square, accum_out=w["s2"][:, o : o + 1]
            )

        def ln_square_sum(w, o):
            nc.vector.scalar_tensor_tensor(
                out=w["hb"][:, halves[o]],
                in0=w["rl"][:, halves[o]],
                scalar=1.0,
                in1=w["rl"][:, halves[o]],
                op0=ALU.mult,
                op1=ALU.mult,
                accum_out=w["s2"][:, o : o + 1],
            )

        def ln_mean(w):
            nc.vector.tensor_scalar(
                out=w["mu"][:],
                in0=w["s1"][:, 0:1],
                scalar1=w["s1"][:, 1:2],
                scalar2=-1.0 / DOUT,
                op0=ALU.add,
                op1=ALU.mult,
            )

        def ln_mean_square(w):
            nc.vector.tensor_scalar(
                out=w["m2"][:], in0=w["mu"][:], scalar1=w["mu"][:], scalar2=-1.0, op0=ALU.mult, op1=ALU.mult
            )

        def ln_rstd(w):
            nc.vector.tensor_scalar(
                out=w["ve"][:],
                in0=w["s2"][:, 0:1],
                scalar1=w["s2"][:, 1:2],
                scalar2=DOUT * LN_EPS,
                op0=ALU.add,
                op1=ALU.add,
            )
            nc.scalar.activation(
                out=w["rs"][:], in_=w["ve"][:], func=ACT.Abs_reciprocal_sqrt, scale=1.0 / DOUT, bias=w["m2"][:]
            )

        def ln_centre(w, o):
            nc.vector.scalar_tensor_tensor(
                out=w["y1"][:, halves[o]],
                in0=w["rl"][:, halves[o]],
                scalar=w["mu"][:],
                in1=lng[:, halves[o]],
                op0=ALU.add,
                op1=ALU.mult,
            )

        def ln_finish(w, o):
            nc.vector.scalar_tensor_tensor(
                out=w["yo"][:, halves[o]],
                in0=w["y1"][:, halves[o]],
                scalar=w["rs"][:],
                in1=lnb[:, halves[o]],
                op0=ALU.mult,
                op1=ALU.add,
            )

        def store(nh, w, o):
            nc.sync.dma_start(out=out[nh * P : (nh + 1) * P, halves[o]], in_=w["yo"][:, halves[o]])

        vcopy = nc.vector.tensor_copy
        scopy = nc.scalar.copy
        tf_first()
        dt_pair(1)
        dt_pair(3)
        tf_uk(1)
        wg_a = new_wg()
        wg_b = new_wg()
        weight_unit(wv_raw, wg_a, 0, 0, 0, False, scopy, ps_t, next_bank())
        weight_unit(wv_raw, wg_b, 1, 0, 0, True, scopy, ps_t, next_bank())

        def acc_start(ch):
            bp = ps_v.tile([P, 512], F32, name="bp", tag="v")
            nc.tensor.matmul(
                out=bp[:],
                lhsT=identb[:, 0:1].to_broadcast([P, P]),
                rhs=brow[:, ch * 512 : (ch + 1) * 512],
                start=True,
                stop=True,
            )
            for nh in range(2):
                nc.scalar.activation(
                    out=acc[nh][:, ch * 512 : (ch + 1) * 512], in_=bp[:], func=ACT.Copy, scale=satt[:, nh, ch : ch + 1]
                )

        tf_first_sin(0)
        sort_edges(0, vcopy)
        attf = const.tile([P, 2, NNEI, 2], F32, name="attf")
        nc.vector.tensor_copy(out=attf[:].rearrange("p h j c -> p h (j c)"), in_=attb[:])
        turn_nodes(0)
        tf_first_sin(1)
        turn_edges(0)
        satt = const.tile([P, 2, 2], F32, name="satt")
        nc.vector.tensor_reduce(
            out=satt[:], in_=attf[:].rearrange("p h j c -> p h c j"), axis=AX.X, op=ALU.add
        )
        weight_quantise_pair(wg_a, wvc, wvs, 0, 0, 0)
        weight_quantise_pair(wg_b, wvc, wvs, 1, 0, 0)
        nc.vector.tensor_copy(out=get_gg(0)[96:128, 1024:2048], in_=tf_t[0][0][96:128, :])
        for g in range(1, 4):
            tf_dma(g)
        for g in range(2, NBUF):
            load_group(g)
        weight_unit(wv_raw, wg_a, 0, 0, 1, False, scopy, ps_t, next_bank())
        weight_unit(wv_raw, wg_b, 1, 0, 1, True, vcopy, ps_t, next_bank())
        quantise(0)
        acc_start(0)
        weight_quantise_pair(wg_a, wvc, wvs, 0, 0, 1)
        weight_quantise_pair(wg_b, wvc, wvs, 1, 0, 1)
        wg_c = new_wg()
        weight_unit(wv_raw, wg_c, 0, 1, 0, False, scopy, ps_t, next_bank())
        wg_d = new_wg()
        weight_unit(wv_raw, wg_d, 1, 1, 0, True, scopy, ps_t, next_bank())
        wob = const.tile([P, DOUT], BF16, name="wob")
        lng = const.tile([P, DOUT], BF16, name="lng")
        lnb = const.tile([P, DOUT], BF16, name="lnb")
        rootb = const.tile([P, 2, DN], BF16, name="rootb")
        one = const.tile([P, 1], F32, name="one")
        nc.vector.memset(one[:], 1.0)

        wo_units = []
        for g in range(2):
            for ch in range(2):
                for pair in range(2):
                    wo_units.append((g, ch, pair))

        def turn_wo(wg, piece):
            src = wo_src[piece // 4][:].rearrange("p s k -> p (s k)").bitcast(F32)
            dst = wg[:].bitcast(F32)
            lo = 512 * (piece % 4)
            hi = 512 * (piece % 2)
            nc.vector.transpose(out=dst[:, hi : hi + 512], in_=src[:, lo : lo + 512])

        def root_unit():
            rw = rootb[:].bitcast(F32)
            srcs = []
            for nh in range(2):
                for u in range(2):
                    srcs.append(rw[:, nh, 128 * u : 128 * u + 128])
            rg = late.tile([P, 1024], BF16, name="rg", align_bytes=64)
            unit4(srcs, words(rg[:]), scopy, P, ps_t, "tc")
            return rg

        sort_edges(1)
        for i in range(2):
            multiply(0, i, (0,))
        pool_rows(0, 0, (0,))
        pool_rows(0, 1, (0,))
        weight_unit(wv_raw, wg_c, 0, 1, 1, False, scopy, ps_t, next_bank())
        acc_start(1)
        weight_unit(wv_raw, wg_d, 1, 1, 1, True, vcopy, ps_t, next_bank())
        weight_quantise(wg_c, wvc, wvs, 0, 1)
        turn_nodes(1)
        turn_edges(1)
        sort_edges(2)
        weight_quantise(wg_d, wvc, wvs, 1, 1)
        for i in range(2):
            multiply(0, i, (1,))
        quantise(1)
        pool_rows(0, 0, (1,))
        tf_frac(1)
        tf_uk(2)
        pool_rows(0, 1, (1,))
        turn_nodes(2)
        turn_edges(2)
        sort_edges(3)
        tf_sin(1)
        tf_dma(4)
        tf_dma(5)
        load_group(NBUF)
        for ct in range(2):
            load_w(wo_raw, wo_w, ct, 1024)
        load_group(NBUF + 1)
        load_group(NBUF + 2)

        pending = []
        wo_wg = {}
        vv = ("v", "v")
        for g in range(1, NG):
            if g + 5 < NG:
                tf_dma(g + 5)
            multiply(g, 0, (0, 1))
            pool_rows(g, 0, (0, 1))
            multiply(g, 1, (0, 1))
            if g == NG - 1:
                out_banks(1, (ps_t, ps_t), (next_bank(), next_bank()))
                out_pass(1, 2, start=True)
            if g < 3:
                quantise(g + 1)
            elif g + 2 < NG:
                quantise(g + 2)
            for job in pending:
                job()
            pending = []
            pool_rows(g, 1, (0, 1))
            if g == 1:
                turn_nodes(3)
                turn_edges(3)
                sort_edges(4)
                turn_nodes(4)
                load_group(3 + NBUF)
            elif g == 2:
                turn_edges(4)
                sort_edges(5)
                turn_nodes(5)
                turn_edges(5)
                sort_edges(6)
                load_group(4 + NBUF)
                load_group(5 + NBUF)
            elif g + 3 < NG:
                turn_nodes(g + 3)
                turn_edges(g + 3)
                if g + 4 < NG:
                    sort_edges(g + 4)
                if g + 3 + NBUF < NG:
                    load_group(g + 3 + NBUF)
            if g == 2:
                quantise(4)
            if g < 4:
                for ct in range(2):
                    load_w(wo_raw, wo_w, 2 * g + ct, 1024)
            if 4 <= g < 6:
                for a in range(4):
                    load_wo(2 + (g - 4) // 2, a, g % 2)
            if g == 4:
                nc.sync.dma_start(out=rootb[:], in_=root_node_feature.rearrange("(h p) k -> p h k", p=P))
            if 11 <= g < 15:
                piece = g - 11
                if piece % 2 == 0:
                    wo_wg[0] = new_wg()
                turn_wo(wo_wg[0], piece)
                if piece % 2 == 1:
                    pending.append(
                        lambda t=wo_wg[0], a=2 + piece // 4, b=(piece % 4) // 2: weight_quantise(t, woc, wos, a, b)
                    )
            if 3 <= g < 11:
                wg_i, wch, wpair = wo_units[g - 3]
                if wpair == 0:
                    wo_wg[0] = new_wg()
                weight_unit(wo_raw, wo_wg[0], wg_i, wch, wpair, False, scopy, ps_t, next_bank())
                if wpair == 1:
                    pending.append(
                        lambda t=wo_wg[0], a=wg_i, b=wch: weight_quantise(t, woc, wos, a, b)
                    )
            if g in (1, 5):
                tf_uk((g + 11) // 4)
            if g in (1, 5, 9):
                tf_frac((g + 7) // 4)
            if g in (2, 6, 10):
                tf_sin((g + 6) // 4)
            if g == 12:
                nc.sync.dma_start(out=wob[:], in_=wo_b.partition_broadcast(P))
            if g == 13:
                nc.sync.dma_start(out=lng[:], in_=ln_g.partition_broadcast(P))
            if g == 14:
                nc.sync.dma_start(out=lnb[:], in_=ln_b.partition_broadcast(P))
            if g == 10:
                pooled_transpose(0, 0, ps_t, next_bank(), scopy)
                pending.append(lambda: pooled_quantise(0, 0))
            if g == 11:
                pooled_transpose(0, 1, ps_t, next_bank(), scopy)
                pending.append(lambda: pooled_quantise(0, 1))
            if g == 12:
                nc.scalar.activation(out=zout[:], in_=one[:], func=ACT.Abs_reciprocal_sqrt)
            if g == 14:
                rg_t = root_unit()
                pending.append(
                    lambda t=rg_t: nc.vector.quantize_mx(out=rcc[:].bitcast(FP8X4), scales=rcs[:], in_=t[:])
                )
            if g == 16:
                out_banks(0, (ps_t, ps_t), (next_bank(), next_bank()))
                ln0 = ln_open(0)
                out_pass(0, 0, start=True)
            if g == 17:
                out_pass(0, 1)
                out_pass(0, 2, stop=True)
                for o in range(2):
                    nc.scalar.copy(out=ln0["yo"][:, halves[o]], in_=hbank[0][o][:])
                    nc.gpsimd.tensor_tensor(
                        out=ln0["hb"][:, halves[o]], in0=ln0["yo"][:, halves[o]], in1=wob[:, halves[o]], op=ALU.add
                    )
            if g == 18:
                for o in range(2):
                    ln_relu(ln0, o)
                for o in range(2):
                    ln_square(ln0, o)

        ln1 = ln_open(1)
        ln_mean(ln0)
        ln_mean_square(ln0)
        pooled_transpose(1, 0, ps_t, next_bank(), scopy)
        pooled_transpose(1, 1, ps_v, "v", scopy)
        pooled_quantise(1, 0)
        out_pass(1, 0)
        pooled_quantise(1, 1)
        out_pass(1, 1, stop=True)
        ln_rstd(ln0)
        ln_centre(ln0, 0)
        ln_centre(ln0, 1)
        for o in range(2):
            nc.vector.tensor_tensor(
                out=ln1["hb"][:, halves[o]], in0=hbank[1][o][:], in1=wob[:, halves[o]], op=ALU.add
            )
        ln_finish(ln0, 0)
        store(0, ln0, 0)
        for o in range(2):
            ln_relu(ln1, o)
        ln_square(ln1, 0)
        ln_square(ln1, 1)
        ln_mean(ln1)
        ln_mean_square(ln1)
        for o in range(2):
            ln_centre(ln1, o)
        ln_finish(ln0, 1)
        ln_rstd(ln1)
        store(0, ln0, 1)
        for o in range(2):
            ln_finish(ln1, o)
            store(1, ln1, o)
